import numpy as np
import ml_dtypes


def mxq(x, axis, fmt="e4m3"):
    dtype, down = {"e4m3": (ml_dtypes.float8_e4m3fn, 7), "e5m2": (ml_dtypes.float8_e5m2, 14)}[fmt]
    v = np.moveaxis(np.asarray(x, np.float32).astype(ml_dtypes.bfloat16).astype(np.float64), axis, -1)
    blocks = v.reshape(v.shape[:-1] + (-1, 32))
    amax = np.abs(blocks).max(-1, keepdims=True)
    byte = np.maximum(np.where(amax > 0, np.frexp(amax)[1] - 1 + 127, 0) - down, 1)
    scale = np.exp2(byte - 127.0)
    codes = (blocks / scale).astype(np.float32).astype(dtype).astype(np.float64)
    return np.moveaxis((codes * scale).reshape(v.shape), -1, axis)


WIDE = False


def mx_kscale(k):
    if not WIDE:
        return np.ones(k)
    levels = np.array([10, -10, 5, -5, 0])
    if k % 512:
        return np.exp2(np.random.permutation(np.resize(levels, k // 32))).repeat(32)
    a = np.empty((k // 512, 16))
    for p in range(k // 512):
        a[p, :8] = np.random.permutation(np.resize(levels, 8))
        for g in range(8):
            far = levels[np.abs(levels - a[p, g]) >= 10]
            a[p, g + 8] = far[np.random.randint(len(far))]
    return np.exp2(a.ravel()).repeat(32)


BF16 = ml_dtypes.bfloat16


def bf(x):
    return np.asarray(x, np.float32).astype(BF16)


def f64(x):
    return np.asarray(x).astype(np.float64)


B, S, I0, I1, I2, I3, I4, O0, O1, O2, O3, O4, R1, R2, R3, R4 = 2, 256, 4, 4, 2, 2, 16, 4, 8, 2, 2, 32, 16, 512, 1024, 512
IA, OA = I0 * I1, O0 * O1


def tt_step(t, c):
    I, O, r = t.shape
    _, i, o, q = c.shape
    p = mxq(t.reshape(I * O, r), 1, "e4m3") @ mxq(c.reshape(r, i * o * q), 0, "e4m3")
    return p.reshape(I, O, i, o, q).transpose(0, 2, 1, 3, 4).reshape(I * i, O * o, q)


def draw0():
    s, u = mx_kscale(R2), mx_kscale(R3)
    return {"t1": bf(np.random.standard_normal((IA, OA, R2)) * s),
            "core2": bf(np.random.standard_normal((R2, I2, O2, R3)) / np.sqrt(R2) / s[:, None, None, None] * u),
            "core3": bf(np.random.standard_normal((R3, I3, O3, R4)) / np.sqrt(R3) / u[:, None, None, None])}


def core(t1, core2, core3):
    t2 = tt_step(f64(t1), f64(core2))
    return tt_step(t2, f64(core3))


def e4m3fn_bytes(y):
    return np.clip(np.asarray(y, np.float64), -448.0, 448.0).astype(np.float32).astype(ml_dtypes.float8_e4m3fn).view(np.uint8)


def e4m3fn_values(b):
    return np.asarray(b, np.uint8).view(ml_dtypes.float8_e4m3fn).astype(np.float64)


def setup_inputs():
    d = draw0()
    x0 = np.asarray(d['core3']).astype(np.float64)
    s = (np.max(np.abs(x0), axis=(1, 2, 3), keepdims=True) / 448.0).astype(np.float32)
    out = {}
    for k, v in d.items():
        if k == 'core3':
            out['core3_bytes'] = e4m3fn_bytes(x0 / s.astype(np.float64))
            out['core3_scale'] = s
        else:
            out[k] = v
    return out


def reference(t1, core2, core3_bytes, core3_scale):
    return core(t1, core2, e4m3fn_values(core3_bytes) * core3_scale.astype(np.float64))

@@ -1,0 +1,237 @@
+from contextlib import ExitStack
+
+import concourse.mybir as mybir
+from concourse.masks import make_identity
+
+F32 = mybir.dt.float32
+BF16 = mybir.dt.bfloat16
+U32 = mybir.dt.uint32
+U8 = mybir.dt.uint8
+FP8 = mybir.dt.float8_e4m3fn
+FP8X4 = mybir.dt.float8_e4m3fn_x4
+MULT = mybir.AluOpType.mult
+COPY = mybir.ActivationFunctionType.Copy
+
+FLOPS = 2 * 512 * 512 * 4096 + 2 * 2048 * 1024 * 2048
+
+
+def deps(o):
+    n, a = o[0], o[1:]
+    if n == "t1c":
+        return [("tr", 2 * a[0]), ("tr", 2 * a[0] + 1)]
+    if n == "t1q":
+        return [("t1c", 0), ("t1c", 1)]
+    if n == "c2q":
+        return [("c2i",) + a]
+    if n == "s1":
+        return [("c2q", a[0], a[1]), ("t1q",)]
+    if n == "ev1":
+        return [("s1",) + a]
+    if n == "t2q":
+        return [("ev1", a[0], a[1], r) for r in range(4)]
+    if n == "c3i":
+        return [("w", a[0], a[1], t) for t in range(4)]
+    if n == "c3q":
+        return [("c3i",) + a]
+    if n == "s2":
+        return [("t2q", a[0], 0), ("t2q", a[0], 1), ("c3q", a[1], 0), ("c3q", a[1], 1)]
+    if n == "ev2":
+        return [("s2",) + a]
+    return []
+
+
+def merge(queues):
+    pos = {"PE": 0, "S": 0, "V": 0}
+    done = set()
+    text = []
+    live = 0
+    while len(text) < len(queues["PE"]) + len(queues["S"]) + len(queues["V"]):
+        before = len(text)
+        for e in ("PE", "S", "V"):
+            while pos[e] < len(queues[e]):
+                o = queues[e][pos[e]]
+                opens = e == "PE" and not (o[0] == "tr" and o[1] % 2 == 1)
+                if opens and live >= 8:
+                    break
+                if not all(d in done for d in deps(o)):
+                    break
+                if opens:
+                    live += 1
+                if o[0] in ("ev1", "ev2", "t1c"):
+                    live -= 1
+                text.append((e,) + o)
+                done.add(o)
+                pos[e] += 1
+        assert len(text) > before
+    return text
+
+
+LOADS = [["t1",0,0],["t1",1,0],["c2",0,0],["c3",0,0],["c2",0,1],["c3",0,1],["c2",1,1],["c3",1,1],["c2",1,0],["c3",1,0],["c2",2,1],["c2",3,0],["c2",3,1],["c2",2,0]]
+LAST = (3, 1)
+
+
+def parse(text):
+    ops = []
+    for item in text.split(", "):
+        w = item.split(" ")
+        ops.append((w[0],) + tuple(int(x) for x in w[1:]))
+    return ops
+
+
+def queues():
+    return {
+        "PE": parse("tr 0, tr 1, tr 2, tr 3, s1 0 0 1, s1 0 0 0, s1 0 1 1, s1 0 1 3, s1 0 0 2, s1 0 1 2, s1 1 1 3, s1 1 1 0, s1 0 1 0, s1 0 0 3, s1 1 0 1, s1 1 0 3, s1 1 0 2, s1 1 0 0, s1 1 1 1, s1 1 1 2, s2 0 0 2, s2 0 0 0, s2 0 0 1, s2 0 1 0, s2 0 1 2, s2 0 1 1, s2 1 1 3, s2 0 1 3, s2 1 0 3, s2 0 0 3, s2 1 1 2, s2 1 0 0, s2 1 1 1, s1 2 1 0, s1 2 0 1, s1 2 1 1, s1 2 1 2, s1 2 0 0, s2 1 1 0, s2 1 0 2, s1 2 0 3, s2 1 0 1, s1 2 1 3, s1 2 0 2, s2 1 2 3, s2 1 2 0, s2 0 2 2, s2 0 2 3, s2 2 0 1, s2 2 1 1, s2 2 0 0, s2 2 0 2, s2 2 1 2, s2 2 1 0, s2 2 0 3, s2 0 2 1, s2 1 2 1, s2 2 2 0, s2 0 3 3, s2 0 3 1, s2 0 3 2, s2 1 3 3, s2 1 3 1, s2 2 1 3, s1 3 1 2, s1 3 1 1, s1 3 1 0, s2 1 3 2, s1 3 0 1, s1 3 1 3, s2 1 2 2, s2 2 3 0, s1 3 0 2, s2 2 2 3, s1 3 0 0, s2 1 3 0, s1 3 0 3, s2 2 3 1, s2 2 2 1, s2 2 3 3, s2 0 3 0, s2 0 2 0, s2 3 3 2, s2 3 1 3, s2 3 3 3, s2 3 1 2, s2 3 3 0, s2 3 0 2, s2 3 2 3, s2 3 1 0, s2 2 2 2, s2 2 3 2, s2 3 0 1, s2 3 2 1, s2 3 0 3, s2 3 0 0, s2 3 2 0, s2 3 3 1, s2 3 1 1, s2 3 2 2"),
+        "S": parse("t1c 0, t1c 1, w 0 0 1, w 1 0 0, w 1 0 3, w 0 0 2, w 0 0 3, w 1 0 2, w 0 1 3, w 0 1 2, w 1 1 3, ev1 0 0 0, ev1 0 0 1, ev1 0 0 2, w 1 0 1, w 0 1 0, ev1 0 1 1, w 0 1 1, w 1 1 2, ev1 0 1 3, ev1 0 1 0, ev1 1 1 3, ev1 0 1 2, w 2 0 1, ev1 1 0 3, w 2 1 0, ev1 0 0 3, ev1 1 1 1, ev1 1 0 1, ev1 1 1 2, ev1 1 0 2, ev1 1 1 0, ev1 1 0 0, ev2 0 0 1, ev2 0 0 2, w 2 0 3, ev2 0 1 0, ev2 0 1 2, ev2 0 1 1, w 2 1 1, ev2 0 0 0, ev2 0 1 3, ev2 0 0 3, ev2 1 1 3, ev2 1 1 2, ev2 1 0 3, ev1 2 1 0, ev1 2 1 1, ev1 2 0 1, ev2 1 1 0, ev1 2 1 2, ev1 2 0 3, ev1 2 0 0, ev1 2 0 2, ev2 1 0 0, ev2 1 0 2, ev2 1 1 1, ev2 0 2 3, ev2 1 0 1, ev2 2 0 1, ev2 2 1 1, ev2 0 2 2, ev2 2 0 2, ev2 2 1 2, ev2 2 1 0, ev2 2 0 0, ev2 0 2 1, ev2 0 3 3, ev2 0 3 1, ev2 0 3 2, ev2 1 2 1, ev2 1 2 3, ev2 1 3 3, ev2 2 1 3, ev2 1 2 0, ev2 1 3 1, ev2 2 0 3, ev1 3 1 1, ev1 3 1 3, ev2 1 3 2, ev2 1 2 2, ev1 3 0 2, ev1 3 0 1, ev2 1 3 0, ev2 2 3 3, ev2 0 3 0, ev2 0 2 0, ev2 2 2 1, ev2 2 3 1, ev2 3 1 3, ev2 3 3 3, ev2 3 2 3, ev2 3 3 0, ev2 3 1 0, ev2 2 3 2, ev2 2 2 2, ev2 3 0 3, ev2 3 0 0, ev2 3 3 1, ev2 3 1 1, ev2 3 2 2"),
+        "V": parse("c2i 0 0, w 0 0 0, c2q 0 0, t1q, c2i 0 1, c3i 0 0, c2q 0 1, c2i 1 1, c3q 0 0, w 1 1 1, c2q 1 1, c2i 1 0, w 2 0 2, c2q 1 0, c3i 0 1, w 1 1 0, c3q 0 1, c3i 1 1, w 3 1 3, t2q 0 0, t2q 0 1, c3i 1 0, c3q 1 1, c3q 1 0, w 2 1 3, t2q 1 1, t2q 1 0, w 2 0 0, c2i 2 1, c2i 2 0, c2q 2 1, w 2 1 2, c2q 2 0, c3i 2 0, c3i 2 1, c3q 2 0, c3q 2 1, ev1 2 1 3, t2q 2 1, t2q 2 0, w 3 0 1, w 3 1 1, w 3 1 2, w 3 0 3, w 3 0 2, w 3 0 0, w 3 1 0, c3i 3 0, c3i 3 1, c3q 3 0, c3q 3 1, c2i 3 1, c2q 3 1, ev2 2 2 0, c2i 3 0, c2q 3 0, ev1 3 1 2, ev1 3 1 0, ev1 3 0 0, ev2 2 3 0, ev1 3 0 3, t2q 3 0, t2q 3 1, ev2 2 2 3, ev2 3 1 2, ev2 3 0 2, ev2 3 0 1, ev2 3 2 0, ev2 3 3 2, ev2 3 2 1"),
+    }
+
+
+def tile_linear2mpo_pa_kernel(tc, t1, core2, core3_bytes, core3_scale, out):
+    nc = tc.nc
+    with ExitStack() as ctx:
+        keep = ctx.enter_context(tc.tile_pool(name="keep", bufs=1))
+        mid = ctx.enter_context(tc.tile_pool(name="mid", bufs=3))
+        mid4 = ctx.enter_context(tc.tile_pool(name="mid4", bufs=4))
+        wide = ctx.enter_context(tc.tile_pool(name="wide", bufs=7))
+        stage = ctx.enter_context(tc.tile_pool(name="stage", bufs=10))
+        psum = ctx.enter_context(tc.psum_pool(name="psum", bufs=8))
+
+        t1_rows = t1.rearrange("i o k -> (i o) k")
+        core2_v = core2.rearrange("(p j) i o q -> p j (i o) q", j=4)
+        core3_v = core3_bytes.rearrange("(g p t) i o q -> g p t (i o q)", g=2, t=4)
+        out_v = out.rearrange("(R s i j) (O o h) q -> s i j o O R (h q)", s=4, i=2, j=2, o=2, h=2)
+
+        ident = keep.tile([128, 128], F32, name="ident")
+        perm = keep.tile([128, 128], F32, name="perm")
+        scale = keep.tile([128, 2, 4], F32, name="scale")
+        t1_raw = keep.tile([128, 4, 512], BF16, name="t1_raw")
+        t1_grouped = keep.tile([128, 512, 4], BF16, name="t1_grouped", align_bytes=64)
+        t1_codes = keep.tile([128, 512], U32, name="t1_codes", align_bytes=64)
+        t1_scales = keep.tile([128, 512], U8, name="t1_scales", align_bytes=64)
+        c2_raw = [keep.tile([128, 4, 1024], BF16, name="c2_raw_%d" % io) for io in range(4)]
+        c3_raw = {}
+        c2_codes, c2_scales, t2_codes, t2_scales, c3_codes, c3_scales = {}, {}, {}, {}, {}, {}
+        for a in range(4):
+            for g in range(2):
+                c2_codes[a, g] = keep.tile([128, 512], U32, name="c2_codes_%d_%d" % (a, g), align_bytes=64)
+                c2_scales[a, g] = keep.tile([128, 512], U8, name="c2_scales_%d_%d" % (a, g), align_bytes=64)
+                t2_codes[a, g] = keep.tile([128, 512], U32, name="t2_codes_%d_%d" % (a, g), align_bytes=64)
+                t2_scales[a, g] = keep.tile([128, 512], U8, name="t2_scales_%d_%d" % (a, g), align_bytes=64)
+                c3_codes[a, g] = keep.tile([128, 512], U32, name="c3_codes_%d_%d" % (a, g), align_bytes=64)
+                c3_scales[a, g] = keep.tile([128, 512], U8, name="c3_scales_%d_%d" % (a, g), align_bytes=64)
+        for h in range(2):
+            for g in range(2):
+                c3_raw[h, g] = keep.tile([128, 4, 1024], U8, name="c3_raw_%d_%d" % (h, g))
+
+        live = {}
+
+        def copy(e, out_ap, in_ap):
+            if e == "S":
+                nc.scalar.copy(out_ap, in_ap)
+            else:
+                nc.vector.tensor_copy(out=out_ap, in_=in_ap)
+
+        def load(kind, a, g):
+            if kind == "t1":
+                nc.sync.dma_start(out=t1_raw[:, 2 * a : 2 * a + 2, :], in_=t1_rows[a * 256 : (a + 1) * 256, :].rearrange("(r p) k -> p r k", r=2))
+            elif kind == "c2" and g is None:
+                nc.sync.dma_start(out=c2_raw[a][:], in_=core2_v[:, :, a, :])
+            elif kind == "c2":
+                cols = slice(g * 512, (g + 1) * 512)
+                nc.sync.dma_start(out=c2_raw[a][:, :, cols], in_=core2_v[:, :, a, cols])
+            else:
+                nc.sync.dma_start(out=c3_raw[a, g][:], in_=core3_v[g][:, :, a * 1024 : (a + 1) * 1024])
+
+        def emit(e, n, *a):
+            if n == "tr":
+                r = a[0]
+                if r % 2 == 0:
+                    live["xt", r // 2] = psum.tile([128, 512], F32, name="bank")
+                xt = live["xt", r // 2][:].rearrange("p (s u n) -> p s u n", s=2, u=2)
+                words = t1_raw[:, r, :].bitcast(F32)
+                for u in range(2):
+                    nc.tensor.transpose(xt[:, r % 2, u, :], words[:, u::2], perm[:])
+            elif n == "t1c":
+                dst = t1_grouped[:, a[0] * 256 : (a[0] + 1) * 256, :].rearrange("p n j -> p (n j)").bitcast(F32)
+                copy(e, dst.rearrange("p (s n u) -> p s n u", s=2, u=2),
+                     live["xt", a[0]][:].rearrange("p (s u n) -> p s n u", s=2, u=2))
+            elif n == "t1q":
+                nc.vector.quantize_mx(out=t1_codes[:].bitcast(FP8X4), scales=t1_scales[:],
+                                      in_=t1_grouped[:].rearrange("p n j -> p (n j)"))
+            elif n == "c2i":
+                io, g = a
+                grouped = mid.tile([128, 512, 4], BF16, name="c2_grouped", align_bytes=64)
+                live["c2g", io, g] = grouped
+                copy(e, grouped[:].rearrange("p (t m) j -> p m j t", t=4),
+                     c2_raw[io][:, :, g * 512 : (g + 1) * 512].rearrange("p j (m t) -> p m j t", t=4))
+            elif n == "c2q":
+                nc.vector.quantize_mx(out=c2_codes[a][:].bitcast(FP8X4), scales=c2_scales[a][:],
+                                      in_=live["c2g", a[0], a[1]][:].rearrange("p n j -> p (n j)"))
+            elif n == "s1":
+                io, g, r = a
+                bank = psum.tile([128, 512], F32, name="bank")
+                live["b1", io, g, r] = bank
+                rows = slice(r * 128, (r + 1) * 128)
+                for t in range(4):
+                    cols = slice(t * 128, (t + 1) * 128)
+                    nc.tensor.matmul_mx(out=bank[:, cols],
+                                        lhsT=c2_codes[io, g][:, cols].bitcast(FP8X4), lhsT_scale=c2_scales[io, g][:, cols],
+                                        rhs=t1_codes[:, rows].bitcast(FP8X4), rhs_scale=t1_scales[:, rows],
+                                        start=True, stop=True)
+            elif n == "ev1":
+                io, g, r = a
+                if ("t2g", io, g) not in live:
+                    live["t2g", io, g] = mid4.tile([128, 512, 4], BF16, name="t2_grouped", align_bytes=64)
+                copy(e, live["t2g", io, g][:, r * 128 : (r + 1) * 128, :],
+                     live["b1", io, g, r][:].rearrange("p (t n) -> p n t", t=4))
+            elif n == "t2q":
+                nc.vector.quantize_mx(out=t2_codes[a][:].bitcast(FP8X4), scales=t2_scales[a][:],
+                                      in_=live["t2g", a[0], a[1]][:].rearrange("p n j -> p (n j)"))
+            elif n == "w":
+                c, g, t = a
+                if ("c3w", c, g) not in live:
+                    live["c3w", c, g] = wide.tile([128, 4, 512], BF16, name="c3_wide", align_bytes=64)
+                src = c3_raw[c // 2, g][:, t, (c % 2) * 512 : (c % 2 + 1) * 512].bitcast(FP8)
+                dst = live["c3w", c, g][:, t, :]
+                if e == "S":
+                    nc.scalar.activation(out=dst, in_=src, func=COPY, scale=scale[:, g, t : t + 1])
+                else:
+                    nc.vector.tensor_scalar(out=dst, in0=src, scalar1=scale[:, g, t : t + 1], scalar2=None, op0=MULT)
+            elif n == "c3i":
+                c, g = a
+                live["c3g", c, g] = mid.tile([128, 512, 4], BF16, name="c3_grouped", align_bytes=64)
+                copy(e, live["c3g", c, g][:].rearrange("p (n i) t -> p n t i", i=4), live["c3w", c, g][:].rearrange("p t (n i) -> p n t i", i=4))
+            elif n == "c3q":
+                nc.vector.quantize_mx(out=c3_codes[a][:].bitcast(FP8X4), scales=c3_scales[a][:],
+                                      in_=live["c3g", a[0], a[1]][:].rearrange("p n j -> p (n j)"))
+            elif n == "s2":
+                io, c, r = a
+                bank = psum.tile([128, 512], F32, name="bank")
+                live["b2", io, c, r] = bank
+                rows = slice(r * 128, (r + 1) * 128)
+                for g in range(2):
+                    nc.tensor.matmul_mx(out=bank[:],
+                                        lhsT=t2_codes[io, g][:, rows].bitcast(FP8X4), lhsT_scale=t2_scales[io, g][:, rows],
+                                        rhs=c3_codes[c, g][:].bitcast(FP8X4), rhs_scale=c3_scales[c, g][:],
+                                        start=(g == 0), stop=(g == 1))
+            elif n == "ev2":
+                io, c, r = a
+                j = c // 2
+                if ("st", io, j, r) not in live:
+                    live["st", io, j, r] = stage.tile([128, 1024], F32, name="result")
+                    live["n", io, j, r] = []
+                result = live["st", io, j, r]
+                copy(e, result[:, (c % 2) * 512 : (c % 2 + 1) * 512], live["b2", io, c, r][:])
+                live["n", io, j, r].append(c)
+                if len(live["n", io, j, r]) == 2:
+                    for s in range(4):
+                        nc.sync.dma_start(out=out_v[s, io // 2, j, io % 2][:, r, :], in_=result[s:128:4, :])
+
+        with tc.manual_schedule():
+            make_identity(nc, ident[:])
+            nc.vector.tensor_copy(out=perm[:].rearrange("p (o i) -> p i o", i=4), in_=ident[:].rearrange("p (i o) -> p i o", i=4))
+            nc.scalar.dma_start(out=scale[:], in_=core3_scale.rearrange("(g p t) a b c -> p g (t a b c)", g=2, t=4))
+            for kind, a, g in LOADS:
+                load(kind, a, g)
+            for step in merge(queues()):
+                emit(*step)

@@ -14,87 +14,16 @@ COPY = mybir.ActivationFunctionType.Copy
 
 FLOPS = 2 * 512 * 512 * 4096 + 2 * 2048 * 1024 * 2048
 
-
-def deps(o):
-    n, a = o[0], o[1:]
-    if n == "t1c":
-        return [("tr", 2 * a[0]), ("tr", 2 * a[0] + 1)]
-    if n == "t1q":
-        return [("t1c", 0), ("t1c", 1)]
-    if n == "c2q":
-        return [("c2i",) + a]
-    if n == "s1":
-        return [("c2q", a[0], a[1]), ("t1q",)]
-    if n == "ev1":
-        return [("s1",) + a]
-    if n == "t2q":
-        return [("ev1", a[0], a[1], r) for r in range(4)]
-    if n == "c3i":
-        return [("w", a[0], a[1], t) for t in range(4)]
-    if n == "c3q":
-        return [("c3i",) + a]
-    if n == "s2":
-        return [("t2q", a[0], 0), ("t2q", a[0], 1), ("c3q", a[1], 0), ("c3q", a[1], 1)]
-    if n == "ev2":
-        return [("s2",) + a]
-    return []
-
-
-def merge(queues):
-    pos = {"PE": 0, "S": 0, "V": 0}
-    done = set()
-    text = []
-    live = 0
-    while len(text) < len(queues["PE"]) + len(queues["S"]) + len(queues["V"]):
-        before = len(text)
-        for e in ("PE", "S", "V"):
-            while pos[e] < len(queues[e]):
-                o = queues[e][pos[e]]
-                opens = e == "PE" and not (o[0] == "tr" and o[1] % 2 == 1)
-                if opens and live >= 8:
-                    break
-                if not all(d in done for d in deps(o)):
-                    break
-                if opens:
-                    live += 1
-                if o[0] in ("ev1", "ev2", "t1c"):
-                    live -= 1
-                text.append((e,) + o)
-                done.add(o)
-                pos[e] += 1
-        assert len(text) > before
-    return text
-
-
-LOADS = [["t1",0,0],["t1",1,0],["c2",0,0],["c3",0,0],["c2",0,1],["c3",0,1],["c2",1,1],["c3",1,1],["c2",1,0],["c3",1,0],["c2",2,1],["c2",3,0],["c2",3,1],["c2",2,0]]
-LAST = (3, 1)
-
-
-def parse(text):
-    ops = []
-    for item in text.split(", "):
-        w = item.split(" ")
-        ops.append((w[0],) + tuple(int(x) for x in w[1:]))
-    return ops
-
-
-def queues():
-    return {
-        "PE": parse("tr 0, tr 1, tr 2, tr 3, s1 0 0 1, s1 0 0 0, s1 0 1 1, s1 0 1 3, s1 0 0 2, s1 0 1 2, s1 1 1 3, s1 1 1 0, s1 0 1 0, s1 0 0 3, s1 1 0 1, s1 1 0 3, s1 1 0 2, s1 1 0 0, s1 1 1 1, s1 1 1 2, s2 0 0 2, s2 0 0 0, s2 0 0 1, s2 0 1 0, s2 0 1 2, s2 0 1 1, s2 1 1 3, s2 0 1 3, s2 1 0 3, s2 0 0 3, s2 1 1 2, s2 1 0 0, s2 1 1 1, s1 2 1 0, s1 2 0 1, s1 2 1 1, s1 2 1 2, s1 2 0 0, s2 1 1 0, s2 1 0 2, s1 2 0 3, s2 1 0 1, s1 2 1 3, s1 2 0 2, s2 1 2 3, s2 1 2 0, s2 0 2 2, s2 0 2 3, s2 2 0 1, s2 2 1 1, s2 2 0 0, s2 2 0 2, s2 2 1 2, s2 2 1 0, s2 2 0 3, s2 0 2 1, s2 1 2 1, s2 2 2 0, s2 0 3 3, s2 0 3 1, s2 0 3 2, s2 1 3 3, s2 1 3 1, s2 2 1 3, s1 3 1 2, s1 3 1 1, s1 3 1 0, s2 1 3 2, s1 3 0 1, s1 3 1 3, s2 1 2 2, s2 2 3 0, s1 3 0 2, s2 2 2 3, s1 3 0 0, s2 1 3 0, s1 3 0 3, s2 2 3 1, s2 2 2 1, s2 2 3 3, s2 0 3 0, s2 0 2 0, s2 3 3 2, s2 3 1 3, s2 3 3 3, s2 3 1 2, s2 3 3 0, s2 3 0 2, s2 3 2 3, s2 3 1 0, s2 2 2 2, s2 2 3 2, s2 3 0 1, s2 3 2 1, s2 3 0 3, s2 3 0 0, s2 3 2 0, s2 3 3 1, s2 3 1 1, s2 3 2 2"),
-        "S": parse("t1c 0, t1c 1, w 0 0 1, w 1 0 0, w 1 0 3, w 0 0 2, w 0 0 3, w 1 0 2, w 0 1 3, w 0 1 2, w 1 1 3, ev1 0 0 0, ev1 0 0 1, ev1 0 0 2, w 1 0 1, w 0 1 0, ev1 0 1 1, w 0 1 1, w 1 1 2, ev1 0 1 3, ev1 0 1 0, ev1 1 1 3, ev1 0 1 2, w 2 0 1, ev1 1 0 3, w 2 1 0, ev1 0 0 3, ev1 1 1 1, ev1 1 0 1, ev1 1 1 2, ev1 1 0 2, ev1 1 1 0, ev1 1 0 0, ev2 0 0 1, ev2 0 0 2, w 2 0 3, ev2 0 1 0, ev2 0 1 2, ev2 0 1 1, w 2 1 1, ev2 0 0 0, ev2 0 1 3, ev2 0 0 3, ev2 1 1 3, ev2 1 1 2, ev2 1 0 3, ev1 2 1 0, ev1 2 1 1, ev1 2 0 1, ev2 1 1 0, ev1 2 1 2, ev1 2 0 3, ev1 2 0 0, ev1 2 0 2, ev2 1 0 0, ev2 1 0 2, ev2 1 1 1, ev2 0 2 3, ev2 1 0 1, ev2 2 0 1, ev2 2 1 1, ev2 0 2 2, ev2 2 0 2, ev2 2 1 2, ev2 2 1 0, ev2 2 0 0, ev2 0 2 1, ev2 0 3 3, ev2 0 3 1, ev2 0 3 2, ev2 1 2 1, ev2 1 2 3, ev2 1 3 3, ev2 2 1 3, ev2 1 2 0, ev2 1 3 1, ev2 2 0 3, ev1 3 1 1, ev1 3 1 3, ev2 1 3 2, ev2 1 2 2, ev1 3 0 2, ev1 3 0 1, ev2 1 3 0, ev2 2 3 3, ev2 0 3 0, ev2 0 2 0, ev2 2 2 1, ev2 2 3 1, ev2 3 1 3, ev2 3 3 3, ev2 3 2 3, ev2 3 3 0, ev2 3 1 0, ev2 2 3 2, ev2 2 2 2, ev2 3 0 3, ev2 3 0 0, ev2 3 3 1, ev2 3 1 1, ev2 3 2 2"),
-        "V": parse("c2i 0 0, w 0 0 0, c2q 0 0, t1q, c2i 0 1, c3i 0 0, c2q 0 1, c2i 1 1, c3q 0 0, w 1 1 1, c2q 1 1, c2i 1 0, w 2 0 2, c2q 1 0, c3i 0 1, w 1 1 0, c3q 0 1, c3i 1 1, w 3 1 3, t2q 0 0, t2q 0 1, c3i 1 0, c3q 1 1, c3q 1 0, w 2 1 3, t2q 1 1, t2q 1 0, w 2 0 0, c2i 2 1, c2i 2 0, c2q 2 1, w 2 1 2, c2q 2 0, c3i 2 0, c3i 2 1, c3q 2 0, c3q 2 1, ev1 2 1 3, t2q 2 1, t2q 2 0, w 3 0 1, w 3 1 1, w 3 1 2, w 3 0 3, w 3 0 2, w 3 0 0, w 3 1 0, c3i 3 0, c3i 3 1, c3q 3 0, c3q 3 1, c2i 3 1, c2q 3 1, ev2 2 2 0, c2i 3 0, c2q 3 0, ev1 3 1 2, ev1 3 1 0, ev1 3 0 0, ev2 2 3 0, ev1 3 0 3, t2q 3 0, t2q 3 1, ev2 2 2 3, ev2 3 1 2, ev2 3 0 2, ev2 3 0 1, ev2 3 2 0, ev2 3 3 2, ev2 3 2 1"),
-    }
+VSHARE = [0, 3, 3, 3, 3, 3, 2]
 
 
 def tile_linear2mpo_pa_kernel(tc, t1, core2, core3_bytes, core3_scale, out):
     nc = tc.nc
     with ExitStack() as ctx:
         keep = ctx.enter_context(tc.tile_pool(name="keep", bufs=1))
-        mid = ctx.enter_context(tc.tile_pool(name="mid", bufs=3))
-        mid4 = ctx.enter_context(tc.tile_pool(name="mid4", bufs=4))
-        wide = ctx.enter_context(tc.tile_pool(name="wide", bufs=7))
-        stage = ctx.enter_context(tc.tile_pool(name="stage", bufs=10))
-        psum = ctx.enter_context(tc.psum_pool(name="psum", bufs=8))
+        work = ctx.enter_context(tc.tile_pool(name="work", bufs=3))
+        stage = ctx.enter_context(tc.tile_pool(name="stage", bufs=16))
+        psum = ctx.enter_context(tc.psum_pool(name="psum", bufs=1))
 
         t1_rows = t1.rearrange("i o k -> (i o) k")
         core2_v = core2.rearrange("(p j) i o q -> p j (i o) q", j=4)
@@ -103,135 +32,304 @@ def tile_linear2mpo_pa_kernel(tc, t1, core2, core3_bytes, core3_scale, out):
 
         ident = keep.tile([128, 128], F32, name="ident")
         perm = keep.tile([128, 128], F32, name="perm")
+        ident_bf = keep.tile([128, 128], BF16, name="ident_bf")
         scale = keep.tile([128, 2, 4], F32, name="scale")
-        t1_raw = keep.tile([128, 4, 512], BF16, name="t1_raw")
+        t1_raw = [keep.tile([128, 2, 512], BF16, name="t1_raw_%d" % a) for a in range(2)]
         t1_grouped = keep.tile([128, 512, 4], BF16, name="t1_grouped", align_bytes=64)
         t1_codes = keep.tile([128, 512], U32, name="t1_codes", align_bytes=64)
         t1_scales = keep.tile([128, 512], U8, name="t1_scales", align_bytes=64)
-        c2_raw = [keep.tile([128, 4, 1024], BF16, name="c2_raw_%d" % io) for io in range(4)]
-        c3_raw = {}
+        banks = [psum.tile([128, 512], F32, name="bank_%d" % b) for b in range(8)]
+        c2_raw, c3_raw = {}, {}
         c2_codes, c2_scales, t2_codes, t2_scales, c3_codes, c3_scales = {}, {}, {}, {}, {}, {}
         for a in range(4):
+            t2_codes[a] = keep.tile([128, 1024], U32, name="t2_codes_%d" % a, align_bytes=64)
+            t2_scales[a] = keep.tile([128, 1024], U8, name="t2_scales_%d" % a, align_bytes=64)
             for g in range(2):
                 c2_codes[a, g] = keep.tile([128, 512], U32, name="c2_codes_%d_%d" % (a, g), align_bytes=64)
                 c2_scales[a, g] = keep.tile([128, 512], U8, name="c2_scales_%d_%d" % (a, g), align_bytes=64)
-                t2_codes[a, g] = keep.tile([128, 512], U32, name="t2_codes_%d_%d" % (a, g), align_bytes=64)
-                t2_scales[a, g] = keep.tile([128, 512], U8, name="t2_scales_%d_%d" % (a, g), align_bytes=64)
                 c3_codes[a, g] = keep.tile([128, 512], U32, name="c3_codes_%d_%d" % (a, g), align_bytes=64)
                 c3_scales[a, g] = keep.tile([128, 512], U8, name="c3_scales_%d_%d" % (a, g), align_bytes=64)
-        for h in range(2):
-            for g in range(2):
-                c3_raw[h, g] = keep.tile([128, 4, 1024], U8, name="c3_raw_%d_%d" % (h, g))
 
         live = {}
+        used = []
 
-        def copy(e, out_ap, in_ap):
-            if e == "S":
-                nc.scalar.copy(out_ap, in_ap)
+        def next_bank():
+            used.append(len(used))
+            return banks[used[-1] % 8]
+
+        def copy(engine, dst, src):
+            if engine == "S":
+                nc.scalar.copy(dst, src)
             else:
-                nc.vector.tensor_copy(out=out_ap, in_=in_ap)
+                nc.vector.tensor_copy(out=dst, in_=src)
 
-        def load(kind, a, g):
-            if kind == "t1":
-                nc.sync.dma_start(out=t1_raw[:, 2 * a : 2 * a + 2, :], in_=t1_rows[a * 256 : (a + 1) * 256, :].rearrange("(r p) k -> p r k", r=2))
-            elif kind == "c2" and g is None:
-                nc.sync.dma_start(out=c2_raw[a][:], in_=core2_v[:, :, a, :])
-            elif kind == "c2":
-                cols = slice(g * 512, (g + 1) * 512)
-                nc.sync.dma_start(out=c2_raw[a][:, :, cols], in_=core2_v[:, :, a, cols])
-            else:
-                nc.sync.dma_start(out=c3_raw[a, g][:], in_=core3_v[g][:, :, a * 1024 : (a + 1) * 1024])
+        def load_t1(a):
+            nc.sync.dma_start(out=t1_raw[a][:], in_=t1_rows[a * 256 : (a + 1) * 256, :].rearrange("(r p) k -> p r k", r=2))
 
-        def emit(e, n, *a):
-            if n == "tr":
-                r = a[0]
-                if r % 2 == 0:
-                    live["xt", r // 2] = psum.tile([128, 512], F32, name="bank")
-                xt = live["xt", r // 2][:].rearrange("p (s u n) -> p s u n", s=2, u=2)
-                words = t1_raw[:, r, :].bitcast(F32)
+        def load_c2_half(io, g):
+            raw = keep.tile([128, 4, 512], BF16, name="c2_raw_%d_%d" % (io, g))
+            c2_raw[io, g] = raw[:]
+            nc.sync.dma_start(out=raw[:], in_=core2_v[:, :, io, g * 512 : (g + 1) * 512])
+
+        def load_c2(io):
+            raw = keep.tile([128, 4, 1024], BF16, name="c2_raw_%d" % io)
+            for g in range(2):
+                c2_raw[io, g] = raw[:, :, g * 512 : (g + 1) * 512]
+            nc.sync.dma_start(out=raw[:], in_=core2_v[:, :, io, :])
+
+        def load_c3(j, g):
+            raw = keep.tile([128, 4, 1024], U8, name="c3_raw_%d_%d" % (j, g))
+            for h in range(2):
+                c3_raw[2 * j + h, g] = raw[:, :, h * 512 : (h + 1) * 512]
+            nc.sync.dma_start(out=raw[:], in_=core3_v[g][:, :, j * 1024 : (j + 1) * 1024])
+
+        def quantize(codes, scales, grouped):
+            nc.vector.quantize_mx(out=codes.bitcast(FP8X4), scales=scales, in_=grouped)
+
+        def turn_t1(a, engine):
+            bank = next_bank()
+            xt = bank[:].rearrange("p (s u n) -> p s u n", s=2, u=2)
+            for s in range(2):
+                words = t1_raw[a][:, s, :].bitcast(F32)
                 for u in range(2):
-                    nc.tensor.transpose(xt[:, r % 2, u, :], words[:, u::2], perm[:])
-            elif n == "t1c":
-                dst = t1_grouped[:, a[0] * 256 : (a[0] + 1) * 256, :].rearrange("p n j -> p (n j)").bitcast(F32)
-                copy(e, dst.rearrange("p (s n u) -> p s n u", s=2, u=2),
-                     live["xt", a[0]][:].rearrange("p (s u n) -> p s n u", s=2, u=2))
-            elif n == "t1q":
-                nc.vector.quantize_mx(out=t1_codes[:].bitcast(FP8X4), scales=t1_scales[:],
-                                      in_=t1_grouped[:].rearrange("p n j -> p (n j)"))
-            elif n == "c2i":
-                io, g = a
-                grouped = mid.tile([128, 512, 4], BF16, name="c2_grouped", align_bytes=64)
-                live["c2g", io, g] = grouped
-                copy(e, grouped[:].rearrange("p (t m) j -> p m j t", t=4),
-                     c2_raw[io][:, :, g * 512 : (g + 1) * 512].rearrange("p j (m t) -> p m j t", t=4))
-            elif n == "c2q":
-                nc.vector.quantize_mx(out=c2_codes[a][:].bitcast(FP8X4), scales=c2_scales[a][:],
-                                      in_=live["c2g", a[0], a[1]][:].rearrange("p n j -> p (n j)"))
-            elif n == "s1":
-                io, g, r = a
-                bank = psum.tile([128, 512], F32, name="bank")
-                live["b1", io, g, r] = bank
-                rows = slice(r * 128, (r + 1) * 128)
-                for t in range(4):
-                    cols = slice(t * 128, (t + 1) * 128)
-                    nc.tensor.matmul_mx(out=bank[:, cols],
-                                        lhsT=c2_codes[io, g][:, cols].bitcast(FP8X4), lhsT_scale=c2_scales[io, g][:, cols],
-                                        rhs=t1_codes[:, rows].bitcast(FP8X4), rhs_scale=t1_scales[:, rows],
-                                        start=True, stop=True)
-            elif n == "ev1":
-                io, g, r = a
-                if ("t2g", io, g) not in live:
-                    live["t2g", io, g] = mid4.tile([128, 512, 4], BF16, name="t2_grouped", align_bytes=64)
-                copy(e, live["t2g", io, g][:, r * 128 : (r + 1) * 128, :],
-                     live["b1", io, g, r][:].rearrange("p (t n) -> p n t", t=4))
-            elif n == "t2q":
-                nc.vector.quantize_mx(out=t2_codes[a][:].bitcast(FP8X4), scales=t2_scales[a][:],
-                                      in_=live["t2g", a[0], a[1]][:].rearrange("p n j -> p (n j)"))
-            elif n == "w":
-                c, g, t = a
-                if ("c3w", c, g) not in live:
-                    live["c3w", c, g] = wide.tile([128, 4, 512], BF16, name="c3_wide", align_bytes=64)
-                src = c3_raw[c // 2, g][:, t, (c % 2) * 512 : (c % 2 + 1) * 512].bitcast(FP8)
-                dst = live["c3w", c, g][:, t, :]
-                if e == "S":
-                    nc.scalar.activation(out=dst, in_=src, func=COPY, scale=scale[:, g, t : t + 1])
-                else:
-                    nc.vector.tensor_scalar(out=dst, in0=src, scalar1=scale[:, g, t : t + 1], scalar2=None, op0=MULT)
-            elif n == "c3i":
-                c, g = a
-                live["c3g", c, g] = mid.tile([128, 512, 4], BF16, name="c3_grouped", align_bytes=64)
-                copy(e, live["c3g", c, g][:].rearrange("p (n i) t -> p n t i", i=4), live["c3w", c, g][:].rearrange("p t (n i) -> p n t i", i=4))
-            elif n == "c3q":
-                nc.vector.quantize_mx(out=c3_codes[a][:].bitcast(FP8X4), scales=c3_scales[a][:],
-                                      in_=live["c3g", a[0], a[1]][:].rearrange("p n j -> p (n j)"))
-            elif n == "s2":
-                io, c, r = a
-                bank = psum.tile([128, 512], F32, name="bank")
-                live["b2", io, c, r] = bank
-                rows = slice(r * 128, (r + 1) * 128)
-                for g in range(2):
-                    nc.tensor.matmul_mx(out=bank[:],
-                                        lhsT=t2_codes[io, g][:, rows].bitcast(FP8X4), lhsT_scale=t2_scales[io, g][:, rows],
-                                        rhs=c3_codes[c, g][:].bitcast(FP8X4), rhs_scale=c3_scales[c, g][:],
-                                        start=(g == 0), stop=(g == 1))
-            elif n == "ev2":
-                io, c, r = a
-                j = c // 2
-                if ("st", io, j, r) not in live:
-                    live["st", io, j, r] = stage.tile([128, 1024], F32, name="result")
-                    live["n", io, j, r] = []
-                result = live["st", io, j, r]
-                copy(e, result[:, (c % 2) * 512 : (c % 2 + 1) * 512], live["b2", io, c, r][:])
-                live["n", io, j, r].append(c)
-                if len(live["n", io, j, r]) == 2:
-                    for s in range(4):
-                        nc.sync.dma_start(out=out_v[s, io // 2, j, io % 2][:, r, :], in_=result[s:128:4, :])
+                    nc.tensor.transpose(xt[:, s, u, :], words[:, u::2], perm[:])
+            dst = t1_grouped[:, a * 256 : (a + 1) * 256, :].rearrange("p n j -> p (n j)").bitcast(F32)
+            copy(engine, dst.rearrange("p (s n u) -> p s n u", s=2, u=2), xt.rearrange("p s u n -> p s n u"))
+
+        def quantize_t1(a):
+            cols = slice(a * 256, (a + 1) * 256)
+            quantize(t1_codes[:, cols], t1_scales[:, cols], t1_grouped[:, cols, :].rearrange("p n j -> p (n j)"))
+
+        def group_c2(io, g, engine):
+            grouped = work.tile([128, 2048], BF16, name="c2_grouped", align_bytes=64)
+            live["c2g", io, g] = grouped
+            if engine == "V":
+                copy("V", grouped[:].rearrange("p (t m j) -> p m j t", t=4, j=4), c2_raw[io, g].rearrange("p j (m t) -> p m j t", t=4))
+            else:
+                src = c2_raw[io, g].rearrange("p j (m t) -> p t m j", t=4)
+                for half in range(2):
+                    bank = next_bank()[:].bitcast(BF16)
+                    for e in range(2):
+                        nc.tensor.matmul(out=bank[:, e * 512 : (e + 1) * 512], lhsT=ident_bf[:], rhs=src[:, 2 * half + e], start=True, stop=True)
+                    copy("S", grouped[:, half * 1024 : (half + 1) * 1024], bank)
+
+        def quantize_c2(io, g):
+            quantize(c2_codes[io, g][:], c2_scales[io, g][:], live["c2g", io, g][:])
+
+        def widen_c3(c, g, t, engine):
+            if t == 0:
+                live["c3w", c, g] = work.tile([128, 4, 512], BF16, name="c3_wide", align_bytes=64)
+            src = c3_raw[c, g][:, t, :].bitcast(FP8)
+            dst = live["c3w", c, g][:, t, :]
+            if engine == "S":
+                nc.scalar.activation(out=dst, in_=src, func=COPY, scale=scale[:, g, t : t + 1])
+            else:
+                nc.vector.tensor_scalar(out=dst, in0=src, scalar1=scale[:, g, t : t + 1], scalar2=None, op0=MULT)
+
+        def widen_all(c, g, engine):
+            for t in range(4):
+                widen_c3(c, g, t, engine)
+
+        def group_c3(c, g, engine):
+            grouped = work.tile([128, 2048], BF16, name="c3_grouped", align_bytes=64)
+            live["c3g", c, g] = grouped
+            wide = live["c3w", c, g]
+            if engine == "V":
+                copy("V", grouped[:].rearrange("p (n i t) -> p n t i", i=4, t=4), wide[:].rearrange("p t (n i) -> p n t i", i=4))
+            else:
+                src = wide[:].rearrange("p t (x n) -> p x n t", x=4)
+                for half in range(2):
+                    bank = next_bank()[:].bitcast(BF16)
+                    for e in range(2):
+                        nc.tensor.matmul(out=bank[:, e * 512 : (e + 1) * 512], lhsT=ident_bf[:], rhs=src[:, 2 * half + e], start=True, stop=True)
+                    copy("S", grouped[:, half * 1024 : (half + 1) * 1024], bank)
+
+        def quantize_c3(c, g):
+            quantize(c3_codes[c, g][:], c3_scales[c, g][:], live["c3g", c, g][:])
+
+        def step1(io, r, g):
+            bank = next_bank()
+            rows = slice(r * 128, (r + 1) * 128)
+            for t in range(4):
+                cols = slice(t * 128, (t + 1) * 128)
+                nc.tensor.matmul_mx(out=bank[:, cols],
+                                    lhsT=c2_codes[io, g][:, cols].bitcast(FP8X4), lhsT_scale=c2_scales[io, g][:, cols],
+                                    rhs=t1_codes[:, rows].bitcast(FP8X4), rhs_scale=t1_scales[:, rows],
+                                    start=True, stop=True)
+            live["b1", io, r, g] = bank
+
+        def empty1(io, r, g, engine):
+            if ("t2g", io, r) not in live:
+                live["t2g", io, r] = work.tile([128, 2, 128, 4], BF16, name="t2_grouped", align_bytes=64, bufs=4)
+            copy(engine, live["t2g", io, r][:, g], live["b1", io, r, g][:].rearrange("p (t n) -> p n t", t=4))
+
+        def quantize_t2(io, r):
+            cols = slice(r * 256, (r + 1) * 256)
+            quantize(t2_codes[io][:, cols], t2_scales[io][:, cols], live["t2g", io, r][:].rearrange("p g n t -> p (g n t)"))
+
+        def step2(io, c, r):
+            bank = next_bank()
+            for g in range(2):
+                rows = slice(r * 256 + g * 128, r * 256 + (g + 1) * 128)
+                nc.tensor.matmul_mx(out=bank[:],
+                                    lhsT=t2_codes[io][:, rows].bitcast(FP8X4), lhsT_scale=t2_scales[io][:, rows],
+                                    rhs=c3_codes[c, g][:].bitcast(FP8X4), rhs_scale=c3_scales[c, g][:],
+                                    start=(g == 0), stop=(g == 1))
+            live["b2", io, c, r] = bank
+
+        def empty2(io, c, r, engine):
+            j, h = c // 2, c % 2
+            form = store_form(io, c, r)
+            if form == "pair":
+                key = (io, j, r // 2, form)
+                shape = [128, 2, 1024]
+                spot = (r % 2, slice(h * 512, (h + 1) * 512))
+                target = [out_v[s, io // 2, j, io % 2][:, 2 * (r // 2) : 2 * (r // 2) + 2, :] for s in range(4)]
+            elif form == "row":
+                key = (io, r, form)
+                shape = [128, 2, 1024]
+                spot = (j, slice(h * 512, (h + 1) * 512))
+                target = [out_j[s, io // 2, io % 2, r] for s in range(4)]
+            elif form == "half":
+                key = (io, r, j, form)
+                shape = [128, 1, 1024]
+                spot = (0, slice(h * 512, (h + 1) * 512))
+                target = [out_v[s, io // 2, j, io % 2][:, r : r + 1, :] for s in range(4)]
+            else:
+                key = (io, c, form)
+                shape = [128, 4, 512]
+                spot = (r, slice(0, 512))
+                target = [out_v[s, io // 2, j, io % 2][:, :, h * 512 : (h + 1) * 512] for s in range(4)]
+            if ("st",) + key not in live:
+                live[("st",) + key] = stage.tile(shape, F32, name="result", bufs=8)
+                live[("n",) + key] = []
+            result = live[("st",) + key]
+            copy(engine, result[:, spot[0], spot[1]], live["b2", io, c, r][:])
+            live[("n",) + key].append(c)
+            if len(live[("n",) + key]) == (2 if form == "half" else 4):
+                for s in range(4):
+                    nc.sync.dma_start(out=target[s], in_=result[s:128:4])
+
+        out_j = out.rearrange("(R s i j) (O o h) q -> s i o R O j (h q)", s=4, i=2, j=2, o=2, h=2)
+
+        def run(jobs):
+            for job in jobs:
+                job[0](*job[1:])
+
+        def one_round(products, tiles, steps, vector1=(), vector2=()):
+            n = len(products)
+            for k in range(n):
+                step2(*products[k])
+                for tile in waiting:
+                    quantize_t2(*tile)
+                waiting.clear()
+                run(steps[len(steps) * k // n : len(steps) * (k + 1) // n])
+                empty2(*products[k], "V" if k in vector2 else "S")
+                for io, r in tiles[k :: n] if len(tiles) != 2 else tiles[k // 2 : k // 2 + 1 - k % 2]:
+                    step1(io, r, 0)
+                    empty1(io, r, 0, "S")
+                    step1(io, r, 1)
+                    empty1(io, r, 1, "V" if r in vector1 else "S")
+                    waiting.append((io, r))
+
+        waiting = []
+
+        def W(c, g, e="V"):
+            return (widen_all, c, g, e)
+
+        def I3(c, g, e="V"):
+            return (group_c3, c, g, e)
+
+        def Q3(c, g):
+            return (quantize_c3, c, g)
+
+        def I2(io, g, e="V"):
+            return (group_c2, io, g, e)
+
+        def Q2(io, g):
+            return (quantize_c2, io, g)
+
+        def col(io, c):
+            return [(io, c, r) for r in range(4)]
+
+        def pair(io, j, p):
+            return [(io, 2 * j + h, 2 * p + e) for e in range(2) for h in range(2)]
+
+        def row(io, r):
+            return [(io, c, r) for c in range(4)]
+
+        def store_form(io, c, r):
+            return ("half" if (io, r) >= (3, 2) else "row") if io >= 2 else ("pair" if c < 2 else "col")
 
         with tc.manual_schedule():
+            nc.scalar.dma_start(out=scale[:], in_=core3_scale.rearrange("(g p t) a b c -> p g (t a b c)", g=2, t=4))
+            load_c3(0, 0)
+            load_c2_half(0, 0)
+            load_t1(0)
+            load_c2_half(0, 1)
+            load_c3(0, 1)
+            load_t1(1)
+            load_c2(1)
+            load_c3(1, 0)
+            load_c3(1, 1)
+            load_c2(2)
+            load_c2(3)
             make_identity(nc, ident[:])
             nc.vector.tensor_copy(out=perm[:].rearrange("p (o i) -> p i o", i=4), in_=ident[:].rearrange("p (i o) -> p i o", i=4))
-            nc.scalar.dma_start(out=scale[:], in_=core3_scale.rearrange("(g p t) a b c -> p g (t a b c)", g=2, t=4))
-            for kind, a, g in LOADS:
-                load(kind, a, g)
-            for step in merge(queues()):
-                emit(*step)
+            nc.vector.tensor_copy(out=ident_bf[:], in_=ident[:])
+
+            widen_all(0, 0, "V")
+            widen_all(1, 0, "S")
+            group_c3(0, 0, "P")
+            group_c2(0, 0, "V")
+            turn_t1(0, "S")
+            group_c3(1, 0, "P")
+            quantize_c2(0, 0)
+            quantize_c3(0, 0)
+            quantize_t1(0)
+            group_c2(0, 1, "V")
+            for r in range(2):
+                step1(0, r, 0)
+                empty1(0, r, 0, "S")
+            widen_all(0, 1, "V")
+            turn_t1(1, "S")
+            group_c3(0, 1, "P")
+            quantize_c2(0, 1)
+            widen_all(1, 1, "V")
+            for r in range(2):
+                step1(0, r, 1)
+                empty1(0, r, 1, "S")
+            quantize_t1(1)
+            quantize_c3(0, 1)
+            group_c3(1, 1, "V")
+            quantize_t2(0, 0)
+            quantize_c3(1, 0)
+            quantize_t2(0, 1)
+            quantize_c3(1, 1)
+            for r in range(2, 4):
+                for g in range(2):
+                    step1(0, r, g)
+                    empty1(0, r, g, "S")
+            group_c2(1, 0, "P")
+            group_c2(1, 1, "V")
+            quantize_t2(0, 2)
+            quantize_c2(1, 0)
+            quantize_t2(0, 3)
+            quantize_c2(1, 1)
+
+            one_round([(0,0,0),(0,0,1),(0,1,0),(0,1,1)], [], [W(2, 0)])
+            one_round(pair(0, 0, 1), [(1, 0), (1, 1)], [W(2, 1), I3(2, 0)])
+            one_round(pair(1, 0, 0), [(1, 2), (1, 3)], [I3(2, 1), Q3(2, 0), Q3(2,1)])
+            one_round(pair(1, 0, 1), [], [W(3, 0), W(3, 1), I3(3, 0)])
+            one_round(col(0, 2), [], [I3(3, 1), Q3(3, 0), Q3(3, 1)])
+            one_round(col(1, 2), [], [I2(2, 0), I2(2, 1)])
+            one_round(col(0, 3), [], [Q2(2, 0), Q2(2, 1)])
+            one_round(col(1, 3), [(2, 0), (2, 1)], [], (0, 1))
+            one_round(row(2, 0), [(2, 2)], [I2(3, 0)], (2,))
+            one_round(row(2, 1), [(2, 3)], [I2(3, 1)], (3,))
+            one_round(row(2, 2), [], [Q2(3, 0), Q2(3, 1)], (), (2,))
+            one_round(row(2, 3), [(3, 0), (3, 1)], [], (0, 1))
+            one_round(row(3, 0), [(3, 2)], [], (2,), (2,))
+            one_round(row(3, 1), [(3, 3)], [], (3,), (2,))
+            one_round(row(3, 2), [], [], (), (1, 3))
+            one_round(row(3, 3), [], [], (), (1, 3))

@@ -32,7 +32,6 @@ def tile_linear2mpo_pa_kernel(tc, t1, core2, core3_bytes, core3_scale, out):
 
         ident = keep.tile([128, 128], F32, name="ident")
         perm = keep.tile([128, 128], F32, name="perm")
-        ident_bf = keep.tile([128, 128], BF16, name="ident_bf")
         scale = keep.tile([128, 2, 4], F32, name="scale")
         t1_raw = [keep.tile([128, 2, 512], BF16, name="t1_raw_%d" % a) for a in range(2)]
         t1_grouped = keep.tile([128, 512, 4], BF16, name="t1_grouped", align_bytes=64)
@@ -103,46 +102,30 @@ def tile_linear2mpo_pa_kernel(tc, t1, core2, core3_bytes, core3_scale, out):
         def group_c2(io, g, engine):
             grouped = work.tile([128, 2048], BF16, name="c2_grouped", align_bytes=64)
             live["c2g", io, g] = grouped
-            if engine == "V":
-                copy("V", grouped[:].rearrange("p (t m j) -> p m j t", t=4, j=4), c2_raw[io, g].rearrange("p j (m t) -> p m j t", t=4))
-            else:
-                src = c2_raw[io, g].rearrange("p j (m t) -> p t m j", t=4)
-                for half in range(2):
-                    bank = next_bank()[:].bitcast(BF16)
-                    for e in range(2):
-                        nc.tensor.matmul(out=bank[:, e * 512 : (e + 1) * 512], lhsT=ident_bf[:], rhs=src[:, 2 * half + e], start=True, stop=True)
-                    copy("S", grouped[:, half * 1024 : (half + 1) * 1024], bank)
+            copy(engine, grouped[:].rearrange("p (t m j) -> p m j t", t=4, j=4), c2_raw[io, g].rearrange("p j (m t) -> p m j t", t=4))
 
         def quantize_c2(io, g):
             quantize(c2_codes[io, g][:], c2_scales[io, g][:], live["c2g", io, g][:])
 
-        def widen_c3(c, g, t, engine):
-            if t == 0:
-                live["c3w", c, g] = work.tile([128, 4, 512], BF16, name="c3_wide", align_bytes=64)
-            src = c3_raw[c, g][:, t, :].bitcast(FP8)
-            dst = live["c3w", c, g][:, t, :]
-            if engine == "S":
-                nc.scalar.activation(out=dst, in_=src, func=COPY, scale=scale[:, g, t : t + 1])
-            else:
-                nc.vector.tensor_scalar(out=dst, in0=src, scalar1=scale[:, g, t : t + 1], scalar2=None, op0=MULT)
-
         def widen_all(c, g, engine):
+            wide = work.tile([128, 2048], BF16, name="c3_wide", align_bytes=64)
+            live["c3w", c, g] = (wide, engine)
             for t in range(4):
-                widen_c3(c, g, t, engine)
+                src = c3_raw[c, g][:, t, :].bitcast(FP8)
+                if engine == "S":
+                    nc.scalar.activation(out=wide[:, t * 512 : (t + 1) * 512], in_=src, func=COPY, scale=scale[:, g, t : t + 1])
+                else:
+                    dst = wide[:].rearrange("p (u n e) -> p u e n", u=2, e=2)[:, t // 2, t % 2, :]
+                    nc.vector.tensor_scalar(out=dst, in0=src, scalar1=scale[:, g, t : t + 1], scalar2=None, op0=MULT)
 
         def group_c3(c, g, engine):
             grouped = work.tile([128, 2048], BF16, name="c3_grouped", align_bytes=64)
             live["c3g", c, g] = grouped
-            wide = live["c3w", c, g]
-            if engine == "V":
-                copy("V", grouped[:].rearrange("p (n i t) -> p n t i", i=4, t=4), wide[:].rearrange("p t (n i) -> p n t i", i=4))
+            wide, widened_by = live["c3w", c, g]
+            if widened_by == "S":
+                copy(engine, grouped[:].rearrange("p (n i t) -> p n t i", i=4, t=4), wide[:].rearrange("p (t n i) -> p n t i", t=4, i=4))
             else:
-                src = wide[:].rearrange("p t (x n) -> p x n t", x=4)
-                for half in range(2):
-                    bank = next_bank()[:].bitcast(BF16)
-                    for e in range(2):
-                        nc.tensor.matmul(out=bank[:, e * 512 : (e + 1) * 512], lhsT=ident_bf[:], rhs=src[:, 2 * half + e], start=True, stop=True)
-                    copy("S", grouped[:, half * 1024 : (half + 1) * 1024], bank)
+                copy(engine, grouped[:].bitcast(F32).rearrange("p (n u) -> p n u", u=2), wide[:].bitcast(F32).rearrange("p (u n) -> p n u", u=2))
 
         def quantize_c3(c, g):
             quantize(c3_codes[c, g][:], c3_scales[c, g][:], live["c3g", c, g][:])
@@ -276,50 +259,39 @@ def tile_linear2mpo_pa_kernel(tc, t1, core2, core3_bytes, core3_scale, out):
             load_c2(3)
             make_identity(nc, ident[:])
             nc.vector.tensor_copy(out=perm[:].rearrange("p (o i) -> p i o", i=4), in_=ident[:].rearrange("p (i o) -> p i o", i=4))
-            nc.vector.tensor_copy(out=ident_bf[:], in_=ident[:])
 
             widen_all(0, 0, "V")
             widen_all(1, 0, "S")
-            group_c3(0, 0, "P")
             group_c2(0, 0, "V")
             turn_t1(0, "S")
-            group_c3(1, 0, "P")
+            group_c3(0, 0, "S")
             quantize_c2(0, 0)
-            quantize_c3(0, 0)
             quantize_t1(0)
             group_c2(0, 1, "V")
             for r in range(2):
                 step1(0, r, 0)
                 empty1(0, r, 0, "S")
             widen_all(0, 1, "V")
+            widen_all(1, 1, "S")
             turn_t1(1, "S")
-            group_c3(0, 1, "P")
             quantize_c2(0, 1)
-            widen_all(1, 1, "V")
+            group_c3(0, 1, "V")
             for r in range(2):
                 step1(0, r, 1)
                 empty1(0, r, 1, "S")
-            quantize_t1(1)
+            quantize_c3(0, 0)
             quantize_c3(0, 1)
-            group_c3(1, 1, "V")
+            quantize_t1(1)
+            group_c3(1, 0, "V")
             quantize_t2(0, 0)
-            quantize_c3(1, 0)
             quantize_t2(0, 1)
+            group_c3(1, 1, "V")
+            quantize_c3(1, 0)
             quantize_c3(1, 1)
-            for r in range(2, 4):
-                for g in range(2):
-                    step1(0, r, g)
-                    empty1(0, r, g, "S")
-            group_c2(1, 0, "P")
-            group_c2(1, 1, "V")
-            quantize_t2(0, 2)
-            quantize_c2(1, 0)
-            quantize_t2(0, 3)
-            quantize_c2(1, 1)
 
-            one_round([(0,0,0),(0,0,1),(0,1,0),(0,1,1)], [], [W(2, 0)])
-            one_round(pair(0, 0, 1), [(1, 0), (1, 1)], [W(2, 1), I3(2, 0)])
-            one_round(pair(1, 0, 0), [(1, 2), (1, 3)], [I3(2, 1), Q3(2, 0), Q3(2,1)])
+            one_round([(0,0,0),(0,0,1),(0,1,0),(0,1,1)], [(0, 2), (0, 3)], [I2(1, 0), I2(1, 1), Q2(1, 0), Q2(1, 1)])
+            one_round(pair(0, 0, 1), [(1, 0), (1, 1)], [W(2, 0), W(2, 1)])
+            one_round(pair(1, 0, 0), [(1, 2), (1, 3)], [I3(2, 0), I3(2, 1), Q3(2, 0), Q3(2,1)])
             one_round(pair(1, 0, 1), [], [W(3, 0), W(3, 1), I3(3, 0)])
             one_round(col(0, 2), [], [I3(3, 1), Q3(3, 0), Q3(3, 1)])
             one_round(col(1, 2), [], [I2(2, 0), I2(2, 1)])

@@ -108,24 +108,21 @@ def tile_linear2mpo_pa_kernel(tc, t1, core2, core3_bytes, core3_scale, out):
             quantize(c2_codes[io, g][:], c2_scales[io, g][:], live["c2g", io, g][:])
 
         def widen_all(c, g, engine):
-            wide = work.tile([128, 2048], BF16, name="c3_wide", align_bytes=64)
+            wide = work.tile([128, 2048], BF16, name="c3_wide", align_bytes=64, bufs=4)
             live["c3w", c, g] = (wide, engine)
             for t in range(4):
                 src = c3_raw[c, g][:, t, :].bitcast(FP8)
                 if engine == "S":
                     nc.scalar.activation(out=wide[:, t * 512 : (t + 1) * 512], in_=src, func=COPY, scale=scale[:, g, t : t + 1])
                 else:
-                    dst = wide[:].rearrange("p (u n e) -> p u e n", u=2, e=2)[:, t // 2, t % 2, :]
+                    dst = wide[:, t * 512 : (t + 1) * 512]
                     nc.vector.tensor_scalar(out=dst, in0=src, scalar1=scale[:, g, t : t + 1], scalar2=None, op0=MULT)
 
         def group_c3(c, g, engine):
-            grouped = work.tile([128, 2048], BF16, name="c3_grouped", align_bytes=64)
+            grouped = work.tile([128, 2048], BF16, name="c3_grouped", align_bytes=64, bufs=4)
             live["c3g", c, g] = grouped
             wide, widened_by = live["c3w", c, g]
-            if widened_by == "S":
-                copy(engine, grouped[:].rearrange("p (n i t) -> p n t i", i=4, t=4), wide[:].rearrange("p (t n i) -> p n t i", t=4, i=4))
-            else:
-                copy(engine, grouped[:].bitcast(F32).rearrange("p (n u) -> p n u", u=2), wide[:].bitcast(F32).rearrange("p (u n) -> p n u", u=2))
+            copy(engine, grouped[:].rearrange("p (n i t) -> p n t i", i=4, t=4), wide[:].rearrange("p (t n i) -> p n t i", t=4, i=4))
 
         def quantize_c3(c, g):
             quantize(c3_codes[c, g][:], c3_scales[c, g][:], live["c3g", c, g][:])
@@ -143,7 +140,7 @@ def tile_linear2mpo_pa_kernel(tc, t1, core2, core3_bytes, core3_scale, out):
 
         def empty1(io, r, g, engine):
             if ("t2g", io, r) not in live:
-                live["t2g", io, r] = work.tile([128, 2, 128, 4], BF16, name="t2_grouped", align_bytes=64, bufs=4)
+                live["t2g", io, r] = work.tile([128, 2, 128, 4], BF16, name="t2_grouped", align_bytes=64, bufs=6)
             copy(engine, live["t2g", io, r][:, g], live["b1", io, r, g][:].rearrange("p (t n) -> p n t", t=4))
 
         def quantize_t2(io, r):
@@ -178,18 +175,28 @@ def tile_linear2mpo_pa_kernel(tc, t1, core2, core3_bytes, core3_scale, out):
                 shape = [128, 1, 1024]
                 spot = (0, slice(h * 512, (h + 1) * 512))
                 target = [out_v[s, io // 2, j, io % 2][:, r : r + 1, :] for s in range(4)]
+            elif form == "two":
+                key = (io, c, r // 2, form)
+                shape = [128, 2, 512]
+                spot = (r % 2, slice(0, 512))
+                target = [out_v[s, io // 2, j, io % 2][:, 2 * (r // 2) : 2 * (r // 2) + 2, h * 512 : (h + 1) * 512] for s in range(4)]
+            elif form == "one":
+                key = (io, c, r, form)
+                shape = [128, 1, 512]
+                spot = (0, slice(0, 512))
+                target = [out_v[s, io // 2, j, io % 2][:, r : r + 1, h * 512 : (h + 1) * 512] for s in range(4)]
             else:
                 key = (io, c, form)
                 shape = [128, 4, 512]
                 spot = (r, slice(0, 512))
                 target = [out_v[s, io // 2, j, io % 2][:, :, h * 512 : (h + 1) * 512] for s in range(4)]
             if ("st",) + key not in live:
-                live[("st",) + key] = stage.tile(shape, F32, name="result", bufs=8)
+                live[("st",) + key] = stage.tile(shape, F32, name="result", bufs=14)
                 live[("n",) + key] = []
             result = live[("st",) + key]
             copy(engine, result[:, spot[0], spot[1]], live["b2", io, c, r][:])
             live[("n",) + key].append(c)
-            if len(live[("n",) + key]) == (2 if form == "half" else 4):
+            if len(live[("n",) + key]) == {"half": 2, "two": 2, "one": 1}.get(form, 4):
                 for s in range(4):
                     nc.sync.dma_start(out=target[s], in_=result[s:128:4])
 
@@ -199,23 +206,33 @@ def tile_linear2mpo_pa_kernel(tc, t1, core2, core3_bytes, core3_scale, out):
             for job in jobs:
                 job[0](*job[1:])
 
-        def one_round(products, tiles, steps, vector1=(), vector2=()):
-            n = len(products)
-            for k in range(n):
+        def one_round(products, tiles, vector):
+            mine = [job[1:-1] for job in vector if job[0] is empty1 or job[0] is empty2]
+            for k in range(len(products)):
+                for io, r in [tile for tile in tiles[k : k + 1] if tile]:
+                    for g in range(2):
+                        step1(io, r, g)
+                        if (io, r, g, 1) not in [m + (1,) for m in mine1(vector)]:
+                            empty1(io, r, g, "S")
                 step2(*products[k])
-                for tile in waiting:
-                    quantize_t2(*tile)
-                waiting.clear()
-                run(steps[len(steps) * k // n : len(steps) * (k + 1) // n])
-                empty2(*products[k], "V" if k in vector2 else "S")
-                for io, r in tiles[k :: n] if len(tiles) != 2 else tiles[k // 2 : k // 2 + 1 - k % 2]:
-                    step1(io, r, 0)
-                    empty1(io, r, 0, "S")
-                    step1(io, r, 1)
-                    empty1(io, r, 1, "V" if r in vector1 else "S")
-                    waiting.append((io, r))
+                if products[k] not in mine2(vector):
+                    empty2(*products[k], "S")
+            run(vector)
 
-        waiting = []
+        def mine1(vector):
+            return [job[1:-1] for job in vector if job[0] is empty1]
+
+        def mine2(vector):
+            return [job[1:-1] for job in vector if job[0] is empty2]
+
+        def E1(io, r, g=1):
+            return (empty1, io, r, g, "V")
+
+        def E2(io, c, r):
+            return (empty2, io, c, r, "V")
+
+        def QT(io, r):
+            return (quantize_t2, io, r)
 
         def W(c, g, e="V"):
             return (widen_all, c, g, e)
@@ -242,7 +259,7 @@ def tile_linear2mpo_pa_kernel(tc, t1, core2, core3_bytes, core3_scale, out):
             return [(io, c, r) for c in range(4)]
 
         def store_form(io, c, r):
-            return ("half" if (io, r) >= (3, 2) else "row") if io >= 2 else ("pair" if c < 2 else "col")
+            return "one" if (io, r, c // 2) == (3, 3, 1) else ("half" if c < 2 or (io, r) >= (2, 2) else "two")
 
         with tc.manual_schedule():
             nc.scalar.dma_start(out=scale[:], in_=core3_scale.rearrange("(g p t) a b c -> p g (t a b c)", g=2, t=4))
@@ -263,45 +280,52 @@ def tile_linear2mpo_pa_kernel(tc, t1, core2, core3_bytes, core3_scale, out):
             widen_all(0, 0, "V")
             widen_all(1, 0, "S")
             group_c2(0, 0, "V")
+            group_c3(1, 0, "S")
+            group_c3(0, 0, "V")
             turn_t1(0, "S")
-            group_c3(0, 0, "S")
-            quantize_c2(0, 0)
-            quantize_t1(0)
             group_c2(0, 1, "V")
-            for r in range(2):
-                step1(0, r, 0)
-                empty1(0, r, 0, "S")
-            widen_all(0, 1, "V")
+            quantize_c2(0, 0)
             widen_all(1, 1, "S")
+            widen_all(0, 1, "V")
             turn_t1(1, "S")
             quantize_c2(0, 1)
-            group_c3(0, 1, "V")
-            for r in range(2):
-                step1(0, r, 1)
-                empty1(0, r, 1, "S")
-            quantize_c3(0, 0)
-            quantize_c3(0, 1)
+            quantize_t1(0)
+            group_c2(1, 0, "V")
             quantize_t1(1)
-            group_c3(1, 0, "V")
-            quantize_t2(0, 0)
-            quantize_t2(0, 1)
+            group_c2(1, 1, "S")
+            group_c3(0, 1, "V")
+            quantize_c2(1, 0)
             group_c3(1, 1, "V")
+            quantize_c3(0, 0)
+            for r in range(4):
+                for g in range(2):
+                    step1(0, r, g)
+                    empty1(0, r, g, "S")
+            quantize_c2(1, 1)
+            quantize_c3(0, 1)
+            quantize_t2(0, 0)
             quantize_c3(1, 0)
+            quantize_t2(0, 1)
             quantize_c3(1, 1)
+            quantize_t2(0, 2)
+            quantize_t2(0, 3)
 
-            one_round([(0,0,0),(0,0,1),(0,1,0),(0,1,1)], [(0, 2), (0, 3)], [I2(1, 0), I2(1, 1), Q2(1, 0), Q2(1, 1)])
-            one_round(pair(0, 0, 1), [(1, 0), (1, 1)], [W(2, 0), W(2, 1)])
-            one_round(pair(1, 0, 0), [(1, 2), (1, 3)], [I3(2, 0), I3(2, 1), Q3(2, 0), Q3(2,1)])
-            one_round(pair(1, 0, 1), [], [W(3, 0), W(3, 1), I3(3, 0)])
-            one_round(col(0, 2), [], [I3(3, 1), Q3(3, 0), Q3(3, 1)])
-            one_round(col(1, 2), [], [I2(2, 0), I2(2, 1)])
-            one_round(col(0, 3), [], [Q2(2, 0), Q2(2, 1)])
-            one_round(col(1, 3), [(2, 0), (2, 1)], [], (0, 1))
-            one_round(row(2, 0), [(2, 2)], [I2(3, 0)], (2,))
-            one_round(row(2, 1), [(2, 3)], [I2(3, 1)], (3,))
-            one_round(row(2, 2), [], [Q2(3, 0), Q2(3, 1)], (), (2,))
-            one_round(row(2, 3), [(3, 0), (3, 1)], [], (0, 1))
-            one_round(row(3, 0), [(3, 2)], [], (2,), (2,))
-            one_round(row(3, 1), [(3, 3)], [], (3,), (2,))
-            one_round(row(3, 2), [], [], (), (1, 3))
-            one_round(row(3, 3), [], [], (), (1, 3))
+            one_round(pair(0, 0, 0)[:2], [(1, 0)], [W(2, 0), QT(1, 0)])
+            one_round(pair(0, 0, 0)[2:], [(1, 1)], [W(2, 1), QT(1, 1)])
+            one_round(pair(0, 0, 1)[:2], [(1, 2)], [I3(2, 0), QT(1, 2)])
+            one_round(pair(0, 0, 1)[2:], [(1, 3)], [I3(2, 1), QT(1, 3)])
+            one_round(pair(1, 0, 0), [], [Q3(2, 0), Q3(2, 1), I2(2, 0)])
+            one_round(pair(1, 0, 1), [], [I2(2, 1), Q2(2, 0), Q2(2, 1)])
+            one_round(col(0, 2), [None, None, (2, 0)], [W(3, 0), QT(2, 0), W(3, 1)])
+            one_round(col(1, 2), [(2, 1), None, (2, 2)], [E1(2, 1), I3(3, 0), QT(2, 1), E1(2, 2), I3(3, 1), QT(2, 2)])
+            one_round(row(2, 0)[:3], [(2, 3)], [E1(2, 3), Q3(3, 0), QT(2, 3), Q3(3, 1)])
+            one_round(row(2, 1)[:3], [], [I2(3, 0)])
+            one_round(row(2, 2), [], [I2(3, 1), Q2(3, 0)])
+            one_round(row(2, 3), [], [Q2(3, 1), E2(2, 2, 3)])
+            one_round([(2, 3, 0), (2, 3, 1)], [], [E2(2, 3, 1)])
+            one_round(col(0, 3), [(3, 0)], [E1(3, 0), E2(0, 3, 1), QT(3, 0)])
+            one_round(col(1, 3), [], [E2(1, 3, 1), E2(1, 3, 3)])
+            one_round(row(3, 0), [(3, 1)], [E1(3, 1), QT(3, 1), E2(3, 2, 0)])
+            one_round(row(3, 1), [(3, 2)], [E1(3, 2), QT(3, 2), E2(3, 2, 1)])
+            one_round(row(3, 2), [(3, 3)], [E1(3, 3), QT(3, 3), E2(3, 2, 2)])
+            one_round(row(3, 3), [], [E2(3, 1, 3), E2(3, 3, 3)])

@@ -76,11 +76,13 @@ def tile_linear2mpo_pa_kernel(tc, t1, core2, core3_bytes, core3_scale, out):
                 c2_raw[io, g] = raw[:, :, g * 512 : (g + 1) * 512]
             nc.sync.dma_start(out=raw[:], in_=core2_v[:, :, io, :])
 
-        def load_c3(j, g):
-            raw = keep.tile([128, 4, 1024], U8, name="c3_raw_%d_%d" % (j, g))
-            for h in range(2):
-                c3_raw[2 * j + h, g] = raw[:, :, h * 512 : (h + 1) * 512]
-            nc.sync.dma_start(out=raw[:], in_=core3_v[g][:, :, j * 1024 : (j + 1) * 1024])
+        def load_c3(j, g, first=0, last=4):
+            if first == 0:
+                raw = keep.tile([128, 4, 1024], U8, name="c3_raw_%d_%d" % (j, g))
+                live["c3r", j, g] = raw
+                for h in range(2):
+                    c3_raw[2 * j + h, g] = raw[:, :, h * 512 : (h + 1) * 512]
+            nc.sync.dma_start(out=live["c3r", j, g][:, first:last, :], in_=core3_v[g][:, first:last, j * 1024 : (j + 1) * 1024])
 
         def quantize(codes, scales, grouped):
             nc.vector.quantize_mx(out=codes.bitcast(FP8X4), scales=scales, in_=grouped)
@@ -107,10 +109,11 @@ def tile_linear2mpo_pa_kernel(tc, t1, core2, core3_bytes, core3_scale, out):
         def quantize_c2(io, g):
             quantize(c2_codes[io, g][:], c2_scales[io, g][:], live["c2g", io, g][:])
 
-        def widen_all(c, g, engine):
-            wide = work.tile([128, 2048], BF16, name="c3_wide", align_bytes=64, bufs=4)
-            live["c3w", c, g] = (wide, engine)
-            for t in range(4):
+        def widen_all(c, g, engine, first=0, last=4):
+            if first == 0:
+                live["c3w", c, g] = (work.tile([128, 2048], BF16, name="c3_wide", align_bytes=64, bufs=4), engine)
+            wide = live["c3w", c, g][0]
+            for t in range(first, last):
                 src = c3_raw[c, g][:, t, :].bitcast(FP8)
                 if engine == "S":
                     nc.scalar.activation(out=wide[:, t * 512 : (t + 1) * 512], in_=src, func=COPY, scale=scale[:, g, t : t + 1])
@@ -259,12 +262,13 @@ def tile_linear2mpo_pa_kernel(tc, t1, core2, core3_bytes, core3_scale, out):
             return [(io, c, r) for c in range(4)]
 
         def store_form(io, c, r):
-            return "one" if (io, r, c // 2) == (3, 3, 1) else ("half" if c < 2 or (io, r) >= (2, 2) else "two")
+            return "half" if c < 2 or io >= 2 else "two"
 
         with tc.manual_schedule():
             nc.scalar.dma_start(out=scale[:], in_=core3_scale.rearrange("(g p t) a b c -> p g (t a b c)", g=2, t=4))
-            load_c3(0, 0)
+            load_c3(0, 0, 0, 2)
             load_c2_half(0, 0)
+            load_c3(0, 0, 2, 4)
             load_t1(0)
             load_c2_half(0, 1)
             load_c3(0, 1)
@@ -277,55 +281,57 @@ def tile_linear2mpo_pa_kernel(tc, t1, core2, core3_bytes, core3_scale, out):
             make_identity(nc, ident[:])
             nc.vector.tensor_copy(out=perm[:].rearrange("p (o i) -> p i o", i=4), in_=ident[:].rearrange("p (i o) -> p i o", i=4))
 
-            widen_all(0, 0, "V")
+            widen_all(0, 0, "V", 0, 2)
             widen_all(1, 0, "S")
             group_c2(0, 0, "V")
-            group_c3(1, 0, "S")
-            group_c3(0, 0, "V")
+            widen_all(0, 0, "V", 2, 4)
             turn_t1(0, "S")
-            group_c2(0, 1, "V")
+            group_c3(1, 0, "S")
             quantize_c2(0, 0)
+            group_c3(0, 0, "V")
+            group_c2(0, 1, "V")
+            quantize_t1(0)
             widen_all(1, 1, "S")
             widen_all(0, 1, "V")
             turn_t1(1, "S")
             quantize_c2(0, 1)
-            quantize_t1(0)
+            group_c2(1, 1, "S")
             group_c2(1, 0, "V")
             quantize_t1(1)
-            group_c2(1, 1, "S")
             group_c3(0, 1, "V")
-            quantize_c2(1, 0)
-            group_c3(1, 1, "V")
-            quantize_c3(0, 0)
             for r in range(4):
                 for g in range(2):
                     step1(0, r, g)
                     empty1(0, r, g, "S")
+            quantize_c2(1, 0)
             quantize_c2(1, 1)
+            group_c3(1, 1, "V")
+            quantize_c3(0, 0)
             quantize_c3(0, 1)
             quantize_t2(0, 0)
             quantize_c3(1, 0)
-            quantize_t2(0, 1)
             quantize_c3(1, 1)
+            quantize_t2(0, 1)
+            for r in range(2):
+                for g in range(2):
+                    step1(1, r, g)
+                    empty1(1, r, g, "S")
             quantize_t2(0, 2)
             quantize_t2(0, 3)
 
-            one_round(pair(0, 0, 0)[:2], [(1, 0)], [W(2, 0), QT(1, 0)])
-            one_round(pair(0, 0, 0)[2:], [(1, 1)], [W(2, 1), QT(1, 1)])
-            one_round(pair(0, 0, 1)[:2], [(1, 2)], [I3(2, 0), QT(1, 2)])
-            one_round(pair(0, 0, 1)[2:], [(1, 3)], [I3(2, 1), QT(1, 3)])
+            one_round(pair(0, 0, 0), [None, None, (1, 2), (1, 3)], [W(2, 0), QT(1, 0), QT(1, 1), W(2, 1)])
+            one_round(pair(0, 0, 1), [], [I3(2, 0), QT(1, 2), I3(2, 1), QT(1, 3)])
             one_round(pair(1, 0, 0), [], [Q3(2, 0), Q3(2, 1), I2(2, 0)])
             one_round(pair(1, 0, 1), [], [I2(2, 1), Q2(2, 0), Q2(2, 1)])
-            one_round(col(0, 2), [None, None, (2, 0)], [W(3, 0), QT(2, 0), W(3, 1)])
-            one_round(col(1, 2), [(2, 1), None, (2, 2)], [E1(2, 1), I3(3, 0), QT(2, 1), E1(2, 2), I3(3, 1), QT(2, 2)])
-            one_round(row(2, 0)[:3], [(2, 3)], [E1(2, 3), Q3(3, 0), QT(2, 3), Q3(3, 1)])
-            one_round(row(2, 1)[:3], [], [I2(3, 0)])
-            one_round(row(2, 2), [], [I2(3, 1), Q2(3, 0)])
-            one_round(row(2, 3), [], [Q2(3, 1), E2(2, 2, 3)])
-            one_round([(2, 3, 0), (2, 3, 1)], [], [E2(2, 3, 1)])
-            one_round(col(0, 3), [(3, 0)], [E1(3, 0), E2(0, 3, 1), QT(3, 0)])
-            one_round(col(1, 3), [], [E2(1, 3, 1), E2(1, 3, 3)])
-            one_round(row(3, 0), [(3, 1)], [E1(3, 1), QT(3, 1), E2(3, 2, 0)])
-            one_round(row(3, 1), [(3, 2)], [E1(3, 2), QT(3, 2), E2(3, 2, 1)])
-            one_round(row(3, 2), [(3, 3)], [E1(3, 3), QT(3, 3), E2(3, 2, 2)])
+            one_round(col(0, 2), [None, None, None, (2, 0)], [W(3, 0), W(3, 1), QT(2, 0)])
+            one_round(col(1, 2), [None, (2, 1), None, (2, 2)], [I3(3, 0), QT(2, 1), I3(3, 1), QT(2, 2)])
+            one_round(pair(2, 0, 0), [None, (2, 3)], [Q3(3, 0), Q3(3, 1), QT(2, 3)])
+            one_round(pair(2, 0, 1), [], [I2(3, 0), E2(2, 1, 3)])
+            one_round(pair(2, 1, 0), [], [I2(3, 1), E2(2, 3, 1), Q2(3, 0)])
+            one_round(pair(2, 1, 1), [], [Q2(3, 1), E2(2, 3, 2), E2(2, 3, 3)])
+            one_round(col(0, 3), [None, (3, 0)], [E2(0, 3, 0), E1(3, 0), E2(0, 3, 2), QT(3, 0)])
+            one_round(col(1, 3), [None, (3, 1)], [E2(1, 3, 0), E1(3, 1), E2(1, 3, 2), QT(3, 1)])
+            one_round(row(3, 0), [None, (3, 2)], [E2(3, 0, 0), E1(3, 2), E2(3, 2, 0), QT(3, 2)])
+            one_round(row(3, 1), [None, (3, 3)], [E2(3, 0, 1), E1(3, 3), E2(3, 2, 1), QT(3, 3)])
+            one_round(row(3, 2), [], [E2(3, 1, 2), E2(3, 3, 2)])
             one_round(row(3, 3), [], [E2(3, 1, 3), E2(3, 3, 3)])

@@ -150,15 +150,16 @@ def tile_linear2mpo_pa_kernel(tc, t1, core2, core3_bytes, core3_scale, out):
             cols = slice(r * 256, (r + 1) * 256)
             quantize(t2_codes[io][:, cols], t2_scales[io][:, cols], live["t2g", io, r][:].rearrange("p g n t -> p (g n t)"))
 
-        def step2(io, c, r):
-            bank = next_bank()
+        def step2(io, chunks, r):
+            for c in chunks:
+                live["b2", io, c, r] = next_bank()
             for g in range(2):
                 rows = slice(r * 256 + g * 128, r * 256 + (g + 1) * 128)
-                nc.tensor.matmul_mx(out=bank[:],
-                                    lhsT=t2_codes[io][:, rows].bitcast(FP8X4), lhsT_scale=t2_scales[io][:, rows],
-                                    rhs=c3_codes[c, g][:].bitcast(FP8X4), rhs_scale=c3_scales[c, g][:],
-                                    start=(g == 0), stop=(g == 1))
-            live["b2", io, c, r] = bank
+                for c in chunks:
+                    nc.tensor.matmul_mx(out=live["b2", io, c, r][:],
+                                        lhsT=t2_codes[io][:, rows].bitcast(FP8X4), lhsT_scale=t2_scales[io][:, rows],
+                                        rhs=c3_codes[c, g][:].bitcast(FP8X4), rhs_scale=c3_scales[c, g][:],
+                                        start=(g == 0), stop=(g == 1))
 
         def empty2(io, c, r, engine):
             j, h = c // 2, c % 2
@@ -217,9 +218,11 @@ def tile_linear2mpo_pa_kernel(tc, t1, core2, core3_bytes, core3_scale, out):
                         step1(io, r, g)
                         if (io, r, g, 1) not in [m + (1,) for m in mine1(vector)]:
                             empty1(io, r, g, "S")
-                step2(*products[k])
-                if products[k] not in mine2(vector):
-                    empty2(*products[k], "S")
+                io, chunks, r = products[k]
+                step2(io, chunks, r)
+                for c in chunks:
+                    if (io, c, r) not in mine2(vector):
+                        empty2(io, c, r, "S")
             run(vector)
 
         def mine1(vector):
@@ -253,13 +256,13 @@ def tile_linear2mpo_pa_kernel(tc, t1, core2, core3_bytes, core3_scale, out):
             return (quantize_c2, io, g)
 
         def col(io, c):
-            return [(io, c, r) for r in range(4)]
+            return [(io, [c], r) for r in range(4)]
 
         def pair(io, j, p):
-            return [(io, 2 * j + h, 2 * p + e) for e in range(2) for h in range(2)]
+            return [(io, [2 * j, 2 * j + 1], 2 * p + e) for e in range(2)]
 
         def row(io, r):
-            return [(io, c, r) for c in range(4)]
+            return [(io, [0, 1], r), (io, [2, 3], r)]
 
         def store_form(io, c, r):
             return "half" if c < 2 or io >= 2 else "two"
@@ -319,13 +322,13 @@ def tile_linear2mpo_pa_kernel(tc, t1, core2, core3_bytes, core3_scale, out):
             quantize_t2(0, 2)
             quantize_t2(0, 3)
 
-            one_round(pair(0, 0, 0), [None, None, (1, 2), (1, 3)], [W(2, 0), QT(1, 0), QT(1, 1), W(2, 1)])
-            one_round(pair(0, 0, 1), [], [I3(2, 0), QT(1, 2), I3(2, 1), QT(1, 3)])
+            one_round(pair(0, 0, 0), [None, (1, 2)], [W(2, 0), QT(1, 0), QT(1, 1), W(2, 1)])
+            one_round(pair(0, 0, 1), [(1, 3)], [I3(2, 0), QT(1, 2), I3(2, 1), QT(1, 3)])
             one_round(pair(1, 0, 0), [], [Q3(2, 0), Q3(2, 1), I2(2, 0)])
             one_round(pair(1, 0, 1), [], [I2(2, 1), Q2(2, 0), Q2(2, 1)])
-            one_round(col(0, 2), [None, None, None, (2, 0)], [W(3, 0), W(3, 1), QT(2, 0)])
-            one_round(col(1, 2), [None, (2, 1), None, (2, 2)], [I3(3, 0), QT(2, 1), I3(3, 1), QT(2, 2)])
-            one_round(pair(2, 0, 0), [None, (2, 3)], [Q3(3, 0), Q3(3, 1), QT(2, 3)])
+            one_round(col(0, 2), [None, None, None, (2, 0)], [W(3, 0), E1(2, 0), W(3, 1), QT(2, 0)])
+            one_round(col(1, 2), [None, (2, 1), None, (2, 2)], [E1(2, 1), I3(3, 0), QT(2, 1), E1(2, 2), I3(3, 1), QT(2, 2)])
+            one_round(pair(2, 0, 0), [(2, 3)], [E1(2, 3), Q3(3, 0), QT(2, 3), Q3(3, 1)])
             one_round(pair(2, 0, 1), [], [I2(3, 0), E2(2, 1, 3)])
             one_round(pair(2, 1, 0), [], [I2(3, 1), E2(2, 3, 1), Q2(3, 0)])
             one_round(pair(2, 1, 1), [], [Q2(3, 1), E2(2, 3, 2), E2(2, 3, 3)])

@@ -14,21 +14,23 @@ COPY = mybir.ActivationFunctionType.Copy
 
 FLOPS = 2 * 512 * 512 * 4096 + 2 * 2048 * 1024 * 2048
 
-VSHARE = [0, 3, 3, 3, 3, 3, 2]
+WHOLE_SLOTS = 6
+HALF_SLOTS = 6
 
 
 def tile_linear2mpo_pa_kernel(tc, t1, core2, core3_bytes, core3_scale, out):
     nc = tc.nc
+    vector, scalar = nc.vector.tensor_copy, nc.scalar.copy
     with ExitStack() as ctx:
         keep = ctx.enter_context(tc.tile_pool(name="keep", bufs=1))
-        work = ctx.enter_context(tc.tile_pool(name="work", bufs=3))
-        stage = ctx.enter_context(tc.tile_pool(name="stage", bufs=16))
+        work = ctx.enter_context(tc.tile_pool(name="work", bufs=1))
+        stage = ctx.enter_context(tc.tile_pool(name="stage", bufs=1))
         psum = ctx.enter_context(tc.psum_pool(name="psum", bufs=1))
 
         t1_rows = t1.rearrange("i o k -> (i o) k")
         core2_v = core2.rearrange("(p j) i o q -> p j (i o) q", j=4)
         core3_v = core3_bytes.rearrange("(g p t) i o q -> g p t (i o q)", g=2, t=4)
-        out_v = out.rearrange("(R s i j) (O o h) q -> s i j o O R (h q)", s=4, i=2, j=2, o=2, h=2)
+        out_v = out.rearrange("(r s i j) (O o h) q -> s i o O r j (h q)", s=4, i=2, j=2, o=2, h=2)
 
         ident = keep.tile([128, 128], F32, name="ident")
         perm = keep.tile([128, 128], F32, name="perm")
@@ -37,8 +39,6 @@ def tile_linear2mpo_pa_kernel(tc, t1, core2, core3_bytes, core3_scale, out):
         t1_grouped = keep.tile([128, 512, 4], BF16, name="t1_grouped", align_bytes=64)
         t1_codes = keep.tile([128, 512], U32, name="t1_codes", align_bytes=64)
         t1_scales = keep.tile([128, 512], U8, name="t1_scales", align_bytes=64)
-        banks = [psum.tile([128, 512], F32, name="bank_%d" % b) for b in range(8)]
-        c2_raw, c3_raw = {}, {}
         c2_codes, c2_scales, t2_codes, t2_scales, c3_codes, c3_scales = {}, {}, {}, {}, {}, {}
         for a in range(4):
             t2_codes[a] = keep.tile([128, 1024], U32, name="t2_codes_%d" % a, align_bytes=64)
@@ -48,90 +48,75 @@ def tile_linear2mpo_pa_kernel(tc, t1, core2, core3_bytes, core3_scale, out):
                 c2_scales[a, g] = keep.tile([128, 512], U8, name="c2_scales_%d_%d" % (a, g), align_bytes=64)
                 c3_codes[a, g] = keep.tile([128, 512], U32, name="c3_codes_%d_%d" % (a, g), align_bytes=64)
                 c3_scales[a, g] = keep.tile([128, 512], U8, name="c3_scales_%d_%d" % (a, g), align_bytes=64)
+        c3_bytes = {(j, g): keep.tile([128, 4, 1024], U8, name="c3_bytes_%d_%d" % (j, g)) for j in range(2) for g in range(2)}
 
-        live = {}
-        used = []
+        free_banks = [psum.tile([128, 512], F32, name="bank_%d" % b) for b in range(8)]
+        c2_raw, c2_grouped, c3_wide, c3_grouped, t2_grouped, full_banks, results = {}, {}, {}, {}, {}, {}, {}
 
-        def next_bank():
-            used.append(len(used))
-            return banks[used[-1] % 8]
-
-        def copy(engine, dst, src):
-            if engine == "S":
-                nc.scalar.copy(dst, src)
-            else:
-                nc.vector.tensor_copy(out=dst, in_=src)
-
-        def load_t1(a):
-            nc.sync.dma_start(out=t1_raw[a][:], in_=t1_rows[a * 256 : (a + 1) * 256, :].rearrange("(r p) k -> p r k", r=2))
-
-        def load_c2_half(io, g):
-            raw = keep.tile([128, 4, 512], BF16, name="c2_raw_%d_%d" % (io, g))
-            c2_raw[io, g] = raw[:]
-            nc.sync.dma_start(out=raw[:], in_=core2_v[:, :, io, g * 512 : (g + 1) * 512])
-
-        def load_c2(io):
-            raw = keep.tile([128, 4, 1024], BF16, name="c2_raw_%d" % io)
-            for g in range(2):
-                c2_raw[io, g] = raw[:, :, g * 512 : (g + 1) * 512]
-            nc.sync.dma_start(out=raw[:], in_=core2_v[:, :, io, :])
-
-        def load_c3(j, g, first=0, last=4):
-            if first == 0:
-                raw = keep.tile([128, 4, 1024], U8, name="c3_raw_%d_%d" % (j, g))
-                live["c3r", j, g] = raw
-                for h in range(2):
-                    c3_raw[2 * j + h, g] = raw[:, :, h * 512 : (h + 1) * 512]
-            nc.sync.dma_start(out=live["c3r", j, g][:, first:last, :], in_=core3_v[g][:, first:last, j * 1024 : (j + 1) * 1024])
+        def take_bank(key):
+            full_banks[key] = free_banks[0]
+            free_banks.remove(full_banks[key])
+            return full_banks[key]
 
         def quantize(codes, scales, grouped):
             nc.vector.quantize_mx(out=codes.bitcast(FP8X4), scales=scales, in_=grouped)
 
-        def turn_t1(a, engine):
-            bank = next_bank()
-            xt = bank[:].rearrange("p (s u n) -> p s u n", s=2, u=2)
-            for s in range(2):
-                words = t1_raw[a][:, s, :].bitcast(F32)
+        def load_t1(a):
+            nc.sync.dma_start(out=t1_raw[a][:], in_=t1_rows[a * 256 : (a + 1) * 256, :].rearrange("(r p) k -> p r k", r=2))
+
+        def load_c2_pass(io, g):
+            raw = stage.tile([128, 4, 512], BF16, name="half", bufs=HALF_SLOTS)
+            c2_raw[io, g] = raw[:]
+            nc.sync.dma_start(out=raw[:], in_=core2_v[:, :, io, g * 512 : (g + 1) * 512])
+
+        def load_c2(io, raw):
+            for g in range(2):
+                c2_raw[io, g] = raw[:, :, g * 512 : (g + 1) * 512]
+            nc.sync.dma_start(out=raw[:], in_=core2_v[:, :, io, :])
+
+        def load_c3(j, g, places=slice(0, 4)):
+            nc.sync.dma_start(out=c3_bytes[j, g][:, places, :], in_=core3_v[g][:, places, j * 1024 : (j + 1) * 1024])
+
+        def turn_t1(a):
+            bank = take_bank(("t1", a))
+            turned = bank[:].rearrange("p (e u n) -> p e u n", e=2, u=2)
+            for e in range(2):
+                words = t1_raw[a][:, e, :].bitcast(F32)
                 for u in range(2):
-                    nc.tensor.transpose(xt[:, s, u, :], words[:, u::2], perm[:])
-            dst = t1_grouped[:, a * 256 : (a + 1) * 256, :].rearrange("p n j -> p (n j)").bitcast(F32)
-            copy(engine, dst.rearrange("p (s n u) -> p s n u", s=2, u=2), xt.rearrange("p s u n -> p s n u"))
+                    nc.tensor.transpose(turned[:, e, u, :], words[:, u::2], perm[:])
+            dst = t1_grouped[:, a * 256 : (a + 1) * 256, :].rearrange("p n t -> p (n t)").bitcast(F32)
+            scalar(dst.rearrange("p (e n u) -> p e n u", e=2, u=2), turned.rearrange("p e u n -> p e n u"))
+            free_banks.append(bank)
 
         def quantize_t1(a):
             cols = slice(a * 256, (a + 1) * 256)
-            quantize(t1_codes[:, cols], t1_scales[:, cols], t1_grouped[:, cols, :].rearrange("p n j -> p (n j)"))
+            quantize(t1_codes[:, cols], t1_scales[:, cols], t1_grouped[:, cols, :].rearrange("p n t -> p (n t)"))
 
-        def group_c2(io, g, engine):
-            grouped = work.tile([128, 2048], BF16, name="c2_grouped", align_bytes=64)
-            live["c2g", io, g] = grouped
-            copy(engine, grouped[:].rearrange("p (t m j) -> p m j t", t=4, j=4), c2_raw[io, g].rearrange("p j (m t) -> p m j t", t=4))
+        def group_c2(io, g, copy=vector):
+            c2_grouped[io, g] = work.tile([128, 2048], BF16, name="c2_grouped", align_bytes=64, bufs=3)
+            copy(c2_grouped[io, g][:].rearrange("p (t m j) -> p m j t", t=4, j=4), c2_raw[io, g].rearrange("p j (m t) -> p m j t", t=4))
 
         def quantize_c2(io, g):
-            quantize(c2_codes[io, g][:], c2_scales[io, g][:], live["c2g", io, g][:])
+            quantize(c2_codes[io, g][:], c2_scales[io, g][:], c2_grouped[io, g][:])
 
-        def widen_all(c, g, engine, first=0, last=4):
-            if first == 0:
-                live["c3w", c, g] = (work.tile([128, 2048], BF16, name="c3_wide", align_bytes=64, bufs=4), engine)
-            wide = live["c3w", c, g][0]
-            for t in range(first, last):
-                src = c3_raw[c, g][:, t, :].bitcast(FP8)
-                if engine == "S":
-                    nc.scalar.activation(out=wide[:, t * 512 : (t + 1) * 512], in_=src, func=COPY, scale=scale[:, g, t : t + 1])
+        def widen_c3(c, g, on_scalar=False):
+            c3_wide[c, g] = work.tile([128, 4, 512], BF16, name="c3_wide", align_bytes=64, bufs=4)
+            for t in range(4):
+                src = c3_bytes[c // 2, g][:, t, (c % 2) * 512 : (c % 2 + 1) * 512].bitcast(FP8)
+                if on_scalar:
+                    nc.scalar.activation(out=c3_wide[c, g][:, t, :], in_=src, func=COPY, scale=scale[:, g, t : t + 1])
                 else:
-                    dst = wide[:, t * 512 : (t + 1) * 512]
-                    nc.vector.tensor_scalar(out=dst, in0=src, scalar1=scale[:, g, t : t + 1], scalar2=None, op0=MULT)
+                    nc.vector.tensor_scalar(out=c3_wide[c, g][:, t, :], in0=src, scalar1=scale[:, g, t : t + 1], scalar2=None, op0=MULT)
 
-        def group_c3(c, g, engine):
-            grouped = work.tile([128, 2048], BF16, name="c3_grouped", align_bytes=64, bufs=4)
-            live["c3g", c, g] = grouped
-            wide, widened_by = live["c3w", c, g]
-            copy(engine, grouped[:].rearrange("p (n i t) -> p n t i", i=4, t=4), wide[:].rearrange("p (t n i) -> p n t i", t=4, i=4))
+        def group_c3(c, g, copy=vector):
+            c3_grouped[c, g] = work.tile([128, 2048], BF16, name="c3_grouped", align_bytes=64, bufs=4)
+            copy(c3_grouped[c, g][:].rearrange("p (n i t) -> p n t i", i=4, t=4), c3_wide[c, g][:].rearrange("p t (n i) -> p n t i", i=4))
 
         def quantize_c3(c, g):
-            quantize(c3_codes[c, g][:], c3_scales[c, g][:], live["c3g", c, g][:])
+            quantize(c3_codes[c, g][:], c3_scales[c, g][:], c3_grouped[c, g][:])
 
         def step1(io, r, g):
-            bank = next_bank()
+            bank = take_bank(("step1", io, r, g))
             rows = slice(r * 128, (r + 1) * 128)
             for t in range(4):
                 cols = slice(t * 128, (t + 1) * 128)
@@ -139,202 +124,172 @@ def tile_linear2mpo_pa_kernel(tc, t1, core2, core3_bytes, core3_scale, out):
                                     lhsT=c2_codes[io, g][:, cols].bitcast(FP8X4), lhsT_scale=c2_scales[io, g][:, cols],
                                     rhs=t1_codes[:, rows].bitcast(FP8X4), rhs_scale=t1_scales[:, rows],
                                     start=True, stop=True)
-            live["b1", io, r, g] = bank
 
-        def empty1(io, r, g, engine):
-            if ("t2g", io, r) not in live:
-                live["t2g", io, r] = work.tile([128, 2, 128, 4], BF16, name="t2_grouped", align_bytes=64, bufs=6)
-            copy(engine, live["t2g", io, r][:, g], live["b1", io, r, g][:].rearrange("p (t n) -> p n t", t=4))
+        def empty1(io, r, g, copy):
+            if (io, r) not in t2_grouped:
+                t2_grouped[io, r] = work.tile([128, 2, 128, 4], BF16, name="t2_grouped", align_bytes=64, bufs=8)
+            bank = full_banks["step1", io, r, g]
+            copy(t2_grouped[io, r][:, g], bank[:].rearrange("p (t n) -> p n t", t=4))
+            free_banks.append(bank)
 
         def quantize_t2(io, r):
             cols = slice(r * 256, (r + 1) * 256)
-            quantize(t2_codes[io][:, cols], t2_scales[io][:, cols], live["t2g", io, r][:].rearrange("p g n t -> p (g n t)"))
+            quantize(t2_codes[io][:, cols], t2_scales[io][:, cols], t2_grouped[io, r][:].rearrange("p g n t -> p (g n t)"))
+
+        def make_tile(io, r):
+            step1(io, r, 0)
+            empty1(io, r, 0, scalar)
+            step1(io, r, 1)
 
         def step2(io, chunks, r):
-            for c in chunks:
-                live["b2", io, c, r] = next_bank()
+            banks = [take_bank(("step2", io, c, r)) for c in chunks]
             for g in range(2):
                 rows = slice(r * 256 + g * 128, r * 256 + (g + 1) * 128)
-                for c in chunks:
-                    nc.tensor.matmul_mx(out=live["b2", io, c, r][:],
+                for c, bank in zip(chunks, banks):
+                    nc.tensor.matmul_mx(out=bank[:],
                                         lhsT=t2_codes[io][:, rows].bitcast(FP8X4), lhsT_scale=t2_scales[io][:, rows],
                                         rhs=c3_codes[c, g][:].bitcast(FP8X4), rhs_scale=c3_scales[c, g][:],
                                         start=(g == 0), stop=(g == 1))
 
-        def empty2(io, c, r, engine):
-            j, h = c // 2, c % 2
-            form = store_form(io, c, r)
-            if form == "pair":
-                key = (io, j, r // 2, form)
-                shape = [128, 2, 1024]
-                spot = (r % 2, slice(h * 512, (h + 1) * 512))
-                target = [out_v[s, io // 2, j, io % 2][:, 2 * (r // 2) : 2 * (r // 2) + 2, :] for s in range(4)]
-            elif form == "row":
-                key = (io, r, form)
-                shape = [128, 2, 1024]
-                spot = (j, slice(h * 512, (h + 1) * 512))
-                target = [out_j[s, io // 2, io % 2, r] for s in range(4)]
-            elif form == "half":
-                key = (io, r, j, form)
-                shape = [128, 1, 1024]
-                spot = (0, slice(h * 512, (h + 1) * 512))
-                target = [out_v[s, io // 2, j, io % 2][:, r : r + 1, :] for s in range(4)]
-            elif form == "two":
-                key = (io, c, r // 2, form)
-                shape = [128, 2, 512]
-                spot = (r % 2, slice(0, 512))
-                target = [out_v[s, io // 2, j, io % 2][:, 2 * (r // 2) : 2 * (r // 2) + 2, h * 512 : (h + 1) * 512] for s in range(4)]
-            elif form == "one":
-                key = (io, c, r, form)
-                shape = [128, 1, 512]
-                spot = (0, slice(0, 512))
-                target = [out_v[s, io // 2, j, io % 2][:, r : r + 1, h * 512 : (h + 1) * 512] for s in range(4)]
-            else:
-                key = (io, c, form)
-                shape = [128, 4, 512]
-                spot = (r, slice(0, 512))
-                target = [out_v[s, io // 2, j, io % 2][:, :, h * 512 : (h + 1) * 512] for s in range(4)]
-            if ("st",) + key not in live:
-                live[("st",) + key] = stage.tile(shape, F32, name="result", bufs=14)
-                live[("n",) + key] = []
-            result = live[("st",) + key]
-            copy(engine, result[:, spot[0], spot[1]], live["b2", io, c, r][:])
-            live[("n",) + key].append(c)
-            if len(live[("n",) + key]) == {"half": 2, "two": 2, "one": 1}.get(form, 4):
+        def store_unit(io, c, r):
+            if io == 3 or (io == 0 and c < 2):
+                return (r, r + 1), (c - c % 2, c - c % 2 + 2)
+            if io == 2:
+                return (r, r + 1), (0, 4)
+            if c < 2:
+                return (r - r % 2, r - r % 2 + 2), (0, 2)
+            return (0, 4), (c, c + 1)
+
+        def empty2(io, c, r, copy):
+            (r0, r1), (c0, c1) = store_unit(io, c, r)
+            key = (io, r0, c0)
+            count = (r1 - r0) * (c1 - c0)
+            if key not in results:
+                if count == 4:
+                    tile = stage.tile([128, r1 - r0, (c1 - c0) * 512], F32, name="whole", bufs=WHOLE_SLOTS)
+                else:
+                    tile = stage.tile([128, r1 - r0, (c1 - c0) * 512], F32, name="half", bufs=HALF_SLOTS)
+                results[key] = (tile, [])
+            tile, done = results[key]
+            bank = full_banks["step2", io, c, r]
+            copy(tile[:, r - r0, (c - c0) * 512 : (c - c0 + 1) * 512], bank[:])
+            free_banks.append(bank)
+            done.append((c, r))
+            if len(done) == count:
                 for s in range(4):
-                    nc.sync.dma_start(out=target[s], in_=result[s:128:4])
+                    rows = out_v[s, io // 2, io % 2]
+                    if c1 - c0 == 4:
+                        nc.sync.dma_start(out=rows[:, r0], in_=tile[s:128:4, 0, :].rearrange("p (j x) -> p j x", j=2))
+                    else:
+                        cols = slice((c0 % 2) * 512, (c0 % 2 + c1 - c0) * 512)
+                        nc.sync.dma_start(out=rows[:, r0:r1, c0 // 2, cols], in_=tile[s:128:4])
 
-        out_j = out.rearrange("(R s i j) (O o h) q -> s i o R O j (h q)", s=4, i=2, j=2, o=2, h=2)
-
-        def run(jobs):
-            for job in jobs:
-                job[0](*job[1:])
-
-        def one_round(products, tiles, vector):
-            mine = [job[1:-1] for job in vector if job[0] is empty1 or job[0] is empty2]
-            for k in range(len(products)):
-                for io, r in [tile for tile in tiles[k : k + 1] if tile]:
-                    for g in range(2):
-                        step1(io, r, g)
-                        if (io, r, g, 1) not in [m + (1,) for m in mine1(vector)]:
-                            empty1(io, r, g, "S")
-                io, chunks, r = products[k]
-                step2(io, chunks, r)
-                for c in chunks:
-                    if (io, c, r) not in mine2(vector):
-                        empty2(io, c, r, "S")
-            run(vector)
-
-        def mine1(vector):
-            return [job[1:-1] for job in vector if job[0] is empty1]
-
-        def mine2(vector):
-            return [job[1:-1] for job in vector if job[0] is empty2]
-
-        def E1(io, r, g=1):
-            return (empty1, io, r, g, "V")
-
-        def E2(io, c, r):
-            return (empty2, io, c, r, "V")
-
-        def QT(io, r):
-            return (quantize_t2, io, r)
-
-        def W(c, g, e="V"):
-            return (widen_all, c, g, e)
-
-        def I3(c, g, e="V"):
-            return (group_c3, c, g, e)
-
-        def Q3(c, g):
-            return (quantize_c3, c, g)
-
-        def I2(io, g, e="V"):
-            return (group_c2, io, g, e)
-
-        def Q2(io, g):
-            return (quantize_c2, io, g)
-
-        def col(io, c):
-            return [(io, [c], r) for r in range(4)]
-
-        def pair(io, j, p):
-            return [(io, [2 * j, 2 * j + 1], 2 * p + e) for e in range(2)]
-
-        def row(io, r):
-            return [(io, [0, 1], r), (io, [2, 3], r)]
-
-        def store_form(io, c, r):
-            return "half" if c < 2 or io >= 2 else "two"
+        def products(io, chunks, r):
+            step2(io, chunks, r)
+            for c in chunks:
+                empty2(io, c, r, scalar)
 
         with tc.manual_schedule():
             nc.scalar.dma_start(out=scale[:], in_=core3_scale.rearrange("(g p t) a b c -> p g (t a b c)", g=2, t=4))
-            load_c3(0, 0, 0, 2)
-            load_c2_half(0, 0)
-            load_c3(0, 0, 2, 4)
+            load_c3(0, 0, slice(0, 2))
+            load_c3(0, 0, slice(2, 4))
+            load_c2_pass(0, 0)
             load_t1(0)
-            load_c2_half(0, 1)
+            load_c2_pass(0, 1)
             load_c3(0, 1)
             load_t1(1)
-            load_c2(1)
+            load_c2(1, stage.tile([128, 4, 1024], BF16, name="whole", bufs=WHOLE_SLOTS))
             load_c3(1, 0)
             load_c3(1, 1)
-            load_c2(2)
-            load_c2(3)
+            load_c2(2, keep.tile([128, 4, 1024], BF16, name="c2_raw_2"))
+            load_c2(3, keep.tile([128, 4, 1024], BF16, name="c2_raw_3"))
             make_identity(nc, ident[:])
-            nc.vector.tensor_copy(out=perm[:].rearrange("p (o i) -> p i o", i=4), in_=ident[:].rearrange("p (i o) -> p i o", i=4))
+            vector(perm[:].rearrange("p (o s) -> p s o", s=4), ident[:].rearrange("p (s o) -> p s o", s=4))
 
-            widen_all(0, 0, "V", 0, 2)
-            widen_all(1, 0, "S")
-            group_c2(0, 0, "V")
-            widen_all(0, 0, "V", 2, 4)
-            turn_t1(0, "S")
-            group_c3(1, 0, "S")
+            widen_c3(0, 0)
+            widen_c3(1, 0, on_scalar=True)
+            group_c2(0, 0)
+            turn_t1(0)
+            group_c3(1, 0, scalar)
             quantize_c2(0, 0)
-            group_c3(0, 0, "V")
-            group_c2(0, 1, "V")
+            group_c3(0, 0)
+            group_c2(0, 1)
             quantize_t1(0)
-            widen_all(1, 1, "S")
-            widen_all(0, 1, "V")
-            turn_t1(1, "S")
+            widen_c3(1, 1, on_scalar=True)
+            widen_c3(0, 1)
+            turn_t1(1)
             quantize_c2(0, 1)
-            group_c2(1, 1, "S")
-            group_c2(1, 0, "V")
+            group_c2(1, 1, scalar)
+            group_c2(1, 0)
             quantize_t1(1)
-            group_c3(0, 1, "V")
-            for r in range(4):
-                for g in range(2):
-                    step1(0, r, g)
-                    empty1(0, r, g, "S")
+            group_c3(0, 1)
             quantize_c2(1, 0)
             quantize_c2(1, 1)
-            group_c3(1, 1, "V")
+            for io in range(2):
+                for r in range(4):
+                    make_tile(io, r)
+                    empty1(io, r, 1, scalar)
+            group_c3(1, 1)
             quantize_c3(0, 0)
             quantize_c3(0, 1)
             quantize_t2(0, 0)
             quantize_c3(1, 0)
             quantize_c3(1, 1)
-            quantize_t2(0, 1)
-            for r in range(2):
-                for g in range(2):
-                    step1(1, r, g)
-                    empty1(1, r, g, "S")
-            quantize_t2(0, 2)
-            quantize_t2(0, 3)
+            for r in range(1, 4):
+                quantize_t2(0, r)
 
-            one_round(pair(0, 0, 0), [None, (1, 2)], [W(2, 0), QT(1, 0), QT(1, 1), W(2, 1)])
-            one_round(pair(0, 0, 1), [(1, 3)], [I3(2, 0), QT(1, 2), I3(2, 1), QT(1, 3)])
-            one_round(pair(1, 0, 0), [], [Q3(2, 0), Q3(2, 1), I2(2, 0)])
-            one_round(pair(1, 0, 1), [], [I2(2, 1), Q2(2, 0), Q2(2, 1)])
-            one_round(col(0, 2), [None, None, None, (2, 0)], [W(3, 0), E1(2, 0), W(3, 1), QT(2, 0)])
-            one_round(col(1, 2), [None, (2, 1), None, (2, 2)], [E1(2, 1), I3(3, 0), QT(2, 1), E1(2, 2), I3(3, 1), QT(2, 2)])
-            one_round(pair(2, 0, 0), [(2, 3)], [E1(2, 3), Q3(3, 0), QT(2, 3), Q3(3, 1)])
-            one_round(pair(2, 0, 1), [], [I2(3, 0), E2(2, 1, 3)])
-            one_round(pair(2, 1, 0), [], [I2(3, 1), E2(2, 3, 1), Q2(3, 0)])
-            one_round(pair(2, 1, 1), [], [Q2(3, 1), E2(2, 3, 2), E2(2, 3, 3)])
-            one_round(col(0, 3), [None, (3, 0)], [E2(0, 3, 0), E1(3, 0), E2(0, 3, 2), QT(3, 0)])
-            one_round(col(1, 3), [None, (3, 1)], [E2(1, 3, 0), E1(3, 1), E2(1, 3, 2), QT(3, 1)])
-            one_round(row(3, 0), [None, (3, 2)], [E2(3, 0, 0), E1(3, 2), E2(3, 2, 0), QT(3, 2)])
-            one_round(row(3, 1), [None, (3, 3)], [E2(3, 0, 1), E1(3, 3), E2(3, 2, 1), QT(3, 3)])
-            one_round(row(3, 2), [], [E2(3, 1, 2), E2(3, 3, 2)])
-            one_round(row(3, 3), [], [E2(3, 1, 3), E2(3, 3, 3)])
+            widen_c3(2, 0)
+            quantize_t2(1, 0)
+            quantize_t2(1, 1)
+            widen_c3(2, 1)
+            for g in range(2):
+                group_c3(2, g)
+                quantize_t2(1, 2 + g)
+            for io in range(2):
+                for r in range(4):
+                    products(io, [0, 1], r)
+            for g in range(2):
+                quantize_c3(2, g)
+            for step in (widen_c3, group_c3, quantize_c3):
+                for g in range(2):
+                    step(3, g)
+            for io in range(2):
+                for r in range(4):
+                    products(io, [2], r)
+            for step in (group_c2, quantize_c2):
+                for g in range(2):
+                    step(2, g)
+            for r in range(4):
+                products(0, [3], r)
+            products(1, [3], 0)
+            make_tile(2, 0)
+            empty1(2, 0, 1, vector)
+            step2(1, [3], 1)
+            empty2(1, 3, 1, vector)
+            quantize_t2(2, 0)
+            products(1, [3], 2)
+            step2(1, [3], 3)
+            empty2(1, 3, 3, vector)
+
+            slice3 = [[(group_c2, 0)], [(group_c2, 1)], [(quantize_c2, 0), (quantize_c2, 1)]]
+            for n in range(7):
+                io, r = 2 + n // 4, n % 4
+                ahead = (2 + (n + 1) // 4, (n + 1) % 4)
+                make_tile(*ahead)
+                empty1(*ahead, 1, vector)
+                step2(io, [0, 1], r)
+                if n < len(slice3):
+                    empty2(io, 0, r, scalar)
+                    for step, g in slice3[n]:
+                        step(3, g)
+                else:
+                    empty2(io, 0, r, vector)
+                empty2(io, 1, r, scalar)
+                quantize_t2(*ahead)
+                step2(io, [2, 3], r)
+                empty2(io, 2, r, vector)
+                empty2(io, 3, r, scalar)
+            for c in (0, 2):
+                step2(3, [c, c + 1], 3)
+                empty2(3, c, 3, scalar)
+                empty2(3, c + 1, 3, vector)

@@ -99,11 +99,11 @@ def tile_linear2mpo_pa_kernel(tc, t1, core2, core3_bytes, core3_scale, out):
         def quantize_c2(io, g):
             quantize(c2_codes[io, g][:], c2_scales[io, g][:], c2_grouped[io, g][:])
 
-        def widen_c3(c, g, on_scalar=False):
+        def widen_c3(c, g, on_scalar=()):
             c3_wide[c, g] = work.tile([128, 4, 512], BF16, name="c3_wide", align_bytes=64, bufs=4)
             for t in range(4):
                 src = c3_bytes[c // 2, g][:, t, (c % 2) * 512 : (c % 2 + 1) * 512].bitcast(FP8)
-                if on_scalar:
+                if t in on_scalar:
                     nc.scalar.activation(out=c3_wide[c, g][:, t, :], in_=src, func=COPY, scale=scale[:, g, t : t + 1])
                 else:
                     nc.vector.tensor_scalar(out=c3_wide[c, g][:, t, :], in0=src, scalar1=scale[:, g, t : t + 1], scalar2=None, op0=MULT)
@@ -204,19 +204,19 @@ def tile_linear2mpo_pa_kernel(tc, t1, core2, core3_bytes, core3_scale, out):
             load_c2(2, keep.tile([128, 4, 1024], BF16, name="c2_raw_2"))
             load_c2(3, keep.tile([128, 4, 1024], BF16, name="c2_raw_3"))
             make_identity(nc, ident[:])
-            vector(perm[:].rearrange("p (o s) -> p s o", s=4), ident[:].rearrange("p (s o) -> p s o", s=4))
+            scalar(perm[:].rearrange("p (o s) -> p s o", s=4), ident[:].rearrange("p (s o) -> p s o", s=4))
 
             widen_c3(0, 0)
-            widen_c3(1, 0, on_scalar=True)
+            widen_c3(1, 0, on_scalar=range(4))
             group_c2(0, 0)
-            turn_t1(0)
             group_c3(1, 0, scalar)
+            turn_t1(0)
             quantize_c2(0, 0)
             group_c3(0, 0)
             group_c2(0, 1)
             quantize_t1(0)
-            widen_c3(1, 1, on_scalar=True)
-            widen_c3(0, 1)
+            widen_c3(1, 1, on_scalar=range(4))
+            widen_c3(0, 1, on_scalar=[3])
             turn_t1(1)
             quantize_c2(0, 1)
             group_c2(1, 1, scalar)

@@ -48,7 +48,7 @@ def tile_linear2mpo_pa_kernel(tc, t1, core2, core3_bytes, core3_scale, out):
                 c2_scales[a, g] = keep.tile([128, 512], U8, name="c2_scales_%d_%d" % (a, g), align_bytes=64)
                 c3_codes[a, g] = keep.tile([128, 512], U32, name="c3_codes_%d_%d" % (a, g), align_bytes=64)
                 c3_scales[a, g] = keep.tile([128, 512], U8, name="c3_scales_%d_%d" % (a, g), align_bytes=64)
-        c3_bytes = {(j, g): keep.tile([128, 4, 1024], U8, name="c3_bytes_%d_%d" % (j, g)) for j in range(2) for g in range(2)}
+        c3_bytes = {}
 
         free_banks = [psum.tile([128, 512], F32, name="bank_%d" % b) for b in range(8)]
         c2_raw, c2_grouped, c3_wide, c3_grouped, t2_grouped, full_banks, results = {}, {}, {}, {}, {}, {}, {}
@@ -74,8 +74,11 @@ def tile_linear2mpo_pa_kernel(tc, t1, core2, core3_bytes, core3_scale, out):
                 c2_raw[io, g] = raw[:, :, g * 512 : (g + 1) * 512]
             nc.sync.dma_start(out=raw[:], in_=core2_v[:, :, io, :])
 
-        def load_c3(j, g, places=slice(0, 4)):
-            nc.sync.dma_start(out=c3_bytes[j, g][:, places, :], in_=core3_v[g][:, places, j * 1024 : (j + 1) * 1024])
+        def load_c3(chunks, g):
+            raw = keep.tile([128, 4, len(chunks) * 512], U8, name="c3_bytes_%d_%d" % (chunks[0], g))
+            for n, c in enumerate(chunks):
+                c3_bytes[c, g] = raw[:, :, n * 512 : (n + 1) * 512]
+            nc.sync.dma_start(out=raw[:], in_=core3_v[g][:, :, chunks[0] * 512 : (chunks[-1] + 1) * 512])
 
         def turn_t1(a):
             bank = take_bank(("t1", a))
@@ -102,7 +105,7 @@ def tile_linear2mpo_pa_kernel(tc, t1, core2, core3_bytes, core3_scale, out):
         def widen_c3(c, g, on_scalar=()):
             c3_wide[c, g] = work.tile([128, 4, 512], BF16, name="c3_wide", align_bytes=64, bufs=4)
             for t in range(4):
-                src = c3_bytes[c // 2, g][:, t, (c % 2) * 512 : (c % 2 + 1) * 512].bitcast(FP8)
+                src = c3_bytes[c, g][:, t, :].bitcast(FP8)
                 if t in on_scalar:
                     nc.scalar.activation(out=c3_wide[c, g][:, t, :], in_=src, func=COPY, scale=scale[:, g, t : t + 1])
                 else:
@@ -152,12 +155,10 @@ def tile_linear2mpo_pa_kernel(tc, t1, core2, core3_bytes, core3_scale, out):
                                         start=(g == 0), stop=(g == 1))
 
         def store_unit(io, c, r):
-            if io == 3 or (io == 0 and c < 2):
-                return (r, r + 1), (c - c % 2, c - c % 2 + 2)
             if io == 2:
                 return (r, r + 1), (0, 4)
-            if c < 2:
-                return (r - r % 2, r - r % 2 + 2), (0, 2)
+            if io == 3 or c < 2:
+                return (r, r + 1), (c - c % 2, c - c % 2 + 2)
             return (0, 4), (c, c + 1)
 
         def empty2(io, c, r, copy):
@@ -191,65 +192,73 @@ def tile_linear2mpo_pa_kernel(tc, t1, core2, core3_bytes, core3_scale, out):
 
         with tc.manual_schedule():
             nc.scalar.dma_start(out=scale[:], in_=core3_scale.rearrange("(g p t) a b c -> p g (t a b c)", g=2, t=4))
-            load_c3(0, 0, slice(0, 2))
-            load_c3(0, 0, slice(2, 4))
+            load_c3([0], 0)
+            load_c3([1], 0)
             load_c2_pass(0, 0)
             load_t1(0)
             load_c2_pass(0, 1)
-            load_c3(0, 1)
             load_t1(1)
-            load_c2(1, stage.tile([128, 4, 1024], BF16, name="whole", bufs=WHOLE_SLOTS))
-            load_c3(1, 0)
-            load_c3(1, 1)
+            load_c3([0], 1)
+            load_c2_pass(1, 0)
+            load_c2_pass(1, 1)
+            load_c3([1], 1)
+            load_c3([2, 3], 0)
+            load_c3([2, 3], 1)
             load_c2(2, keep.tile([128, 4, 1024], BF16, name="c2_raw_2"))
             load_c2(3, keep.tile([128, 4, 1024], BF16, name="c2_raw_3"))
             make_identity(nc, ident[:])
             scalar(perm[:].rearrange("p (o s) -> p s o", s=4), ident[:].rearrange("p (s o) -> p s o", s=4))
 
-            widen_c3(0, 0)
+            widen_c3(0, 0, on_scalar=[3])
             widen_c3(1, 0, on_scalar=range(4))
-            group_c2(0, 0)
-            group_c3(1, 0, scalar)
-            turn_t1(0)
-            quantize_c2(0, 0)
             group_c3(0, 0)
-            group_c2(0, 1)
+            group_c2(0, 0)
+            turn_t1(0)
+            quantize_c3(0, 0)
+            quantize_c2(0, 0)
             quantize_t1(0)
-            widen_c3(1, 1, on_scalar=range(4))
-            widen_c3(0, 1, on_scalar=[3])
+            group_c2(0, 1)
+            group_c3(1, 0, scalar)
             turn_t1(1)
+            step1(0, 0, 0)
+            empty1(0, 0, 0, scalar)
+            step1(0, 1, 0)
+            empty1(0, 1, 0, scalar)
+            widen_c3(0, 1, on_scalar=[3])
             quantize_c2(0, 1)
-            group_c2(1, 1, scalar)
             group_c2(1, 0)
             quantize_t1(1)
-            group_c3(0, 1)
+            quantize_c3(1, 0)
+            for r, g in [(0, 1), (1, 1), (2, 0), (2, 1), (3, 0), (3, 1)]:
+                step1(0, r, g)
+                empty1(0, r, g, scalar)
+            group_c2(1, 1)
             quantize_c2(1, 0)
+            group_c3(0, 1)
             quantize_c2(1, 1)
-            for io in range(2):
-                for r in range(4):
-                    make_tile(io, r)
-                    empty1(io, r, 1, scalar)
-            group_c3(1, 1)
-            quantize_c3(0, 0)
+            widen_c3(1, 1, on_scalar=range(4))
             quantize_c3(0, 1)
             quantize_t2(0, 0)
-            quantize_c3(1, 0)
+            quantize_t2(0, 1)
+            group_c3(1, 1)
+            quantize_t2(0, 2)
             quantize_c3(1, 1)
-            for r in range(1, 4):
-                quantize_t2(0, r)
-
+            for g in range(2):
+                for r in range(4):
+                    step1(1, r, g)
+                    empty1(1, r, g, scalar)
             widen_c3(2, 0)
-            quantize_t2(1, 0)
-            quantize_t2(1, 1)
+            quantize_t2(0, 3)
             widen_c3(2, 1)
             for g in range(2):
+                quantize_t2(1, g)
                 group_c3(2, g)
+            for g in range(2):
                 quantize_t2(1, 2 + g)
+                quantize_c3(2, g)
             for io in range(2):
                 for r in range(4):
                     products(io, [0, 1], r)
-            for g in range(2):
-                quantize_c3(2, g)
             for step in (widen_c3, group_c3, quantize_c3):
                 for g in range(2):
                     step(3, g)
@@ -262,20 +271,20 @@ def tile_linear2mpo_pa_kernel(tc, t1, core2, core3_bytes, core3_scale, out):
             for r in range(4):
                 products(0, [3], r)
             products(1, [3], 0)
-            make_tile(2, 0)
-            empty1(2, 0, 1, vector)
-            step2(1, [3], 1)
-            empty2(1, 3, 1, vector)
+            products(1, [3], 1)
+            for g in range(2):
+                step1(2, 0, g)
+                empty1(2, 0, g, vector)
             quantize_t2(2, 0)
             products(1, [3], 2)
-            step2(1, [3], 3)
-            empty2(1, 3, 3, vector)
-
+            products(1, [3], 3)
             slice3 = [[(group_c2, 0)], [(group_c2, 1)], [(quantize_c2, 0), (quantize_c2, 1)]]
             for n in range(7):
                 io, r = 2 + n // 4, n % 4
                 ahead = (2 + (n + 1) // 4, (n + 1) % 4)
-                make_tile(*ahead)
+                step1(*ahead, 0)
+                empty1(*ahead, 0, vector if n == 0 else scalar)
+                step1(*ahead, 1)
                 empty1(*ahead, 1, vector)
                 step2(io, [0, 1], r)
                 if n < len(slice3):

@@ -97,7 +97,7 @@ def tile_linear2mpo_pa_kernel(tc, t1, core2, core3_bytes, core3_scale, out):
 
         def group_c2(io, g, copy=vector):
             c2_grouped[io, g] = work.tile([128, 2048], BF16, name="c2_grouped", align_bytes=64, bufs=3)
-            copy(c2_grouped[io, g][:].rearrange("p (t m j) -> p m j t", t=4, j=4), c2_raw[io, g].rearrange("p j (m t) -> p m j t", t=4))
+            copy(c2_grouped[io, g][:].rearrange("p (t m e j) -> p m t j e", t=4, e=2, j=4), c2_raw[io, g].rearrange("p j (m e t) -> p m t j e", e=2, t=4))
 
         def quantize_c2(io, g):
             quantize(c2_codes[io, g][:], c2_scales[io, g][:], c2_grouped[io, g][:])
@@ -113,7 +113,7 @@ def tile_linear2mpo_pa_kernel(tc, t1, core2, core3_bytes, core3_scale, out):
 
         def group_c3(c, g, copy=vector):
             c3_grouped[c, g] = work.tile([128, 2048], BF16, name="c3_grouped", align_bytes=64, bufs=4)
-            copy(c3_grouped[c, g][:].rearrange("p (n i t) -> p n t i", i=4, t=4), c3_wide[c, g][:].rearrange("p t (n i) -> p n t i", i=4))
+            copy(c3_grouped[c, g][:].rearrange("p (n i t) -> p n t i", i=2, t=4), c3_wide[c, g][:].rearrange("p t (n i) -> p n t i", i=2))
 
         def quantize_c3(c, g):
             quantize(c3_codes[c, g][:], c3_scales[c, g][:], c3_grouped[c, g][:])

@@ -74,11 +74,13 @@ def tile_linear2mpo_pa_kernel(tc, t1, core2, core3_bytes, core3_scale, out):
                 c2_raw[io, g] = raw[:, :, g * 512 : (g + 1) * 512]
             nc.sync.dma_start(out=raw[:], in_=core2_v[:, :, io, :])
 
-        def load_c3(chunks, g):
+        def load_c3(chunks, g, parts=1):
             raw = keep.tile([128, 4, len(chunks) * 512], U8, name="c3_bytes_%d_%d" % (chunks[0], g))
             for n, c in enumerate(chunks):
                 c3_bytes[c, g] = raw[:, :, n * 512 : (n + 1) * 512]
-            nc.sync.dma_start(out=raw[:], in_=core3_v[g][:, :, chunks[0] * 512 : (chunks[-1] + 1) * 512])
+            for t in range(0, 4, 4 // parts):
+                places = slice(t, t + 4 // parts)
+                nc.sync.dma_start(out=raw[:, places, :], in_=core3_v[g][:, places, chunks[0] * 512 : (chunks[-1] + 1) * 512])
 
         def turn_t1(a):
             bank = take_bank(("t1", a))
@@ -192,16 +194,14 @@ def tile_linear2mpo_pa_kernel(tc, t1, core2, core3_bytes, core3_scale, out):
 
         with tc.manual_schedule():
             nc.scalar.dma_start(out=scale[:], in_=core3_scale.rearrange("(g p t) a b c -> p g (t a b c)", g=2, t=4))
-            load_c3([0], 0)
-            load_c3([1], 0)
+            load_c3([0, 1], 0, parts=2)
             load_c2_pass(0, 0)
             load_t1(0)
+            load_c3([0, 1], 1)
             load_c2_pass(0, 1)
             load_t1(1)
-            load_c3([0], 1)
             load_c2_pass(1, 0)
             load_c2_pass(1, 1)
-            load_c3([1], 1)
             load_c3([2, 3], 0)
             load_c3([2, 3], 1)
             load_c2(2, keep.tile([128, 4, 1024], BF16, name="c2_raw_2"))
@@ -209,57 +209,58 @@ def tile_linear2mpo_pa_kernel(tc, t1, core2, core3_bytes, core3_scale, out):
             make_identity(nc, ident[:])
             scalar(perm[:].rearrange("p (o s) -> p s o", s=4), ident[:].rearrange("p (s o) -> p s o", s=4))
 
-            widen_c3(0, 0, on_scalar=[3])
-            widen_c3(1, 0, on_scalar=range(4))
+            widen_c3(0, 0)
+            widen_c3(1, 0, on_scalar=[1, 2, 3])
             group_c3(0, 0)
             group_c2(0, 0)
-            turn_t1(0)
+            group_c3(1, 0, scalar)
             quantize_c3(0, 0)
             quantize_c2(0, 0)
-            quantize_t1(0)
+            turn_t1(0)
+            widen_c3(0, 1, on_scalar=range(4))
             group_c2(0, 1)
-            group_c3(1, 0, scalar)
+            quantize_t1(0)
             turn_t1(1)
-            step1(0, 0, 0)
-            empty1(0, 0, 0, scalar)
-            step1(0, 1, 0)
-            empty1(0, 1, 0, scalar)
-            widen_c3(0, 1, on_scalar=[3])
+            widen_c3(1, 1, on_scalar=range(4))
             quantize_c2(0, 1)
             group_c2(1, 0)
             quantize_t1(1)
-            quantize_c3(1, 0)
-            for r, g in [(0, 1), (1, 1), (2, 0), (2, 1), (3, 0), (3, 1)]:
-                step1(0, r, g)
-                empty1(0, r, g, scalar)
             group_c2(1, 1)
             quantize_c2(1, 0)
             group_c3(0, 1)
             quantize_c2(1, 1)
-            widen_c3(1, 1, on_scalar=range(4))
-            quantize_c3(0, 1)
-            quantize_t2(0, 0)
-            quantize_t2(0, 1)
-            group_c3(1, 1)
-            quantize_t2(0, 2)
-            quantize_c3(1, 1)
-            for g in range(2):
-                for r in range(4):
-                    step1(1, r, g)
-                    empty1(1, r, g, scalar)
-            widen_c3(2, 0)
-            quantize_t2(0, 3)
-            widen_c3(2, 1)
-            for g in range(2):
-                quantize_t2(1, g)
-                group_c3(2, g)
-            for g in range(2):
-                quantize_t2(1, 2 + g)
-                quantize_c3(2, g)
             for io in range(2):
                 for r in range(4):
-                    products(io, [0, 1], r)
-            for step in (widen_c3, group_c3, quantize_c3):
+                    make_tile(io, r)
+                    empty1(io, r, 1, scalar)
+            group_c3(1, 1)
+            quantize_c3(0, 1)
+            for r in range(4):
+                quantize_t2(0, r)
+            quantize_c3(1, 0)
+            quantize_c3(1, 1)
+            widen_c3(2, 0)
+            for c in range(2):
+                for r in range(4):
+                    step2(0, [c], r)
+                    if c == 1:
+                        empty2(0, 0, r, scalar)
+                        empty2(0, 1, r, scalar)
+            quantize_t2(1, 0)
+            widen_c3(2, 1, on_scalar=[])
+            quantize_t2(1, 1)
+            for g in range(2):
+                group_c3(2, g)
+                quantize_t2(1, 2 + g)
+            for g in range(2):
+                quantize_c3(2, g)
+            widen_c3(3, 0)
+            for r in range(2):
+                products(1, [0, 1], r)
+            widen_c3(3, 1, on_scalar=[3])
+            for r in range(2, 4):
+                products(1, [0, 1], r)
+            for step in (group_c3, quantize_c3):
                 for g in range(2):
                     step(3, g)
             for io in range(2):
@@ -286,15 +287,12 @@ def tile_linear2mpo_pa_kernel(tc, t1, core2, core3_bytes, core3_scale, out):
                 empty1(*ahead, 0, vector if n == 0 else scalar)
                 step1(*ahead, 1)
                 empty1(*ahead, 1, vector)
-                step2(io, [0, 1], r)
-                if n < len(slice3):
-                    empty2(io, 0, r, scalar)
-                    for step, g in slice3[n]:
-                        step(3, g)
-                else:
-                    empty2(io, 0, r, vector)
-                empty2(io, 1, r, scalar)
+                for step, g in slice3[n] if n < len(slice3) else []:
+                    step(3, g)
                 quantize_t2(*ahead)
+                step2(io, [0, 1], r)
+                empty2(io, 0, r, scalar if n < len(slice3) else vector)
+                empty2(io, 1, r, scalar)
                 step2(io, [2, 3], r)
                 empty2(io, 2, r, vector)
                 empty2(io, 3, r, scalar)

@@ -14,8 +14,8 @@ COPY = mybir.ActivationFunctionType.Copy
 
 FLOPS = 2 * 512 * 512 * 4096 + 2 * 2048 * 1024 * 2048
 
-WHOLE_SLOTS = 6
-HALF_SLOTS = 6
+SLOTS = 35
+SLOT_BYTES = 4096
 
 
 def tile_linear2mpo_pa_kernel(tc, t1, core2, core3_bytes, core3_scale, out):
@@ -35,8 +35,6 @@ def tile_linear2mpo_pa_kernel(tc, t1, core2, core3_bytes, core3_scale, out):
         ident = keep.tile([128, 128], F32, name="ident")
         perm = keep.tile([128, 128], F32, name="perm")
         scale = keep.tile([128, 2, 4], F32, name="scale")
-        t1_raw = [keep.tile([128, 2, 512], BF16, name="t1_raw_%d" % a) for a in range(2)]
-        t1_grouped = keep.tile([128, 512, 4], BF16, name="t1_grouped", align_bytes=64)
         t1_codes = keep.tile([128, 512], U32, name="t1_codes", align_bytes=64)
         t1_scales = keep.tile([128, 512], U8, name="t1_scales", align_bytes=64)
         c2_codes, c2_scales, t2_codes, t2_scales, c3_codes, c3_scales = {}, {}, {}, {}, {}, {}
@@ -50,29 +48,50 @@ def tile_linear2mpo_pa_kernel(tc, t1, core2, core3_bytes, core3_scale, out):
                 c3_scales[a, g] = keep.tile([128, 512], U8, name="c3_scales_%d_%d" % (a, g), align_bytes=64)
         c3_bytes = {}
 
-        free_banks = [psum.tile([128, 512], F32, name="bank_%d" % b) for b in range(8)]
-        c2_raw, c2_grouped, c3_wide, c3_grouped, t2_grouped, full_banks, results = {}, {}, {}, {}, {}, {}, {}
+        written, awaited, quantised_at, copied_at, group = [], {vector: 0, scalar: 0}, {}, {}, {"banks": 1}
+        free_banks = [(psum.tile([128, 512], F32, name="bank_%d" % b), scalar, 0) for b in range(8)]
+        t1_raw, t1_grouped, c2_raw, c2_grouped, c3_wide, c3_grouped, t2_grouped, full_banks, results = {}, {}, {}, {}, {}, {}, {}, {}, {}
+
+        free_slots, slot_of = list(range(SLOTS)), {}
+
+        def take_slot(key, shape, dtype):
+            slot_of[key] = free_slots[0]
+            free_slots.remove(slot_of[key])
+            name = "_".join(str(part) for part in key)
+            return stage.tile(shape, dtype, name=name, align_bytes=64, offset=slot_of[key] * SLOT_BYTES)
+
+        def release_slot(key):
+            free_slots.append(slot_of[key])
 
         def take_bank(key):
-            full_banks[key] = free_banks[0]
-            free_banks.remove(full_banks[key])
-            return full_banks[key]
+            covered = [entry for entry in free_banks if entry[2] <= awaited[entry[1]]]
+            entry = covered[0] if covered else free_banks[: group["banks"]][-1]
+            bank, engine, number = entry
+            awaited[engine] = max(awaited[engine], number)
+            free_banks.remove(entry)
+            full_banks[key] = bank
+            return bank
 
-        def quantize(codes, scales, grouped):
+        def release_bank(bank, engine):
+            written.append(bank)
+            free_banks.append((bank, engine, len(written)))
+
+        def quantize(key, codes, scales, grouped):
             nc.vector.quantize_mx(out=codes.bitcast(FP8X4), scales=scales, in_=grouped)
+            written.append(codes)
+            quantised_at[key] = len(written)
+
+        def await_operands(*keys):
+            awaited[vector] = max([awaited[vector]] + [quantised_at[key] for key in keys])
+            awaited[scalar] = max([awaited[scalar]] + [copied_at.get(key, 0) for key in keys])
 
         def load_t1(a):
+            t1_raw[a] = take_slot(("t1_raw", a), [128, 2, 512], BF16)
             nc.sync.dma_start(out=t1_raw[a][:], in_=t1_rows[a * 256 : (a + 1) * 256, :].rearrange("(r p) k -> p r k", r=2))
 
         def load_c2_pass(io, g):
-            raw = stage.tile([128, 4, 512], BF16, name="half", bufs=HALF_SLOTS)
-            c2_raw[io, g] = raw[:]
-            nc.sync.dma_start(out=raw[:], in_=core2_v[:, :, io, g * 512 : (g + 1) * 512])
-
-        def load_c2(io, raw):
-            for g in range(2):
-                c2_raw[io, g] = raw[:, :, g * 512 : (g + 1) * 512]
-            nc.sync.dma_start(out=raw[:], in_=core2_v[:, :, io, :])
+            c2_raw[io, g] = take_slot(("c2_raw", io, g), [128, 4, 512], BF16)
+            nc.sync.dma_start(out=c2_raw[io, g][:], in_=core2_v[:, :, io, g * 512 : (g + 1) * 512])
 
         def load_c3(chunks, g, parts=1):
             raw = keep.tile([128, 4, len(chunks) * 512], U8, name="c3_bytes_%d_%d" % (chunks[0], g))
@@ -89,23 +108,28 @@ def tile_linear2mpo_pa_kernel(tc, t1, core2, core3_bytes, core3_scale, out):
                 words = t1_raw[a][:, e, :].bitcast(F32)
                 for u in range(2):
                     nc.tensor.transpose(turned[:, e, u, :], words[:, u::2], perm[:])
-            dst = t1_grouped[:, a * 256 : (a + 1) * 256, :].rearrange("p n t -> p (n t)").bitcast(F32)
+            release_slot(("t1_raw", a))
+            t1_grouped[a] = take_slot(("t1_grouped", a), [128, 1024], BF16)
+            dst = t1_grouped[a][:].bitcast(F32)
             scalar(dst.rearrange("p (e n u) -> p e n u", e=2, u=2), turned.rearrange("p e u n -> p e n u"))
-            free_banks.append(bank)
+            release_bank(bank, scalar)
 
         def quantize_t1(a):
             cols = slice(a * 256, (a + 1) * 256)
-            quantize(t1_codes[:, cols], t1_scales[:, cols], t1_grouped[:, cols, :].rearrange("p n t -> p (n t)"))
+            quantize(("t1", a), t1_codes[:, cols], t1_scales[:, cols], t1_grouped[a][:])
+            release_slot(("t1_grouped", a))
 
         def group_c2(io, g, copy=vector):
-            c2_grouped[io, g] = work.tile([128, 2048], BF16, name="c2_grouped", align_bytes=64, bufs=3)
-            copy(c2_grouped[io, g][:].rearrange("p (t m e j) -> p m t j e", t=4, e=2, j=4), c2_raw[io, g].rearrange("p j (m e t) -> p m t j e", e=2, t=4))
+            c2_grouped[io, g] = take_slot(("c2_grouped", io, g), [128, 2048], BF16)
+            copy(c2_grouped[io, g][:].rearrange("p (t m e j) -> p m t j e", t=4, e=2, j=4), c2_raw[io, g][:].rearrange("p j (m e t) -> p m t j e", e=2, t=4))
+            release_slot(("c2_raw", io, g))
 
         def quantize_c2(io, g):
-            quantize(c2_codes[io, g][:], c2_scales[io, g][:], c2_grouped[io, g][:])
+            quantize(("c2", io, g), c2_codes[io, g][:], c2_scales[io, g][:], c2_grouped[io, g][:])
+            release_slot(("c2_grouped", io, g))
 
         def widen_c3(c, g, on_scalar=()):
-            c3_wide[c, g] = work.tile([128, 4, 512], BF16, name="c3_wide", align_bytes=64, bufs=4)
+            c3_wide[c, g] = take_slot(("c3_wide", c, g), [128, 4, 512], BF16)
             for t in range(4):
                 src = c3_bytes[c, g][:, t, :].bitcast(FP8)
                 if t in on_scalar:
@@ -114,13 +138,16 @@ def tile_linear2mpo_pa_kernel(tc, t1, core2, core3_bytes, core3_scale, out):
                     nc.vector.tensor_scalar(out=c3_wide[c, g][:, t, :], in0=src, scalar1=scale[:, g, t : t + 1], scalar2=None, op0=MULT)
 
         def group_c3(c, g, copy=vector):
-            c3_grouped[c, g] = work.tile([128, 2048], BF16, name="c3_grouped", align_bytes=64, bufs=4)
+            c3_grouped[c, g] = take_slot(("c3_grouped", c, g), [128, 2048], BF16)
             copy(c3_grouped[c, g][:].rearrange("p (n i t) -> p n t i", i=2, t=4), c3_wide[c, g][:].rearrange("p t (n i) -> p n t i", i=2))
+            release_slot(("c3_wide", c, g))
 
         def quantize_c3(c, g):
-            quantize(c3_codes[c, g][:], c3_scales[c, g][:], c3_grouped[c, g][:])
+            quantize(("c3", c, g), c3_codes[c, g][:], c3_scales[c, g][:], c3_grouped[c, g][:])
+            release_slot(("c3_grouped", c, g))
 
         def step1(io, r, g):
+            await_operands(("c2", io, g), ("t1", r // 2))
             bank = take_bank(("step1", io, r, g))
             rows = slice(r * 128, (r + 1) * 128)
             for t in range(4):
@@ -135,11 +162,13 @@ def tile_linear2mpo_pa_kernel(tc, t1, core2, core3_bytes, core3_scale, out):
                 t2_grouped[io, r] = work.tile([128, 2, 128, 4], BF16, name="t2_grouped", align_bytes=64, bufs=8)
             bank = full_banks["step1", io, r, g]
             copy(t2_grouped[io, r][:, g], bank[:].rearrange("p (t n) -> p n t", t=4))
-            free_banks.append(bank)
+            release_bank(bank, copy)
+            if copy == scalar:
+                copied_at["t2", io, r] = len(written)
 
         def quantize_t2(io, r):
             cols = slice(r * 256, (r + 1) * 256)
-            quantize(t2_codes[io][:, cols], t2_scales[io][:, cols], t2_grouped[io, r][:].rearrange("p g n t -> p (g n t)"))
+            quantize(("t2", io, r), t2_codes[io][:, cols], t2_scales[io][:, cols], t2_grouped[io, r][:].rearrange("p g n t -> p (g n t)"))
 
         def make_tile(io, r):
             step1(io, r, 0)
@@ -147,6 +176,7 @@ def tile_linear2mpo_pa_kernel(tc, t1, core2, core3_bytes, core3_scale, out):
             step1(io, r, 1)
 
         def step2(io, chunks, r):
+            await_operands(("t2", io, r), ("c3", chunks[0], 0))
             banks = [take_bank(("step2", io, c, r)) for c in chunks]
             for g in range(2):
                 rows = slice(r * 256 + g * 128, r * 256 + (g + 1) * 128)
@@ -157,35 +187,26 @@ def tile_linear2mpo_pa_kernel(tc, t1, core2, core3_bytes, core3_scale, out):
                                         start=(g == 0), stop=(g == 1))
 
         def store_unit(io, c, r):
-            if io == 2:
-                return (r, r + 1), (0, 4)
-            if io == 3 or c < 2:
+            if io >= 2 or c < 2:
                 return (r, r + 1), (c - c % 2, c - c % 2 + 2)
-            return (0, 4), (c, c + 1)
+            return (r - r % 2, r - r % 2 + 2), (c, c + 1)
 
         def empty2(io, c, r, copy):
             (r0, r1), (c0, c1) = store_unit(io, c, r)
             key = (io, r0, c0)
             count = (r1 - r0) * (c1 - c0)
             if key not in results:
-                if count == 4:
-                    tile = stage.tile([128, r1 - r0, (c1 - c0) * 512], F32, name="whole", bufs=WHOLE_SLOTS)
-                else:
-                    tile = stage.tile([128, r1 - r0, (c1 - c0) * 512], F32, name="half", bufs=HALF_SLOTS)
-                results[key] = (tile, [])
+                results[key] = (take_slot(("result",) + key, [128, r1 - r0, (c1 - c0) * 512], F32), [])
             tile, done = results[key]
             bank = full_banks["step2", io, c, r]
             copy(tile[:, r - r0, (c - c0) * 512 : (c - c0 + 1) * 512], bank[:])
-            free_banks.append(bank)
+            release_bank(bank, copy)
             done.append((c, r))
             if len(done) == count:
                 for s in range(4):
                     rows = out_v[s, io // 2, io % 2]
-                    if c1 - c0 == 4:
-                        nc.sync.dma_start(out=rows[:, r0], in_=tile[s:128:4, 0, :].rearrange("p (j x) -> p j x", j=2))
-                    else:
-                        cols = slice((c0 % 2) * 512, (c0 % 2 + c1 - c0) * 512)
-                        nc.sync.dma_start(out=rows[:, r0:r1, c0 // 2, cols], in_=tile[s:128:4])
+                    cols = slice((c0 % 2) * 512, (c0 % 2 + c1 - c0) * 512)
+                    nc.sync.dma_start(out=rows[:, r0:r1, c0 // 2, cols], in_=tile[s:128:4])
 
         def products(io, chunks, r):
             step2(io, chunks, r)
@@ -204,8 +225,9 @@ def tile_linear2mpo_pa_kernel(tc, t1, core2, core3_bytes, core3_scale, out):
             load_c2_pass(1, 1)
             load_c3([2, 3], 0)
             load_c3([2, 3], 1)
-            load_c2(2, keep.tile([128, 4, 1024], BF16, name="c2_raw_2"))
-            load_c2(3, keep.tile([128, 4, 1024], BF16, name="c2_raw_3"))
+            for io in range(2, 4):
+                for g in range(2):
+                    load_c2_pass(io, g)
             make_identity(nc, ident[:])
             scalar(perm[:].rearrange("p (o s) -> p s o", s=4), ident[:].rearrange("p (s o) -> p s o", s=4))
 
@@ -239,6 +261,7 @@ def tile_linear2mpo_pa_kernel(tc, t1, core2, core3_bytes, core3_scale, out):
                 quantize_t2(0, r)
             quantize_c3(1, 0)
             quantize_c3(1, 1)
+            group["banks"] = 2
             widen_c3(2, 0)
             for c in range(2):
                 for r in range(4):
@@ -279,6 +302,7 @@ def tile_linear2mpo_pa_kernel(tc, t1, core2, core3_bytes, core3_scale, out):
             quantize_t2(2, 0)
             products(1, [3], 2)
             products(1, [3], 3)
+            group["banks"] = 2
             slice3 = [[(group_c2, 0)], [(group_c2, 1)], [(quantize_c2, 0), (quantize_c2, 1)]]
             for n in range(7):
                 io, r = 2 + n // 4, n % 4

@@ -16,6 +16,7 @@ FLOPS = 2 * 512 * 512 * 4096 + 2 * 2048 * 1024 * 2048
 
 SLOTS = 35
 SLOT_BYTES = 4096
+HEAD_TILES = 8
 
 
 def tile_linear2mpo_pa_kernel(tc, t1, core2, core3_bytes, core3_scale, out):
@@ -48,7 +49,8 @@ def tile_linear2mpo_pa_kernel(tc, t1, core2, core3_bytes, core3_scale, out):
                 c3_scales[a, g] = keep.tile([128, 512], U8, name="c3_scales_%d_%d" % (a, g), align_bytes=64)
         c3_bytes = {}
 
-        written, awaited, quantised_at, copied_at, group = [], {vector: 0, scalar: 0}, {}, {}, {"banks": 1}
+        written, awaited, quantised_at, copied_at = [], {vector: 0, scalar: 0}, {}, {}
+        choice = {"oldest": 1}
         free_banks = [(psum.tile([128, 512], F32, name="bank_%d" % b), scalar, 0) for b in range(8)]
         t1_raw, t1_grouped, c2_raw, c2_grouped, c3_wide, c3_grouped, t2_grouped, full_banks, results = {}, {}, {}, {}, {}, {}, {}, {}, {}
 
@@ -65,7 +67,7 @@ def tile_linear2mpo_pa_kernel(tc, t1, core2, core3_bytes, core3_scale, out):
 
         def take_bank(key):
             covered = [entry for entry in free_banks if entry[2] <= awaited[entry[1]]]
-            entry = covered[0] if covered else free_banks[: group["banks"]][-1]
+            entry = covered[0] if covered else free_banks[: choice["oldest"]][-1]
             bank, engine, number = entry
             awaited[engine] = max(awaited[engine], number)
             free_banks.remove(entry)
@@ -119,18 +121,20 @@ def tile_linear2mpo_pa_kernel(tc, t1, core2, core3_bytes, core3_scale, out):
             quantize(("t1", a), t1_codes[:, cols], t1_scales[:, cols], t1_grouped[a][:])
             release_slot(("t1_grouped", a))
 
-        def group_c2(io, g, copy=vector):
+        def group_c2(io, g):
             c2_grouped[io, g] = take_slot(("c2_grouped", io, g), [128, 2048], BF16)
-            copy(c2_grouped[io, g][:].rearrange("p (t m e j) -> p m t j e", t=4, e=2, j=4), c2_raw[io, g][:].rearrange("p j (m e t) -> p m t j e", e=2, t=4))
+            vector(c2_grouped[io, g][:].rearrange("p (t n e j) -> p n t j e", t=4, e=2, j=4),
+                   c2_raw[io, g][:].rearrange("p j (n e t) -> p n t j e", e=2, t=4))
             release_slot(("c2_raw", io, g))
 
         def quantize_c2(io, g):
             quantize(("c2", io, g), c2_codes[io, g][:], c2_scales[io, g][:], c2_grouped[io, g][:])
             release_slot(("c2_grouped", io, g))
 
-        def widen_c3(c, g, on_scalar=()):
-            c3_wide[c, g] = take_slot(("c3_wide", c, g), [128, 4, 512], BF16)
-            for t in range(4):
+        def widen_c3(c, g, on_scalar=(), places=range(4)):
+            if (c, g) not in c3_wide:
+                c3_wide[c, g] = take_slot(("c3_wide", c, g), [128, 4, 512], BF16)
+            for t in places:
                 src = c3_bytes[c, g][:, t, :].bitcast(FP8)
                 if t in on_scalar:
                     nc.scalar.activation(out=c3_wide[c, g][:, t, :], in_=src, func=COPY, scale=scale[:, g, t : t + 1])
@@ -159,24 +163,25 @@ def tile_linear2mpo_pa_kernel(tc, t1, core2, core3_bytes, core3_scale, out):
 
         def empty1(io, r, g, copy):
             if (io, r) not in t2_grouped:
-                t2_grouped[io, r] = work.tile([128, 2, 128, 4], BF16, name="t2_grouped", align_bytes=64, bufs=8)
+                t2_grouped[io, r] = work.tile([128, 2, 128, 4], BF16, name="t2_grouped", align_bytes=64, bufs=HEAD_TILES)
             bank = full_banks["step1", io, r, g]
             copy(t2_grouped[io, r][:, g], bank[:].rearrange("p (t n) -> p n t", t=4))
             release_bank(bank, copy)
             if copy == scalar:
-                copied_at["t2", io, r] = len(written)
+                copied_at["t2", io, r, 0] = len(written)
 
-        def quantize_t2(io, r):
-            cols = slice(r * 256, (r + 1) * 256)
-            quantize(("t2", io, r), t2_codes[io][:, cols], t2_scales[io][:, cols], t2_grouped[io, r][:].rearrange("p g n t -> p (g n t)"))
+        def quantize_t2(io, r, passes=slice(0, 2)):
+            cols = slice(r * 256 + passes.start * 128, r * 256 + passes.stop * 128)
+            values = t2_grouped[io, r][:, passes].rearrange("p g n t -> p (g n t)")
+            quantize(("t2", io, r, passes.start), t2_codes[io][:, cols], t2_scales[io][:, cols], values)
 
-        def make_tile(io, r):
-            step1(io, r, 0)
-            empty1(io, r, 0, scalar)
-            step1(io, r, 1)
+        def make_tile(io, r, copies):
+            for g in range(2):
+                step1(io, r, g)
+                empty1(io, r, g, copies[g])
 
         def step2(io, chunks, r):
-            await_operands(("t2", io, r), ("c3", chunks[0], 0))
+            await_operands(("t2", io, r, 0), ("c3", chunks[0], 0))
             banks = [take_bank(("step2", io, c, r)) for c in chunks]
             for g in range(2):
                 rows = slice(r * 256 + g * 128, r * 256 + (g + 1) * 128)
@@ -194,7 +199,6 @@ def tile_linear2mpo_pa_kernel(tc, t1, core2, core3_bytes, core3_scale, out):
         def empty2(io, c, r, copy):
             (r0, r1), (c0, c1) = store_unit(io, c, r)
             key = (io, r0, c0)
-            count = (r1 - r0) * (c1 - c0)
             if key not in results:
                 results[key] = (take_slot(("result",) + key, [128, r1 - r0, (c1 - c0) * 512], F32), [])
             tile, done = results[key]
@@ -202,7 +206,7 @@ def tile_linear2mpo_pa_kernel(tc, t1, core2, core3_bytes, core3_scale, out):
             copy(tile[:, r - r0, (c - c0) * 512 : (c - c0 + 1) * 512], bank[:])
             release_bank(bank, copy)
             done.append((c, r))
-            if len(done) == count:
+            if len(done) == 2:
                 for s in range(4):
                     rows = out_v[s, io // 2, io % 2]
                     cols = slice((c0 % 2) * 512, (c0 % 2 + c1 - c0) * 512)
@@ -238,12 +242,14 @@ def tile_linear2mpo_pa_kernel(tc, t1, core2, core3_bytes, core3_scale, out):
             group_c3(1, 0, scalar)
             quantize_c3(0, 0)
             quantize_c2(0, 0)
+            quantize_c3(1, 0)
             turn_t1(0)
             widen_c3(0, 1, on_scalar=range(4))
             group_c2(0, 1)
             quantize_t1(0)
+            widen_c3(1, 1, on_scalar=range(4), places=range(2))
             turn_t1(1)
-            widen_c3(1, 1, on_scalar=range(4))
+            widen_c3(1, 1, on_scalar=range(4), places=range(2, 4))
             quantize_c2(0, 1)
             group_c2(1, 0)
             quantize_t1(1)
@@ -251,17 +257,22 @@ def tile_linear2mpo_pa_kernel(tc, t1, core2, core3_bytes, core3_scale, out):
             quantize_c2(1, 0)
             group_c3(0, 1)
             quantize_c2(1, 1)
-            for io in range(2):
-                for r in range(4):
-                    make_tile(io, r)
-                    empty1(io, r, 1, scalar)
-            group_c3(1, 1)
-            quantize_c3(0, 1)
             for r in range(4):
-                quantize_t2(0, r)
-            quantize_c3(1, 0)
+                make_tile(0, r, (scalar, scalar))
+            for r in range(4):
+                step1(1, r, 0)
+            for r in range(4):
+                step1(1, r, 1)
+                for g in range(2):
+                    empty1(1, r, g, scalar)
+            quantize_c3(0, 1)
+            quantize_t2(0, 0)
+            quantize_t2(0, 1)
+            group_c3(1, 1)
+            quantize_t2(0, 2)
             quantize_c3(1, 1)
-            group["banks"] = 2
+            quantize_t2(0, 3)
+
             widen_c3(2, 0)
             for c in range(2):
                 for r in range(4):
@@ -269,8 +280,9 @@ def tile_linear2mpo_pa_kernel(tc, t1, core2, core3_bytes, core3_scale, out):
                     if c == 1:
                         empty2(0, 0, r, scalar)
                         empty2(0, 1, r, scalar)
+            choice["oldest"] = 2
             quantize_t2(1, 0)
-            widen_c3(2, 1, on_scalar=[])
+            widen_c3(2, 1)
             quantize_t2(1, 1)
             for g in range(2):
                 group_c3(2, g)
@@ -294,23 +306,19 @@ def tile_linear2mpo_pa_kernel(tc, t1, core2, core3_bytes, core3_scale, out):
                     step(2, g)
             for r in range(4):
                 products(0, [3], r)
-            products(1, [3], 0)
-            products(1, [3], 1)
+            for r in range(2):
+                products(1, [3], r)
+            make_tile(2, 0, (vector, vector))
             for g in range(2):
-                step1(2, 0, g)
-                empty1(2, 0, g, vector)
-            quantize_t2(2, 0)
-            products(1, [3], 2)
-            products(1, [3], 3)
-            group["banks"] = 2
+                quantize_t2(2, 0, slice(g, g + 1))
+            for r in range(2, 4):
+                products(1, [3], r)
+
             slice3 = [[(group_c2, 0)], [(group_c2, 1)], [(quantize_c2, 0), (quantize_c2, 1)]]
             for n in range(7):
                 io, r = 2 + n // 4, n % 4
                 ahead = (2 + (n + 1) // 4, (n + 1) % 4)
-                step1(*ahead, 0)
-                empty1(*ahead, 0, vector if n == 0 else scalar)
-                step1(*ahead, 1)
-                empty1(*ahead, 1, vector)
+                make_tile(*ahead, (vector if n == 0 else scalar, vector))
                 for step, g in slice3[n] if n < len(slice3) else []:
                     step(3, g)
                 quantize_t2(*ahead)

@@ -34,6 +34,7 @@ def tile_linear2mpo_pa_kernel(tc, t1, core2, core3_bytes, core3_scale, out):
         out_v = out.rearrange("(r s i j) (O o h) q -> s i o O r j (h q)", s=4, i=2, j=2, o=2, h=2)
 
         ident = keep.tile([128, 128], F32, name="ident")
+        ident_bf = keep.tile([128, 128], BF16, name="ident_bf")
         perm = keep.tile([128, 128], F32, name="perm")
         scale = keep.tile([128, 2, 4], F32, name="scale")
         t1_codes = keep.tile([128, 512], U32, name="t1_codes", align_bytes=64)
@@ -111,6 +112,10 @@ def tile_linear2mpo_pa_kernel(tc, t1, core2, core3_bytes, core3_scale, out):
                 for u in range(2):
                     nc.tensor.transpose(turned[:, e, u, :], words[:, u::2], perm[:])
             release_slot(("t1_raw", a))
+
+        def empty_t1(a):
+            bank = full_banks["t1", a]
+            turned = bank[:].rearrange("p (e u n) -> p e u n", e=2, u=2)
             t1_grouped[a] = take_slot(("t1_grouped", a), [128, 1024], BF16)
             dst = t1_grouped[a][:].bitcast(F32)
             scalar(dst.rearrange("p (e n u) -> p e n u", e=2, u=2), turned.rearrange("p e u n -> p e n u"))
@@ -145,6 +150,21 @@ def tile_linear2mpo_pa_kernel(tc, t1, core2, core3_bytes, core3_scale, out):
             c3_grouped[c, g] = take_slot(("c3_grouped", c, g), [128, 2048], BF16)
             copy(c3_grouped[c, g][:].rearrange("p (n i t) -> p n t i", i=2, t=4), c3_wide[c, g][:].rearrange("p t (n i) -> p n t i", i=2))
             release_slot(("c3_wide", c, g))
+
+        def weave_c3(c, g, half):
+            woven = take_bank(("c3", c, g, half))[:].bitcast(BF16).rearrange("p (b n t) -> p b t n", b=2, t=4)
+            for b in range(2):
+                first = half * 256 + b * 128
+                nc.tensor.matmul(out=woven[:, b], lhsT=ident_bf[:], rhs=c3_wide[c, g][:, :, first : first + 128], start=True, stop=True)
+            if half == 1:
+                release_slot(("c3_wide", c, g))
+
+        def empty_c3(c, g, half, copy=scalar):
+            if (c, g) not in c3_grouped:
+                c3_grouped[c, g] = take_slot(("c3_grouped", c, g), [128, 2048], BF16)
+            bank = full_banks["c3", c, g, half]
+            copy(c3_grouped[c, g][:, half * 1024 : (half + 1) * 1024], bank[:].bitcast(BF16))
+            release_bank(bank, copy)
 
         def quantize_c3(c, g):
             quantize(("c3", c, g), c3_codes[c, g][:], c3_scales[c, g][:], c3_grouped[c, g][:])
@@ -220,11 +240,11 @@ def tile_linear2mpo_pa_kernel(tc, t1, core2, core3_bytes, core3_scale, out):
         with tc.manual_schedule():
             nc.scalar.dma_start(out=scale[:], in_=core3_scale.rearrange("(g p t) a b c -> p g (t a b c)", g=2, t=4))
             load_c3([0, 1], 0, parts=2)
+            load_c3([0, 1], 1)
             load_c2_pass(0, 0)
             load_t1(0)
-            load_c3([0, 1], 1)
-            load_c2_pass(0, 1)
             load_t1(1)
+            load_c2_pass(0, 1)
             load_c2_pass(1, 0)
             load_c2_pass(1, 1)
             load_c3([2, 3], 0)
@@ -234,49 +254,69 @@ def tile_linear2mpo_pa_kernel(tc, t1, core2, core3_bytes, core3_scale, out):
                     load_c2_pass(io, g)
             make_identity(nc, ident[:])
             scalar(perm[:].rearrange("p (o s) -> p s o", s=4), ident[:].rearrange("p (s o) -> p s o", s=4))
+            scalar(ident_bf[:], ident[:])
 
             widen_c3(0, 0)
-            widen_c3(1, 0, on_scalar=[1, 2, 3])
+            widen_c3(1, 0, on_scalar=[0, 1, 2])
+            weave_c3(1, 0, 0)
+            weave_c3(1, 0, 1)
             group_c3(0, 0)
-            group_c2(0, 0)
-            group_c3(1, 0, scalar)
+            widen_c3(0, 1, on_scalar=[1, 2, 3])
             quantize_c3(0, 0)
-            quantize_c2(0, 0)
-            quantize_c3(1, 0)
+            widen_c3(1, 1, on_scalar=[0, 1], places=[0, 1])
             turn_t1(0)
-            widen_c3(0, 1, on_scalar=range(4))
-            group_c2(0, 1)
-            quantize_t1(0)
-            widen_c3(1, 1, on_scalar=range(4), places=range(2))
             turn_t1(1)
-            widen_c3(1, 1, on_scalar=range(4), places=range(2, 4))
-            quantize_c2(0, 1)
-            group_c2(1, 0)
+            weave_c3(0, 1, 0)
+            group_c2(0, 0)
+            empty_t1(0)
+            widen_c3(1, 1, on_scalar=[], places=[2, 3])
+            empty_t1(1)
+            quantize_c2(0, 0)
+            quantize_t1(0)
+            group_c2(0, 1)
             quantize_t1(1)
-            group_c2(1, 1)
-            quantize_c2(1, 0)
-            group_c3(0, 1)
-            quantize_c2(1, 1)
-            for r in range(4):
+            quantize_c2(0, 1)
+            empty_c3(1, 0, 0)
+            empty_c3(1, 0, 1)
+            step1(0, 0, 0)
+            weave_c3(0, 1, 1)
+            empty1(0, 0, 0, scalar)
+            empty_c3(0, 1, 0)
+            step1(0, 1, 0)
+            empty_c3(0, 1, 1)
+
+            step1(0, 0, 1)
+            step1(0, 1, 1)
+            empty1(0, 1, 0, scalar)
+            for r in range(2):
+                empty1(0, r, 1, scalar)
+            for r in range(2, 4):
                 make_tile(0, r, (scalar, scalar))
+            group_c2(1, 0)
+            quantize_c3(0, 1)
+            quantize_c2(1, 0)
+            group_c2(1, 1)
+            quantize_t2(0, 0)
+            quantize_c2(1, 1)
+            quantize_t2(0, 1)
+            group_c3(1, 1)
+            quantize_t2(0, 2)
+            quantize_c3(1, 0)
+            quantize_t2(0, 3)
+            quantize_c3(1, 1)
             for r in range(4):
                 step1(1, r, 0)
+            step2(0, [0], 0)
             for r in range(4):
                 step1(1, r, 1)
                 for g in range(2):
                     empty1(1, r, g, scalar)
-            quantize_c3(0, 1)
-            quantize_t2(0, 0)
-            quantize_t2(0, 1)
-            group_c3(1, 1)
-            quantize_t2(0, 2)
-            quantize_c3(1, 1)
-            quantize_t2(0, 3)
 
             widen_c3(2, 0)
             for c in range(2):
                 for r in range(4):
-                    step2(0, [c], r)
+                    if (c, r) != (0, 0):
+                        step2(0, [c], r)
                     if c == 1:
                         empty2(0, 0, r, scalar)
                         empty2(0, 1, r, scalar)

@@ -16,6 +16,10 @@ FLOPS = 2 * 512 * 512 * 4096 + 2 * 2048 * 1024 * 2048
 
 SLOTS = 35
 SLOT_BYTES = 4096
+WIDE_A = []
+WIDE_B = []
+ALONE = []
+PAIRED = [(2, 2), (2, 3)]
 HEAD_TILES = 8
 
 
@@ -48,7 +52,7 @@ def tile_linear2mpo_pa_kernel(tc, t1, core2, core3_bytes, core3_scale, out):
                 c2_scales[a, g] = keep.tile([128, 512], U8, name="c2_scales_%d_%d" % (a, g), align_bytes=64)
                 c3_codes[a, g] = keep.tile([128, 512], U32, name="c3_codes_%d_%d" % (a, g), align_bytes=64)
                 c3_scales[a, g] = keep.tile([128, 512], U8, name="c3_scales_%d_%d" % (a, g), align_bytes=64)
-        c3_bytes = {}
+        c3_bytes, t2_pairs = {}, {}
 
         written, awaited, quantised_at, copied_at = [], {vector: 0, scalar: 0}, {}, {}
         choice = {"oldest": 1}
@@ -57,9 +61,10 @@ def tile_linear2mpo_pa_kernel(tc, t1, core2, core3_bytes, core3_scale, out):
 
         free_slots, slot_of = list(range(SLOTS)), {}
 
-        def take_slot(key, shape, dtype):
-            slot_of[key] = free_slots[0]
-            free_slots.remove(slot_of[key])
+        def take_slot(key, shape, dtype, count=1):
+            slot_of[key] = [n for n in free_slots if all(n + m in free_slots for m in range(count))][0]
+            for m in range(count):
+                free_slots.remove(slot_of[key] + m)
             name = "_".join(str(part) for part in key)
             return stage.tile(shape, dtype, name=name, align_bytes=64, offset=slot_of[key] * SLOT_BYTES)
 
@@ -146,18 +151,22 @@ def tile_linear2mpo_pa_kernel(tc, t1, core2, core3_bytes, core3_scale, out):
                 else:
                     nc.vector.tensor_scalar(out=c3_wide[c, g][:, t, :], in0=src, scalar1=scale[:, g, t : t + 1], scalar2=None, op0=MULT)
 
-        def group_c3(c, g, copy=vector):
-            c3_grouped[c, g] = take_slot(("c3_grouped", c, g), [128, 2048], BF16)
-            copy(c3_grouped[c, g][:].rearrange("p (n i t) -> p n t i", i=2, t=4), c3_wide[c, g][:].rearrange("p t (n i) -> p n t i", i=2))
-            release_slot(("c3_wide", c, g))
-
-        def weave_c3(c, g, half):
-            woven = take_bank(("c3", c, g, half))[:].bitcast(BF16).rearrange("p (b n t) -> p b t n", b=2, t=4)
-            for b in range(2):
-                first = half * 256 + b * 128
-                nc.tensor.matmul(out=woven[:, b], lhsT=ident_bf[:], rhs=c3_wide[c, g][:, :, first : first + 128], start=True, stop=True)
-            if half == 1:
+        def group_c3(c, g, copy=vector, halves=slice(0, 2)):
+            if (c, g) not in c3_grouped:
+                c3_grouped[c, g] = take_slot(("c3_grouped", c, g), [128, 2048], BF16)
+            dst = c3_grouped[c, g][:, halves.start * 1024 : halves.stop * 1024]
+            src = c3_wide[c, g][:, :, halves.start * 256 : halves.stop * 256]
+            copy(dst.rearrange("p (n i t) -> p n t i", i=2, t=4), src.rearrange("p t (n i) -> p n t i", i=2))
+            if halves.stop == 2:
                 release_slot(("c3_wide", c, g))
+
+        def weave_c3(c, g, half, pairs=(0, 1)):
+            if ("c3", c, g, half) not in full_banks:
+                take_bank(("c3", c, g, half))
+            woven = full_banks["c3", c, g, half][:].bitcast(BF16).rearrange("p (n t) -> p t n", t=4)
+            for u in pairs:
+                places = slice(2 * u, 2 * u + 2)
+                nc.tensor.matmul(out=woven[:, places], lhsT=ident_bf[:], rhs=c3_wide[c, g][:, places, half * 256 : (half + 1) * 256], start=True, stop=True)
 
         def empty_c3(c, g, half, copy=scalar):
             if (c, g) not in c3_grouped:
@@ -165,6 +174,8 @@ def tile_linear2mpo_pa_kernel(tc, t1, core2, core3_bytes, core3_scale, out):
             bank = full_banks["c3", c, g, half]
             copy(c3_grouped[c, g][:, half * 1024 : (half + 1) * 1024], bank[:].bitcast(BF16))
             release_bank(bank, copy)
+            if half == 1:
+                release_slot(("c3_wide", c, g))
 
         def quantize_c3(c, g):
             quantize(("c3", c, g), c3_codes[c, g][:], c3_scales[c, g][:], c3_grouped[c, g][:])
@@ -200,6 +211,28 @@ def tile_linear2mpo_pa_kernel(tc, t1, core2, core3_bytes, core3_scale, out):
                 step1(io, r, g)
                 empty1(io, r, g, copies[g])
 
+        def step1_pair(io, r, g, u):
+            await_operands(("c2", io, g))
+            bank = take_bank(("step1", io, r, g, u))
+            rows = slice(r * 128, (r + 2) * 128)
+            for e in range(2):
+                cols = slice((2 * u + e) * 128, (2 * u + e + 1) * 128)
+                nc.tensor.matmul_mx(out=bank[:, e * 256 : (e + 1) * 256],
+                                    lhsT=c2_codes[io, g][:, cols].bitcast(FP8X4), lhsT_scale=c2_scales[io, g][:, cols],
+                                    rhs=t1_codes[:, rows].bitcast(FP8X4), rhs_scale=t1_scales[:, rows],
+                                    start=True, stop=True)
+
+        def empty1_pair(io, r, g, u, copy):
+            if (io, r) not in t2_pairs:
+                t2_pairs[io, r] = take_slot(("t2_pair", io, r), [128, 2, 2, 128, 4], BF16)
+                for n in range(2):
+                    t2_grouped[io, r + n] = t2_pairs[io, r][:, n]
+            bank = full_banks["step1", io, r, g, u]
+            copy(t2_pairs[io, r][:, :, g, :, 2 * u : 2 * u + 2], bank[:].rearrange("p (e r n) -> p r n e", e=2, r=2))
+            release_bank(bank, copy)
+            if copy == scalar:
+                copied_at["t2", io, r, 0] = len(written)
+
         def step2(io, chunks, r):
             await_operands(("t2", io, r, 0), ("c3", chunks[0], 0))
             banks = [take_bank(("step2", io, c, r)) for c in chunks]
@@ -212,23 +245,32 @@ def tile_linear2mpo_pa_kernel(tc, t1, core2, core3_bytes, core3_scale, out):
                                         start=(g == 0), stop=(g == 1))
 
         def store_unit(io, c, r):
-            if io >= 2 or c < 2:
-                return (r, r + 1), (c - c % 2, c - c % 2 + 2)
-            return (r - r % 2, r - r % 2 + 2), (c, c + 1)
+            if io < 3 and c >= 2 and (io, r) not in PAIRED:
+                if (io, c) in WIDE_A:
+                    return (0, 4), (c, c + 1)
+                return (r - r % 2, r - r % 2 + 2), (c, c + 1)
+            if (io, r) in WIDE_B:
+                return (r, r + 1), (0, 4)
+            return (r, r + 1), (c - c % 2, c - c % 2 + 2)
 
-        def empty2(io, c, r, copy):
+        def empty2(io, c, r, copy, alone=False):
             (r0, r1), (c0, c1) = store_unit(io, c, r)
             key = (io, r0, c0)
+            banks = (r1 - r0) * (c1 - c0)
             if key not in results:
-                results[key] = (take_slot(("result",) + key, [128, r1 - r0, (c1 - c0) * 512], F32), [])
+                results[key] = (take_slot(("result",) + key, [128, r1 - r0, (c1 - c0) * 512], F32, banks // 2), [])
             tile, done = results[key]
             bank = full_banks["step2", io, c, r]
             copy(tile[:, r - r0, (c - c0) * 512 : (c - c0 + 1) * 512], bank[:])
             release_bank(bank, copy)
             done.append((c, r))
-            if len(done) == 2:
-                for s in range(4):
-                    rows = out_v[s, io // 2, io % 2]
+            for s in range(4):
+                rows = out_v[s, io // 2, io % 2]
+                if alone:
+                    nc.sync.dma_start(out=rows[:, r, c // 2, (c % 2) * 512 : (c % 2 + 1) * 512], in_=tile[s:128:4, r - r0, (c - c0) * 512 : (c - c0 + 1) * 512])
+                elif len(done) == banks and c1 - c0 == 4:
+                    nc.sync.dma_start(out=rows[:, r], in_=tile[s:128:4, 0].rearrange("p (j n) -> p j n", j=2))
+                elif len(done) == banks:
                     cols = slice((c0 % 2) * 512, (c0 % 2 + c1 - c0) * 512)
                     nc.sync.dma_start(out=rows[:, r0:r1, c0 // 2, cols], in_=tile[s:128:4])
 
@@ -263,7 +305,9 @@ def tile_linear2mpo_pa_kernel(tc, t1, core2, core3_bytes, core3_scale, out):
             group_c3(0, 0)
             widen_c3(0, 1, on_scalar=[1, 2, 3])
             quantize_c3(0, 0)
-            widen_c3(1, 1, on_scalar=[0, 1], places=[0, 1])
+            empty_c3(1, 0, 0)
+            widen_c3(1, 1, on_scalar=[0], places=[0])
+            empty_c3(1, 0, 1)
             turn_t1(0)
             turn_t1(1)
             weave_c3(0, 1, 0)
@@ -271,103 +315,132 @@ def tile_linear2mpo_pa_kernel(tc, t1, core2, core3_bytes, core3_scale, out):
             empty_t1(0)
             widen_c3(1, 1, on_scalar=[], places=[2, 3])
             empty_t1(1)
+            widen_c3(1, 1, on_scalar=[1], places=[1])
             quantize_c2(0, 0)
             quantize_t1(0)
             group_c2(0, 1)
             quantize_t1(1)
-            quantize_c2(0, 1)
-            empty_c3(1, 0, 0)
-            empty_c3(1, 0, 1)
-            step1(0, 0, 0)
-            weave_c3(0, 1, 1)
-            empty1(0, 0, 0, scalar)
-            empty_c3(0, 1, 0)
-            step1(0, 1, 0)
-            empty_c3(0, 1, 1)
-
-            step1(0, 0, 1)
-            step1(0, 1, 1)
-            empty1(0, 1, 0, scalar)
-            for r in range(2):
-                empty1(0, r, 1, scalar)
-            for r in range(2, 4):
-                make_tile(0, r, (scalar, scalar))
             group_c2(1, 0)
-            quantize_c3(0, 1)
+            quantize_c2(0, 1)
             quantize_c2(1, 0)
+            empty_c3(0, 1, 0)
+            for r in range(4):
+                step1(0, r, 0)
+                empty1(0, r, 0, scalar)
+                if r % 2 == 1:
+                    weave_c3(0, 1, 1, [r // 2])
+            empty_c3(0, 1, 1)
+            for r in range(4):
+                step1(0, r, 1)
+                empty1(0, r, 1, scalar)
             group_c2(1, 1)
+            quantize_c3(0, 1)
             quantize_t2(0, 0)
             quantize_c2(1, 1)
             quantize_t2(0, 1)
             group_c3(1, 1)
             quantize_t2(0, 2)
-            quantize_c3(1, 0)
             quantize_t2(0, 3)
+            quantize_c3(1, 0)
             quantize_c3(1, 1)
             for r in range(4):
                 step1(1, r, 0)
             step2(0, [0], 0)
             for r in range(4):
+                empty1(1, r, 0, scalar)
                 step1(1, r, 1)
-                for g in range(2):
-                    empty1(1, r, g, scalar)
-
+            for r in range(2):
+                empty1(1, r, 1, scalar)
             widen_c3(2, 0)
-            for c in range(2):
-                for r in range(4):
-                    if (c, r) != (0, 0):
-                        step2(0, [c], r)
-                    if c == 1:
-                        empty2(0, 0, r, scalar)
-                        empty2(0, 1, r, scalar)
+            empty2(0, 0, 0, scalar)
+            step2(0, [0], 1)
+            empty2(0, 0, 1, scalar)
+            step2(0, [0], 2)
+            step2(0, [0], 3)
+            step2(0, [1], 0)
+            empty2(0, 1, 0, scalar)
+            empty1(1, 2, 1, scalar)
+            step2(0, [1], 1)
+            empty2(0, 1, 1, scalar)
+            empty1(1, 3, 1, scalar)
+            for r in range(2, 4):
+                step2(0, [1], r)
+                empty2(0, 0, r, scalar)
+                empty2(0, 1, r, scalar)
             choice["oldest"] = 2
             quantize_t2(1, 0)
             widen_c3(2, 1)
             quantize_t2(1, 1)
-            for g in range(2):
-                group_c3(2, g)
-                quantize_t2(1, 2 + g)
+            group_c3(2, 0)
+            for r in range(2, 4):
+                quantize_t2(1, r)
+            group_c3(2, 1)
             for g in range(2):
                 quantize_c3(2, g)
-            widen_c3(3, 0)
-            for r in range(2):
+            for r in range(4):
                 products(1, [0, 1], r)
-            widen_c3(3, 1, on_scalar=[3])
-            for r in range(2, 4):
-                products(1, [0, 1], r)
-            for step in (group_c3, quantize_c3):
-                for g in range(2):
-                    step(3, g)
-            for io in range(2):
-                for r in range(4):
-                    products(io, [2], r)
             for step in (group_c2, quantize_c2):
                 for g in range(2):
                     step(2, g)
+            widen_c3(3, 0, places=[0, 1, 2])
+            for r in range(4):
+                products(0, [2], r)
+            products(1, [2], 0)
+            step2(1, [2], 1)
+            choice["oldest"] = 1
+            make_tile(2, 0, (vector, vector))
+            empty2(1, 2, 1, scalar)
+            quantize_t2(2, 0, slice(0, 1))
+            widen_c3(3, 0, places=[3])
+            quantize_t2(2, 0, slice(1, 2))
+            step2(1, [2], 2)
+            make_tile(2, 1, (scalar, vector))
+            empty2(1, 2, 2, scalar)
+            widen_c3(3, 1, places=[0])
+            quantize_t2(2, 1)
+            products(1, [2], 3)
+            choice["oldest"] = 2
+            step2(2, [0, 1], 0)
+            group_c3(3, 0, vector)
+            empty2(2, 0, 0, scalar)
+            make_tile(2, 2, (scalar, vector))
+            empty2(2, 1, 0, scalar)
+            widen_c3(3, 1, places=[1])
+            quantize_t2(2, 2)
+            products(2, [0, 1], 1)
+            widen_c3(3, 1, places=[2])
+            make_tile(2, 3, (vector, vector))
+            products(2, [2], 0)
+            widen_c3(3, 1, places=[3])
+            quantize_t2(2, 3)
+            products(2, [0, 1], 2)
+            group_c3(3, 1, vector)
+            products(2, [2], 1)
+            products(2, [0, 1], 3)
+            for g in range(2):
+                quantize_c3(3, g)
+            for r in range(2, 4):
+                products(2, [2], r)
+            for step in (group_c2, quantize_c2):
+                for g in range(2):
+                    step(3, g)
+            for r in (2, 3, 0, 1):
+                products(2, [3], r)
             for r in range(4):
                 products(0, [3], r)
-            for r in range(2):
-                products(1, [3], r)
-            make_tile(2, 0, (vector, vector))
-            for g in range(2):
-                quantize_t2(2, 0, slice(g, g + 1))
-            for r in range(2, 4):
-                products(1, [3], r)
-
-            slice3 = [[(group_c2, 0)], [(group_c2, 1)], [(quantize_c2, 0), (quantize_c2, 1)]]
-            for n in range(7):
-                io, r = 2 + n // 4, n % 4
-                ahead = (2 + (n + 1) // 4, (n + 1) % 4)
-                make_tile(*ahead, (vector if n == 0 else scalar, vector))
-                for step, g in slice3[n] if n < len(slice3) else []:
-                    step(3, g)
-                quantize_t2(*ahead)
-                step2(io, [0, 1], r)
-                empty2(io, 0, r, scalar if n < len(slice3) else vector)
-                empty2(io, 1, r, scalar)
-                step2(io, [2, 3], r)
-                empty2(io, 2, r, vector)
-                empty2(io, 3, r, scalar)
+            make_tile(3, 0, (vector, vector))
+            for r in range(4):
+                step2(1, [3], r)
+                empty2(1, 3, r, (scalar, vector)[r % 2])
+                if r == 0:
+                    quantize_t2(3, 0)
+            for r in range(3):
+                make_tile(3, r + 1, (scalar, vector))
+                quantize_t2(3, r + 1)
+                for c in (0, 2):
+                    step2(3, [c, c + 1], r)
+                    empty2(3, c, r, vector)
+                    empty2(3, c + 1, r, scalar)
             for c in (0, 2):
                 step2(3, [c, c + 1], 3)
                 empty2(3, c, 3, scalar)

@@ -95,7 +95,7 @@ def tile_linear2mpo_pa_kernel(tc, t1, core2, core3_bytes, core3_scale, out):
 
         def load_t1(a):
             t1_raw[a] = take_slot(("t1_raw", a), [128, 2, 512], BF16)
-            nc.sync.dma_start(out=t1_raw[a][:], in_=t1_rows[a * 256 : (a + 1) * 256, :].rearrange("(r p) k -> p r k", r=2))
+            nc.sync.dma_start(out=t1_raw[a][:], in_=t1_rows[a * 256 : (a + 1) * 256, :].rearrange("(p e) k -> p e k", e=2))
 
         def load_c2_pass(io, g):
             c2_raw[io, g] = take_slot(("c2_raw", io, g), [128, 4, 512], BF16)
@@ -123,7 +123,7 @@ def tile_linear2mpo_pa_kernel(tc, t1, core2, core3_bytes, core3_scale, out):
             turned = bank[:].rearrange("p (e u n) -> p e u n", e=2, u=2)
             t1_grouped[a] = take_slot(("t1_grouped", a), [128, 1024], BF16)
             dst = t1_grouped[a][:].bitcast(F32)
-            scalar(dst.rearrange("p (e n u) -> p e n u", e=2, u=2), turned.rearrange("p e u n -> p e n u"))
+            scalar(dst.rearrange("p (n e s u) -> p n e s u", e=2, s=4, u=2), turned.rearrange("p e u (n s) -> p n e s u", s=4))
             release_bank(bank, scalar)
 
         def quantize_t1(a):
@@ -279,6 +279,13 @@ def tile_linear2mpo_pa_kernel(tc, t1, core2, core3_bytes, core3_scale, out):
             for c in chunks:
                 empty2(io, c, r, scalar)
 
+        def unit_of_products(io, chunks, tiles):
+            for r in tiles:
+                step2(io, chunks, r)
+            for r in reversed(tiles):
+                for c in reversed(chunks):
+                    empty2(io, c, r, scalar)
+
         with tc.manual_schedule():
             nc.scalar.dma_start(out=scale[:], in_=core3_scale.rearrange("(g p t) a b c -> p g (t a b c)", g=2, t=4))
             load_c3([0, 1], 0, parts=2)
@@ -295,7 +302,7 @@ def tile_linear2mpo_pa_kernel(tc, t1, core2, core3_bytes, core3_scale, out):
                 for g in range(2):
                     load_c2_pass(io, g)
             make_identity(nc, ident[:])
-            scalar(perm[:].rearrange("p (o s) -> p s o", s=4), ident[:].rearrange("p (s o) -> p s o", s=4))
+            scalar(perm[:].rearrange("p (r o s) -> p r s o", r=2, s=4), ident[:].rearrange("p (r s o) -> p r s o", r=2, s=4))
             scalar(ident_bf[:], ident[:])
 
             widen_c3(0, 0)
@@ -346,50 +353,50 @@ def tile_linear2mpo_pa_kernel(tc, t1, core2, core3_bytes, core3_scale, out):
             for r in range(4):
                 step1(1, r, 0)
             step2(0, [0], 0)
-            for r in range(4):
+            for r in (0, 2):
+                empty1(1, r + 1, 0, scalar)
                 empty1(1, r, 0, scalar)
                 step1(1, r, 1)
-            for r in range(2):
-                empty1(1, r, 1, scalar)
+                step1(1, r + 1, 1)
+            empty1(1, 0, 1, scalar)
             widen_c3(2, 0)
             empty2(0, 0, 0, scalar)
-            step2(0, [0], 1)
-            empty2(0, 0, 1, scalar)
-            step2(0, [0], 2)
-            step2(0, [0], 3)
-            step2(0, [1], 0)
-            empty2(0, 1, 0, scalar)
-            empty1(1, 2, 1, scalar)
-            step2(0, [1], 1)
-            empty2(0, 1, 1, scalar)
-            empty1(1, 3, 1, scalar)
-            for r in range(2, 4):
-                step2(0, [1], r)
+            for r in range(1, 3):
+                step2(0, [0], r)
                 empty2(0, 0, r, scalar)
+            step2(0, [0], 3)
+            for r in range(3):
+                step2(0, [1], r)
                 empty2(0, 1, r, scalar)
+                empty1(1, r + 1, 1, scalar)
+            step2(0, [1], 3)
+            empty2(0, 1, 3, scalar)
+            empty2(0, 0, 3, scalar)
             choice["oldest"] = 2
             quantize_t2(1, 0)
             widen_c3(2, 1)
             quantize_t2(1, 1)
             group_c3(2, 0)
-            for r in range(2, 4):
-                quantize_t2(1, r)
-            group_c3(2, 1)
+            quantize_t2(1, 2)
+            group_c3(2, 1, vector, slice(0, 1))
+            quantize_t2(1, 3)
+            group_c3(2, 1, vector, slice(1, 2))
             for g in range(2):
                 quantize_c3(2, g)
             for r in range(4):
-                products(1, [0, 1], r)
+                unit_of_products(1, [0, 1], [r])
             for step in (group_c2, quantize_c2):
                 for g in range(2):
                     step(2, g)
             widen_c3(3, 0, places=[0, 1, 2])
-            for r in range(4):
-                products(0, [2], r)
-            products(1, [2], 0)
+            for r in (0, 2):
+                unit_of_products(0, [2], [r, r + 1])
+            step2(1, [2], 0)
             step2(1, [2], 1)
             choice["oldest"] = 1
             make_tile(2, 0, (vector, vector))
             empty2(1, 2, 1, scalar)
+            empty2(1, 2, 0, scalar)
             quantize_t2(2, 0, slice(0, 1))
             widen_c3(3, 0, places=[3])
             quantize_t2(2, 0, slice(1, 2))
@@ -407,36 +414,46 @@ def tile_linear2mpo_pa_kernel(tc, t1, core2, core3_bytes, core3_scale, out):
             empty2(2, 1, 0, scalar)
             widen_c3(3, 1, places=[1])
             quantize_t2(2, 2)
-            products(2, [0, 1], 1)
+            step2(2, [0, 1], 1)
+            empty2(2, 0, 1, scalar)
             widen_c3(3, 1, places=[2])
-            make_tile(2, 3, (vector, vector))
-            products(2, [2], 0)
+            make_tile(2, 3, (scalar, vector))
+            empty2(2, 1, 1, scalar)
+            step2(2, [2], 0)
             widen_c3(3, 1, places=[3])
             quantize_t2(2, 3)
             products(2, [0, 1], 2)
+            empty2(2, 2, 0, scalar)
             group_c3(3, 1, vector)
             products(2, [2], 1)
             products(2, [0, 1], 3)
             for g in range(2):
                 quantize_c3(3, g)
             for r in range(2, 4):
-                products(2, [2], r)
+                step2(2, [2], r)
+                empty2(2, 2, r, vector)
             for step in (group_c2, quantize_c2):
                 for g in range(2):
                     step(3, g)
-            for r in (2, 3, 0, 1):
+            for r in range(2, 4):
                 products(2, [3], r)
-            for r in range(4):
-                products(0, [3], r)
-            make_tile(3, 0, (vector, vector))
-            for r in range(4):
-                step2(1, [3], r)
-                empty2(1, 3, r, (scalar, vector)[r % 2])
-                if r == 0:
-                    quantize_t2(3, 0)
+            unit_of_products(2, [3], [0, 1])
+            unit_of_products(0, [3], [0, 1])
+            products(0, [3], 2)
+            for g in range(2):
+                for u in range(2):
+                    step1_pair(3, 0, g, u)
+                    empty1_pair(3, 0, g, u, vector if (g, u) != (1, 1) else scalar)
+                products(*((0, [3], 3), (1, [3], 0))[g])
+            for r in range(1, 4):
+                products(1, [3], r)
+                if r >= 2:
+                    quantize_t2(3, r - 2)
+            release_slot(("t2_pair", 3, 0))
             for r in range(3):
-                make_tile(3, r + 1, (scalar, vector))
-                quantize_t2(3, r + 1)
+                if r > 0:
+                    make_tile(3, r + 1, (scalar, vector))
+                    quantize_t2(3, r + 1)
                 for c in (0, 2):
                     step2(3, [c, c + 1], r)
                     empty2(3, c, r, vector)

@@ -414,46 +414,34 @@ def tile_linear2mpo_pa_kernel(tc, t1, core2, core3_bytes, core3_scale, out):
             empty2(2, 1, 0, scalar)
             widen_c3(3, 1, places=[1])
             quantize_t2(2, 2)
-            step2(2, [0, 1], 1)
-            empty2(2, 0, 1, scalar)
-            widen_c3(3, 1, places=[2])
+            products(2, [0, 1], 1)
             make_tile(2, 3, (scalar, vector))
-            empty2(2, 1, 1, scalar)
-            step2(2, [2], 0)
-            widen_c3(3, 1, places=[3])
+            widen_c3(3, 1, places=[2, 3])
             quantize_t2(2, 3)
-            products(2, [0, 1], 2)
-            empty2(2, 2, 0, scalar)
-            group_c3(3, 1, vector)
-            products(2, [2], 1)
-            products(2, [0, 1], 3)
+            group_c3(3, 1)
+            for r in range(2):
+                products(2, [2], r)
+            for r in range(2, 4):
+                products(2, [0, 1], r)
             for g in range(2):
                 quantize_c3(3, g)
-            for r in range(2, 4):
-                step2(2, [2], r)
-                empty2(2, 2, r, vector)
+            for c, r in ((2, 2), (2, 3), (3, 2), (3, 3)):
+                products(2, [c], r)
             for step in (group_c2, quantize_c2):
                 for g in range(2):
                     step(3, g)
-            for r in range(2, 4):
-                products(2, [3], r)
             unit_of_products(2, [3], [0, 1])
-            unit_of_products(0, [3], [0, 1])
-            products(0, [3], 2)
-            for g in range(2):
-                for u in range(2):
-                    step1_pair(3, 0, g, u)
-                    empty1_pair(3, 0, g, u, vector if (g, u) != (1, 1) else scalar)
-                products(*((0, [3], 3), (1, [3], 0))[g])
-            for r in range(1, 4):
-                products(1, [3], r)
-                if r >= 2:
-                    quantize_t2(3, r - 2)
-            release_slot(("t2_pair", 3, 0))
+            for r in (0, 2):
+                unit_of_products(0, [3], [r, r + 1])
+            make_tile(3, 0, (vector, vector))
+            for r in range(4):
+                step2(1, [3], r)
+                empty2(1, 3, r, (scalar, vector)[r % 2])
+                if r == 0:
+                    quantize_t2(3, 0)
             for r in range(3):
-                if r > 0:
-                    make_tile(3, r + 1, (scalar, vector))
-                    quantize_t2(3, r + 1)
+                make_tile(3, r + 1, (scalar, vector))
+                quantize_t2(3, r + 1)
                 for c in (0, 2):
                     step2(3, [c, c + 1], r)
                     empty2(3, c, r, vector)

from contextlib import ExitStack

import concourse.mybir as mybir
from concourse.masks import make_identity

F32 = mybir.dt.float32
BF16 = mybir.dt.bfloat16
U32 = mybir.dt.uint32
U8 = mybir.dt.uint8
FP8 = mybir.dt.float8_e4m3fn
FP8X4 = mybir.dt.float8_e4m3fn_x4
MULT = mybir.AluOpType.mult
COPY = mybir.ActivationFunctionType.Copy

FLOPS = 2 * 512 * 512 * 4096 + 2 * 2048 * 1024 * 2048

SLOTS = 35
SLOT_BYTES = 4096
WIDE_A = []
WIDE_B = []
ALONE = []
PAIRED = [(2, 2), (2, 3)]
HEAD_TILES = 8


def tile_linear2mpo_pa_kernel(tc, t1, core2, core3_bytes, core3_scale, out):
    nc = tc.nc
    vector, scalar = nc.vector.tensor_copy, nc.scalar.copy
    with ExitStack() as ctx:
        keep = ctx.enter_context(tc.tile_pool(name="keep", bufs=1))
        work = ctx.enter_context(tc.tile_pool(name="work", bufs=1))
        stage = ctx.enter_context(tc.tile_pool(name="stage", bufs=1))
        psum = ctx.enter_context(tc.psum_pool(name="psum", bufs=1))

        t1_rows = t1.rearrange("i o k -> (i o) k")
        core2_v = core2.rearrange("(p j) i o q -> p j (i o) q", j=4)
        core3_v = core3_bytes.rearrange("(g p t) i o q -> g p t (i o q)", g=2, t=4)
        out_v = out.rearrange("(r s i j) (O o h) q -> s i o O r j (h q)", s=4, i=2, j=2, o=2, h=2)

        ident = keep.tile([128, 128], F32, name="ident")
        ident_bf = keep.tile([128, 128], BF16, name="ident_bf")
        perm = keep.tile([128, 128], F32, name="perm")
        scale = keep.tile([128, 2, 4], F32, name="scale")
        t1_codes = keep.tile([128, 512], U32, name="t1_codes", align_bytes=64)
        t1_scales = keep.tile([128, 512], U8, name="t1_scales", align_bytes=64)
        c2_codes, c2_scales, t2_codes, t2_scales, c3_codes, c3_scales = {}, {}, {}, {}, {}, {}
        for a in range(4):
            t2_codes[a] = keep.tile([128, 1024], U32, name="t2_codes_%d" % a, align_bytes=64)
            t2_scales[a] = keep.tile([128, 1024], U8, name="t2_scales_%d" % a, align_bytes=64)
            for g in range(2):
                c2_codes[a, g] = keep.tile([128, 512], U32, name="c2_codes_%d_%d" % (a, g), align_bytes=64)
                c2_scales[a, g] = keep.tile([128, 512], U8, name="c2_scales_%d_%d" % (a, g), align_bytes=64)
                c3_codes[a, g] = keep.tile([128, 512], U32, name="c3_codes_%d_%d" % (a, g), align_bytes=64)
                c3_scales[a, g] = keep.tile([128, 512], U8, name="c3_scales_%d_%d" % (a, g), align_bytes=64)
        c3_bytes, t2_pairs = {}, {}

        written, awaited, quantised_at, copied_at = [], {vector: 0, scalar: 0}, {}, {}
        choice = {"oldest": 1}
        free_banks = [(psum.tile([128, 512], F32, name="bank_%d" % b), scalar, 0) for b in range(8)]
        t1_raw, t1_grouped, c2_raw, c2_grouped, c3_wide, c3_grouped, t2_grouped, full_banks, results = {}, {}, {}, {}, {}, {}, {}, {}, {}

        free_slots, slot_of = list(range(SLOTS)), {}

        def take_slot(key, shape, dtype, count=1):
            slot_of[key] = [n for n in free_slots if all(n + m in free_slots for m in range(count))][0]
            for m in range(count):
                free_slots.remove(slot_of[key] + m)
            name = "_".join(str(part) for part in key)
            return stage.tile(shape, dtype, name=name, align_bytes=64, offset=slot_of[key] * SLOT_BYTES)

        def release_slot(key):
            free_slots.append(slot_of[key])

        def take_bank(key):
            covered = [entry for entry in free_banks if entry[2] <= awaited[entry[1]]]
            entry = covered[0] if covered else free_banks[: choice["oldest"]][-1]
            bank, engine, number = entry
            awaited[engine] = max(awaited[engine], number)
            free_banks.remove(entry)
            full_banks[key] = bank
            return bank

        def release_bank(bank, engine):
            written.append(bank)
            free_banks.append((bank, engine, len(written)))

        def quantize(key, codes, scales, grouped):
            nc.vector.quantize_mx(out=codes.bitcast(FP8X4), scales=scales, in_=grouped)
            written.append(codes)
            quantised_at[key] = len(written)

        def await_operands(*keys):
            awaited[vector] = max([awaited[vector]] + [quantised_at[key] for key in keys])
            awaited[scalar] = max([awaited[scalar]] + [copied_at.get(key, 0) for key in keys])

        def load_t1(a):
            t1_raw[a] = take_slot(("t1_raw", a), [128, 2, 512], BF16)
            nc.sync.dma_start(out=t1_raw[a][:], in_=t1_rows[a * 256 : (a + 1) * 256, :].rearrange("(p e) k -> p e k", e=2))

        def load_c2_pass(io, g):
            c2_raw[io, g] = take_slot(("c2_raw", io, g), [128, 4, 512], BF16)
            nc.sync.dma_start(out=c2_raw[io, g][:], in_=core2_v[:, :, io, g * 512 : (g + 1) * 512])

        def load_c3(chunks, g, parts=1):
            raw = keep.tile([128, 4, len(chunks) * 512], U8, name="c3_bytes_%d_%d" % (chunks[0], g))
            for n, c in enumerate(chunks):
                c3_bytes[c, g] = raw[:, :, n * 512 : (n + 1) * 512]
            for t in range(0, 4, 4 // parts):
                places = slice(t, t + 4 // parts)
                nc.sync.dma_start(out=raw[:, places, :], in_=core3_v[g][:, places, chunks[0] * 512 : (chunks[-1] + 1) * 512])

        def turn_t1(a):
            bank = take_bank(("t1", a))
            turned = bank[:].rearrange("p (e u n) -> p e u n", e=2, u=2)
            for e in range(2):
                words = t1_raw[a][:, e, :].bitcast(F32)
                for u in range(2):
                    nc.tensor.transpose(turned[:, e, u, :], words[:, u::2], perm[:])
            release_slot(("t1_raw", a))

        def empty_t1(a):
            bank = full_banks["t1", a]
            turned = bank[:].rearrange("p (e u n) -> p e u n", e=2, u=2)
            t1_grouped[a] = take_slot(("t1_grouped", a), [128, 1024], BF16)
            dst = t1_grouped[a][:].bitcast(F32)
            scalar(dst.rearrange("p (n e s u) -> p n e s u", e=2, s=4, u=2), turned.rearrange("p e u (n s) -> p n e s u", s=4))
            release_bank(bank, scalar)

        def quantize_t1(a):
            cols = slice(a * 256, (a + 1) * 256)
            quantize(("t1", a), t1_codes[:, cols], t1_scales[:, cols], t1_grouped[a][:])
            release_slot(("t1_grouped", a))

        def group_c2(io, g):
            c2_grouped[io, g] = take_slot(("c2_grouped", io, g), [128, 2048], BF16)
            vector(c2_grouped[io, g][:].rearrange("p (t n e j) -> p n t j e", t=4, e=2, j=4),
                   c2_raw[io, g][:].rearrange("p j (n e t) -> p n t j e", e=2, t=4))
            release_slot(("c2_raw", io, g))

        def quantize_c2(io, g):
            quantize(("c2", io, g), c2_codes[io, g][:], c2_scales[io, g][:], c2_grouped[io, g][:])
            release_slot(("c2_grouped", io, g))

        def widen_c3(c, g, on_scalar=(), places=range(4)):
            if (c, g) not in c3_wide:
                c3_wide[c, g] = take_slot(("c3_wide", c, g), [128, 4, 512], BF16)
            for t in places:
                src = c3_bytes[c, g][:, t, :].bitcast(FP8)
                if t in on_scalar:
                    nc.scalar.activation(out=c3_wide[c, g][:, t, :], in_=src, func=COPY, scale=scale[:, g, t : t + 1])
                else:
                    nc.vector.tensor_scalar(out=c3_wide[c, g][:, t, :], in0=src, scalar1=scale[:, g, t : t + 1], scalar2=None, op0=MULT)

        def group_c3(c, g, copy=vector, halves=slice(0, 2)):
            if (c, g) not in c3_grouped:
                c3_grouped[c, g] = take_slot(("c3_grouped", c, g), [128, 2048], BF16)
            dst = c3_grouped[c, g][:, halves.start * 1024 : halves.stop * 1024]
            src = c3_wide[c, g][:, :, halves.start * 256 : halves.stop * 256]
            copy(dst.rearrange("p (n i t) -> p n t i", i=2, t=4), src.rearrange("p t (n i) -> p n t i", i=2))
            if halves.stop == 2:
                release_slot(("c3_wide", c, g))

        def weave_c3(c, g, half, pairs=(0, 1)):
            if ("c3", c, g, half) not in full_banks:
                take_bank(("c3", c, g, half))
            woven = full_banks["c3", c, g, half][:].bitcast(BF16).rearrange("p (n t) -> p t n", t=4)
            for u in pairs:
                places = slice(2 * u, 2 * u + 2)
                nc.tensor.matmul(out=woven[:, places], lhsT=ident_bf[:], rhs=c3_wide[c, g][:, places, half * 256 : (half + 1) * 256], start=True, stop=True)

        def empty_c3(c, g, half, copy=scalar):
            if (c, g) not in c3_grouped:
                c3_grouped[c, g] = take_slot(("c3_grouped", c, g), [128, 2048], BF16)
            bank = full_banks["c3", c, g, half]
            copy(c3_grouped[c, g][:, half * 1024 : (half + 1) * 1024], bank[:].bitcast(BF16))
            release_bank(bank, copy)
            if half == 1:
                release_slot(("c3_wide", c, g))

        def quantize_c3(c, g):
            quantize(("c3", c, g), c3_codes[c, g][:], c3_scales[c, g][:], c3_grouped[c, g][:])
            release_slot(("c3_grouped", c, g))

        def step1(io, r, g):
            await_operands(("c2", io, g), ("t1", r // 2))
            bank = take_bank(("step1", io, r, g))
            rows = slice(r * 128, (r + 1) * 128)
            for t in range(4):
                cols = slice(t * 128, (t + 1) * 128)
                nc.tensor.matmul_mx(out=bank[:, cols],
                                    lhsT=c2_codes[io, g][:, cols].bitcast(FP8X4), lhsT_scale=c2_scales[io, g][:, cols],
                                    rhs=t1_codes[:, rows].bitcast(FP8X4), rhs_scale=t1_scales[:, rows],
                                    start=True, stop=True)

        def empty1(io, r, g, copy):
            if (io, r) not in t2_grouped:
                t2_grouped[io, r] = work.tile([128, 2, 128, 4], BF16, name="t2_grouped", align_bytes=64, bufs=HEAD_TILES)
            bank = full_banks["step1", io, r, g]
            copy(t2_grouped[io, r][:, g], bank[:].rearrange("p (t n) -> p n t", t=4))
            release_bank(bank, copy)
            if copy == scalar:
                copied_at["t2", io, r, 0] = len(written)

        def quantize_t2(io, r, passes=slice(0, 2)):
            cols = slice(r * 256 + passes.start * 128, r * 256 + passes.stop * 128)
            values = t2_grouped[io, r][:, passes].rearrange("p g n t -> p (g n t)")
            quantize(("t2", io, r, passes.start), t2_codes[io][:, cols], t2_scales[io][:, cols], values)

        def make_tile(io, r, copies):
            for g in range(2):
                step1(io, r, g)
                empty1(io, r, g, copies[g])

        def step1_pair(io, r, g, u):
            await_operands(("c2", io, g))
            bank = take_bank(("step1", io, r, g, u))
            rows = slice(r * 128, (r + 2) * 128)
            for e in range(2):
                cols = slice((2 * u + e) * 128, (2 * u + e + 1) * 128)
                nc.tensor.matmul_mx(out=bank[:, e * 256 : (e + 1) * 256],
                                    lhsT=c2_codes[io, g][:, cols].bitcast(FP8X4), lhsT_scale=c2_scales[io, g][:, cols],
                                    rhs=t1_codes[:, rows].bitcast(FP8X4), rhs_scale=t1_scales[:, rows],
                                    start=True, stop=True)

        def empty1_pair(io, r, g, u, copy):
            if (io, r) not in t2_pairs:
                t2_pairs[io, r] = take_slot(("t2_pair", io, r), [128, 2, 2, 128, 4], BF16)
                for n in range(2):
                    t2_grouped[io, r + n] = t2_pairs[io, r][:, n]
            bank = full_banks["step1", io, r, g, u]
            copy(t2_pairs[io, r][:, :, g, :, 2 * u : 2 * u + 2], bank[:].rearrange("p (e r n) -> p r n e", e=2, r=2))
            release_bank(bank, copy)
            if copy == scalar:
                copied_at["t2", io, r, 0] = len(written)

        def step2(io, chunks, r):
            await_operands(("t2", io, r, 0), ("c3", chunks[0], 0))
            banks = [take_bank(("step2", io, c, r)) for c in chunks]
            for g in range(2):
                rows = slice(r * 256 + g * 128, r * 256 + (g + 1) * 128)
                for c, bank in zip(chunks, banks):
                    nc.tensor.matmul_mx(out=bank[:],
                                        lhsT=t2_codes[io][:, rows].bitcast(FP8X4), lhsT_scale=t2_scales[io][:, rows],
                                        rhs=c3_codes[c, g][:].bitcast(FP8X4), rhs_scale=c3_scales[c, g][:],
                                        start=(g == 0), stop=(g == 1))

        def store_unit(io, c, r):
            if io < 3 and c >= 2 and (io, r) not in PAIRED:
                if (io, c) in WIDE_A:
                    return (0, 4), (c, c + 1)
                return (r - r % 2, r - r % 2 + 2), (c, c + 1)
            if (io, r) in WIDE_B:
                return (r, r + 1), (0, 4)
            return (r, r + 1), (c - c % 2, c - c % 2 + 2)

        def empty2(io, c, r, copy, alone=False):
            (r0, r1), (c0, c1) = store_unit(io, c, r)
            key = (io, r0, c0)
            banks = (r1 - r0) * (c1 - c0)
            if key not in results:
                results[key] = (take_slot(("result",) + key, [128, r1 - r0, (c1 - c0) * 512], F32, banks // 2), [])
            tile, done = results[key]
            bank = full_banks["step2", io, c, r]
            copy(tile[:, r - r0, (c - c0) * 512 : (c - c0 + 1) * 512], bank[:])
            release_bank(bank, copy)
            done.append((c, r))
            for s in range(4):
                rows = out_v[s, io // 2, io % 2]
                if alone:
                    nc.sync.dma_start(out=rows[:, r, c // 2, (c % 2) * 512 : (c % 2 + 1) * 512], in_=tile[s:128:4, r - r0, (c - c0) * 512 : (c - c0 + 1) * 512])
                elif len(done) == banks and c1 - c0 == 4:
                    nc.sync.dma_start(out=rows[:, r], in_=tile[s:128:4, 0].rearrange("p (j n) -> p j n", j=2))
                elif len(done) == banks:
                    cols = slice((c0 % 2) * 512, (c0 % 2 + c1 - c0) * 512)
                    nc.sync.dma_start(out=rows[:, r0:r1, c0 // 2, cols], in_=tile[s:128:4])

        def products(io, chunks, r):
            step2(io, chunks, r)
            for c in chunks:
                empty2(io, c, r, scalar)

        def unit_of_products(io, chunks, tiles):
            for r in tiles:
                step2(io, chunks, r)
            for r in reversed(tiles):
                for c in reversed(chunks):
                    empty2(io, c, r, scalar)

        with tc.manual_schedule():
            nc.scalar.dma_start(out=scale[:], in_=core3_scale.rearrange("(g p t) a b c -> p g (t a b c)", g=2, t=4))
            load_c3([0, 1], 0, parts=2)
            load_c3([0, 1], 1)
            load_c2_pass(0, 0)
            load_t1(0)
            load_t1(1)
            load_c2_pass(0, 1)
            load_c2_pass(1, 0)
            load_c2_pass(1, 1)
            load_c3([2, 3], 0)
            load_c3([2, 3], 1)
            for io in range(2, 4):
                for g in range(2):
                    load_c2_pass(io, g)
            make_identity(nc, ident[:])
            scalar(perm[:].rearrange("p (r o s) -> p r s o", r=2, s=4), ident[:].rearrange("p (r s o) -> p r s o", r=2, s=4))
            scalar(ident_bf[:], ident[:])

            widen_c3(0, 0)
            widen_c3(1, 0, on_scalar=[0, 1, 2])
            weave_c3(1, 0, 0)
            weave_c3(1, 0, 1)
            group_c3(0, 0)
            widen_c3(0, 1, on_scalar=[1, 2, 3])
            quantize_c3(0, 0)
            empty_c3(1, 0, 0)
            widen_c3(1, 1, on_scalar=[0], places=[0])
            empty_c3(1, 0, 1)
            turn_t1(0)
            turn_t1(1)
            weave_c3(0, 1, 0)
            group_c2(0, 0)
            empty_t1(0)
            widen_c3(1, 1, on_scalar=[], places=[2, 3])
            empty_t1(1)
            widen_c3(1, 1, on_scalar=[1], places=[1])
            quantize_c2(0, 0)
            quantize_t1(0)
            group_c2(0, 1)
            quantize_t1(1)
            group_c2(1, 0)
            quantize_c2(0, 1)
            quantize_c2(1, 0)
            empty_c3(0, 1, 0)
            for r in range(4):
                step1(0, r, 0)
                empty1(0, r, 0, scalar)
                if r % 2 == 1:
                    weave_c3(0, 1, 1, [r // 2])
            empty_c3(0, 1, 1)
            for r in range(4):
                step1(0, r, 1)
                empty1(0, r, 1, scalar)
            group_c2(1, 1)
            quantize_c3(0, 1)
            quantize_t2(0, 0)
            quantize_c2(1, 1)
            quantize_t2(0, 1)
            group_c3(1, 1)
            quantize_t2(0, 2)
            quantize_t2(0, 3)
            quantize_c3(1, 0)
            quantize_c3(1, 1)
            for r in range(4):
                step1(1, r, 0)
            step2(0, [0], 0)
            for r in (0, 2):
                empty1(1, r + 1, 0, scalar)
                empty1(1, r, 0, scalar)
                step1(1, r, 1)
                step1(1, r + 1, 1)
            empty1(1, 0, 1, scalar)
            widen_c3(2, 0)
            empty2(0, 0, 0, scalar)
            for r in range(1, 3):
                step2(0, [0], r)
                empty2(0, 0, r, scalar)
            step2(0, [0], 3)
            for r in range(3):
                step2(0, [1], r)
                empty2(0, 1, r, scalar)
                empty1(1, r + 1, 1, scalar)
            step2(0, [1], 3)
            empty2(0, 1, 3, scalar)
            empty2(0, 0, 3, scalar)
            choice["oldest"] = 2
            quantize_t2(1, 0)
            widen_c3(2, 1)
            quantize_t2(1, 1)
            group_c3(2, 0)
            quantize_t2(1, 2)
            group_c3(2, 1, vector, slice(0, 1))
            quantize_t2(1, 3)
            group_c3(2, 1, vector, slice(1, 2))
            for g in range(2):
                quantize_c3(2, g)
            for r in range(4):
                unit_of_products(1, [0, 1], [r])
            for step in (group_c2, quantize_c2):
                for g in range(2):
                    step(2, g)
            widen_c3(3, 0, places=[0, 1, 2])
            for r in (0, 2):
                unit_of_products(0, [2], [r, r + 1])
            step2(1, [2], 0)
            step2(1, [2], 1)
            choice["oldest"] = 1
            make_tile(2, 0, (vector, vector))
            empty2(1, 2, 1, scalar)
            empty2(1, 2, 0, scalar)
            quantize_t2(2, 0, slice(0, 1))
            widen_c3(3, 0, places=[3])
            quantize_t2(2, 0, slice(1, 2))
            step2(1, [2], 2)
            make_tile(2, 1, (scalar, vector))
            empty2(1, 2, 2, scalar)
            widen_c3(3, 1, places=[0])
            quantize_t2(2, 1)
            products(1, [2], 3)
            choice["oldest"] = 2
            step2(2, [0, 1], 0)
            group_c3(3, 0, vector)
            empty2(2, 0, 0, scalar)
            make_tile(2, 2, (scalar, vector))
            empty2(2, 1, 0, scalar)
            widen_c3(3, 1, places=[1])
            quantize_t2(2, 2)
            products(2, [0, 1], 1)
            make_tile(2, 3, (scalar, vector))
            widen_c3(3, 1, places=[2, 3])
            quantize_t2(2, 3)
            group_c3(3, 1)
            for r in range(2):
                products(2, [2], r)
            for r in range(2, 4):
                products(2, [0, 1], r)
            for g in range(2):
                quantize_c3(3, g)
            for c, r in ((2, 2), (2, 3), (3, 2), (3, 3)):
                products(2, [c], r)
            for step in (group_c2, quantize_c2):
                for g in range(2):
                    step(3, g)
            unit_of_products(2, [3], [0, 1])
            for r in (0, 2):
                unit_of_products(0, [3], [r, r + 1])
            make_tile(3, 0, (vector, vector))
            for r in range(4):
                step2(1, [3], r)
                empty2(1, 3, r, (scalar, vector)[r % 2])
                if r == 0:
                    quantize_t2(3, 0)
            for r in range(3):
                make_tile(3, r + 1, (scalar, vector))
                quantize_t2(3, r + 1)
                for c in (0, 2):
                    step2(3, [c, c + 1], r)
                    empty2(3, c, r, vector)
                    empty2(3, c + 1, r, scalar)
            for c in (0, 2):
                step2(3, [c, c + 1], 3)
                empty2(3, c, 3, scalar)
                empty2(3, c + 1, 3, vector)
